import numpy as np
import ml_dtypes


def mxq(x, axis, fmt="e4m3"):
    dtype, down = {"e4m3": (ml_dtypes.float8_e4m3fn, 7), "e5m2": (ml_dtypes.float8_e5m2, 14)}[fmt]
    v = np.moveaxis(np.asarray(x, np.float32).astype(ml_dtypes.bfloat16).astype(np.float64), axis, -1)
    blocks = v.reshape(v.shape[:-1] + (-1, 32))
    amax = np.abs(blocks).max(-1, keepdims=True)
    byte = np.maximum(np.where(amax > 0, np.frexp(amax)[1] - 1 + 127, 0) - down, 1)
    scale = np.exp2(byte - 127.0)
    codes = (blocks / scale).astype(np.float32).astype(dtype).astype(np.float64)
    return np.moveaxis((codes * scale).reshape(v.shape), -1, axis)


WIDE = False


def mx_kscale(k):
    if not WIDE:
        return np.ones(k)
    levels = np.array([10, -10, 5, -5, 0])
    if k % 512:
        return np.exp2(np.random.permutation(np.resize(levels, k // 32))).repeat(32)
    a = np.empty((k // 512, 16))
    for p in range(k // 512):
        a[p, :8] = np.random.permutation(np.resize(levels, 8))
        for g in range(8):
            far = levels[np.abs(levels - a[p, g]) >= 10]
            a[p, g + 8] = far[np.random.randint(len(far))]
    return np.exp2(a.ravel()).repeat(32)


BF16 = ml_dtypes.bfloat16


def bf(x):
    return np.asarray(x, np.float32).astype(BF16)


def f64(x):
    return np.asarray(x).astype(np.float64)


E2M1 = np.array([0.0, 0.5, 1.0, 1.5, 2.0, 3.0, 4.0, 6.0, -0.0, -0.5, -1.0, -1.5, -2.0, -3.0, -4.0, -6.0])


def pack_weight(w, fmt):
    k, n = w.shape
    w = f64(bf(w)).reshape(k // 32, 32, n)
    amax = np.abs(w).max(1)
    if fmt == "e4m3":
        byte = np.frexp(amax)[1] - 1 + 127 - 7
    else:
        mant, ex = np.frexp(amax / 6.0)
        byte = np.where(mant > 0.5, ex, ex - 1) + 127
    byte = np.clip(np.where(amax > 0, byte, 1), 1, 254)
    scaled = (w * np.exp2(127.0 - byte)[:, None, :]).reshape(k, n).astype(np.float32)
    by_word = np.ascontiguousarray(scaled.reshape(k // 512, 128, 4, n).transpose(0, 1, 3, 2))
    if fmt == "e4m3":
        words = by_word.astype(ml_dtypes.float8_e4m3fn).view(np.uint8)
    else:
        c = by_word.astype(ml_dtypes.float4_e2m1fn).view(np.uint8) & 0xF
        words = c[..., 0::2] | (c[..., 1::2] << 4)
    return np.ascontiguousarray(words), np.ascontiguousarray(byte.astype(np.uint8).reshape(k // 512, 16, n))


def unpack_weight(words, scales, fmt):
    g, p, n, _ = words.shape
    if fmt == "e4m3":
        vals = np.ascontiguousarray(words).view(ml_dtypes.float8_e4m3fn).astype(np.float64)
    else:
        nib = np.empty((g, p, n, 4), np.uint8)
        nib[..., 0::2] = words & 0xF
        nib[..., 1::2] = words >> 4
        vals = E2M1[nib]
    vals = vals * np.repeat(np.exp2(scales.astype(np.float64) - 127.0), 8, axis=1)[..., None]
    return vals.transpose(0, 1, 3, 2).reshape(g * 512, n)
def pack4(w):
    words, scales = pack_weight(w, "e2m1")
    return words.reshape(words.shape[0], 128, -1), scales


def unpack4(words, scales):
    return unpack_weight(words.reshape(words.shape[0], 128, -1, 2), scales, "e2m1")


B, S, D, H = 2, 256, 1024, 4096
NS = int(round(np.log2(H)))


def erf(z):
    z = np.clip(z, -6.0, 6.0)
    z2 = 2.0 * z * z
    term = z.copy()
    tot = z.copy()
    for n in range(1, 130):
        term = term * (z2 / (2 * n + 1))
        tot = tot + term
    return 2.0 / np.sqrt(np.pi) * np.exp(-z * z) * tot


def gelu_exact(v):
    return 0.5 * v * (1.0 + erf(v / np.sqrt(2.0)))


def butterfly(y, weights, dim):
    lead = y.shape[:-1]
    for stage in range(weights.shape[0]):
        s = 2 ** stage
        nb = dim // (2 * s)
        yr = y.reshape(*lead, nb, 2, s)
        a = yr[..., 0, :]
        b = yr[..., 1, :]
        w = weights[stage].reshape(nb, s, 2, 2)
        na = w[..., 0, 0] * a + w[..., 0, 1] * b
        nb2 = w[..., 1, 0] * a + w[..., 1, 1] * b
        y = np.stack([na, nb2], axis=-2).reshape(*lead, dim)
    return y


def bfly_draw():
    g = np.random.standard_normal((NS, H // 2, 2, 2))
    return np.sign(g) * 0.58 + 0.15 * g


def draw0():
    s, t = mx_kscale(D), mx_kscale(H)
    x = np.random.standard_normal((B, S, D)) * s
    W_exp = np.random.standard_normal((D, H)) / np.sqrt(D) / s[:, None]
    b_exp = np.random.standard_normal(H) * 0.1
    up_weights = bfly_draw()
    up_bias = np.random.standard_normal(H) * 0.1
    down_weights = bfly_draw()
    down_weights[NS - 1] = down_weights[NS - 1] * t.reshape(2, H // 2).T[:, :, None]
    W_con = np.random.standard_normal((H, D)) * 1.5 / np.sqrt(H) / t[:, None]
    b_con = np.random.standard_normal(D) * 0.1
    down_bias = np.random.standard_normal(D) * 0.1
    W_exp_words, W_exp_scales = pack4(W_exp)
    W_con_words, W_con_scales = pack4(W_con)
    return {"x": bf(x), "W_exp_words": W_exp_words, "W_exp_scales": W_exp_scales, "b_exp": bf(b_exp), "up_weights": bf(up_weights), "up_bias": bf(up_bias),
            "down_weights": bf(down_weights), "W_con_words": W_con_words, "W_con_scales": W_con_scales, "b_con": bf(b_con), "down_bias": bf(down_bias)}


def core(x, W_exp_words, W_exp_scales, b_exp, up_weights, up_bias, down_weights, W_con_words, W_con_scales, b_con, down_bias):
    h = (mxq(f64(x), 2, "e4m3") @ unpack4(W_exp_words, W_exp_scales)) + f64(b_exp)
    h = butterfly(h, f64(up_weights), H)
    h = gelu_exact(h + f64(up_bias))
    h = butterfly(h, f64(down_weights), H)
    y = (mxq(h, 2, "e4m3") @ unpack4(W_con_words, W_con_scales)) + f64(b_con)
    return y + f64(down_bias)


def e4m3fn_bytes(y):
    return np.clip(np.asarray(y, np.float64), -448.0, 448.0).astype(np.float32).astype(ml_dtypes.float8_e4m3fn).view(np.uint8)


def e4m3fn_values(b):
    return np.asarray(b, np.uint8).view(ml_dtypes.float8_e4m3fn).astype(np.float64)


def setup_inputs():
    d = draw0()
    x0 = np.asarray(d['x']).astype(np.float64)
    s = (np.max(np.abs(x0), axis=(0, 1), keepdims=True) / 448.0).astype(np.float32)
    out = {}
    for k, v in d.items():
        if k == 'x':
            out['x_bytes'] = e4m3fn_bytes(x0 / s.astype(np.float64))
            out['x_scale'] = s
        else:
            out[k] = v
    return out


def reference(x_bytes, x_scale, W_exp_words, W_exp_scales, b_exp, up_weights, up_bias, down_weights, W_con_words, W_con_scales, b_con, down_bias):
    return core(e4m3fn_values(x_bytes) * x_scale.astype(np.float64), W_exp_words, W_exp_scales, b_exp, up_weights, up_bias, down_weights, W_con_words, W_con_scales, b_con, down_bias)

@@ -1,0 +1,514 @@
+from contextlib import ExitStack
+
+import concourse.mybir as mybir
+from concourse.masks import make_identity
+
+F32 = mybir.dt.float32
+BF16 = mybir.dt.bfloat16
+U32 = mybir.dt.uint32
+I32 = mybir.dt.int32
+U8 = mybir.dt.uint8
+FP8 = mybir.dt.float8_e4m3fn
+FP8X4 = mybir.dt.float8_e4m3fn_x4
+FP4X4 = mybir.dt.float4_e2m1fn_x4
+ADD = mybir.AluOpType.add
+MULT = mybir.AluOpType.mult
+COPY = mybir.ActivationFunctionType.Copy
+IDENT = mybir.ActivationFunctionType.Identity
+GELU = mybir.ActivationFunctionType.Gelu
+
+P = 128
+D = 1024
+H = 4096
+HALF = 256
+FLOPS = 2 * 2 * 512 * D * H
+V_EVERY = 8
+
+
+def tile_butterflymlp_w4_kernel(
+    tc, x_bytes, x_scale, w_exp_words, w_exp_scales, b_exp, up_w, up_bias, down_w, w_con_words, w_con_scales, b_con, down_bias, out
+):
+    nc = tc.nc
+    out_flat = out.rearrange("b s d -> (b s d)")
+    out_rows = out.rearrange("b s d -> (b s) d")
+    x_rows = x_bytes.rearrange("b s k -> (b s) k")
+    region = HALF * 1024
+
+    with ExitStack() as ctx:
+        const = ctx.enter_context(tc.tile_pool(name="const", bufs=1))
+        big = ctx.enter_context(tc.tile_pool(name="big", bufs=1))
+        tmp = ctx.enter_context(tc.tile_pool(name="tmp", bufs=4))
+        psf = ctx.enter_context(tc.psum_pool(name="psf", bufs=2))
+        with ExitStack() as head_ctx:
+            head = head_ctx.enter_context(tc.tile_pool(name="head", bufs=1))
+            psh = head_ctx.enter_context(tc.psum_pool(name="psh", bufs=1))
+
+            ident = const.tile([P, P], F32, name="ident")
+            make_identity(nc, ident[:])
+
+            scale_row = head.tile([P, D], F32, name="scale_row")
+            nc.sync.dma_start(out=scale_row[:], in_=x_scale.rearrange("a b k -> (a b k)").partition_broadcast(P))
+            x_bytes_tiles = {}
+
+            def load_x(i):
+                xb = head.tile([P, D], U8, name="xb%d" % i, tag="xb", bufs=2)
+                nc.sync.dma_start(out=xb[:], in_=x_rows[i * P : (i + 1) * P, :])
+                x_bytes_tiles[i] = xb
+
+            load_x(0)
+            load_x(1)
+
+            we_s = head.tile([P, 2, H], U8, name="we_s", align_bytes=64)
+            nc.gpsimd.memset(we_s[:].rearrange("p g n -> p (g n)").bitcast(I32), 0)
+            for q in range(4):
+                nc.sync.dma_start(
+                    out=we_s[32 * q : 32 * q + 4, :, :].bitcast(I32),
+                    in_=w_exp_scales[:, 4 * q : 4 * q + 4, :].rearrange("g q n -> q g n").bitcast(I32),
+                )
+            we = head.tile([P, 2, 2 * H], U8, name="we", align_bytes=64)
+            for c in range(4):
+                cols = slice(c * 2048, (c + 1) * 2048)
+                nc.sync.dma_start(
+                    out=we[:, :, cols].bitcast(I32), in_=w_exp_words[:, :, cols].rearrange("g p n -> p g n").bitcast(I32)
+                )
+
+            wq_raw = head.tile([P, 5, 64], BF16, name="wq_raw")
+            nc.sync.dma_start(out=wq_raw[:], in_=up_w[0:5].rearrange("s (q k) r c -> q s (k r c)", q=P))
+            wq = const.tile([P, 5, 64], F32, name="wq")
+            nc.gpsimd.tensor_copy(out=wq[:], in_=wq_raw[:])
+            bq_raw = head.tile([P, 32], BF16, name="bq_raw")
+            nc.sync.dma_start(out=bq_raw[:], in_=b_exp.rearrange("(q r) -> q r", q=P))
+
+            load_x(2)
+            load_x(3)
+
+            def load_wp(w, name):
+                raw = head.tile([P, 5, 64], BF16, name=name + "_raw")
+                for col, st in ((0, 0), (1, 1)):
+                    nc.sync.dma_start(
+                        out=raw[:, col, :].rearrange("p (g e) -> p g e", g=8), in_=w[st].rearrange("(g p e) r c -> p g (e r c)", g=8, p=P)
+                    )
+                for col, st in ((2, 9), (3, 10), (4, 11)):
+                    nc.sync.dma_start(
+                        out=raw[:, col, :].rearrange("p (g e) -> p g e", g=4), in_=w[st].rearrange("(g p e) r c -> p g (e r c)", g=4, p=P)
+                    )
+                full = const.tile([P, 5, 64], F32, name=name)
+                nc.gpsimd.tensor_copy(out=full[:], in_=raw[:])
+                return full
+
+            def load_vec_p(v, name):
+                raw = head.tile([P, 8, 4], BF16, name=name + "_raw")
+                nc.sync.dma_start(out=raw[:], in_=v.rearrange("(g p t) -> p g t", g=8, p=P))
+                return raw
+
+            wp_up = load_wp(up_w, "wp_up")
+            bp_raw = load_vec_p(b_exp, "bp")
+            ub_raw = load_vec_p(up_bias, "ub")
+            ub = const.tile([P, 32], F32, name="ub")
+            nc.gpsimd.tensor_copy(out=ub[:], in_=ub_raw[:].rearrange("p g t -> p (g t)"))
+
+            def stage0_bias(w, b_raw, name):
+                b32 = head.tile([P, 16, 2], F32, name=name + "_b32")
+                nc.gpsimd.tensor_copy(out=b32[:].rearrange("p k c -> p (k c)"), in_=b_raw)
+                prod = head.tile([P, 2, 16, 2], F32, name=name + "_prod")
+                res = const.tile([P, 16, 2], F32, name=name)
+                w4 = w[:, 0, :].rearrange("p (k r c) -> p r k c", r=2, c=2)
+                for r in range(2):
+                    nc.gpsimd.tensor_tensor(out=prod[:, r], in0=w4[:, r], in1=b32[:], op=MULT)
+                    nc.gpsimd.tensor_tensor(out=res[:, :, r], in0=prod[:, r, :, 0], in1=prod[:, r, :, 1], op=ADD)
+                return res
+
+            cq = stage0_bias(wq, bq_raw[:], "cq")
+            cp = stage0_bias(wp_up, bp_raw[:].rearrange("p g t -> p (g t)"), "cp")
+            wp_dn = load_wp(down_w, "wp_dn")
+
+            xq = const.tile([P, 2, 512], U32, name="xq", align_bytes=64)
+            xs = const.tile([P, 2, 512], U8, name="xs", align_bytes=64)
+            xg_tiles = {}
+
+            def prep_x(i):
+                xw = head.tile([P, D], BF16, name="xw%d" % i, tag="xw", bufs=2)
+                nc.vector.tensor_tensor(out=xw[:], in0=x_bytes_tiles[i][:].bitcast(FP8), in1=scale_row[:], op=MULT)
+                words = xw[:].bitcast(F32)
+                xt = psh.tile([P, 2, 2, P], F32, name="xt%d" % i, tag="xt", bufs=1)
+                for g in range(2):
+                    for u in range(2):
+                        nc.tensor.transpose(xt[:, g, u, :], words[:, 256 * g + u : 256 * (g + 1) : 2], ident[:])
+                if i % 2 == 0:
+                    xg_new = head.tile([P, 2, HALF, 4], BF16, name="xg%d" % i, tag="xg", bufs=1, align_bytes=64)
+                    xg_tiles[i // 2] = xg_new
+                xg = xg_tiles[i // 2]
+                for g in range(2):
+                    dst = xg[:, g, (i % 2) * P : (i % 2 + 1) * P, :].rearrange("p n t -> p (n t)").bitcast(F32)
+                    nc.vector.tensor_copy(out=dst.rearrange("p (n u) -> p n u", u=2), in_=xt[:, g].rearrange("p u n -> p n u"))
+                if i % 2 == 1:
+                    tok = slice((i // 2) * HALF, (i // 2 + 1) * HALF)
+                    for g in range(2):
+                        nc.vector.quantize_mx(
+                            out=xq[:, g, tok].bitcast(FP8X4), scales=xs[:, g, tok], in_=xg[:, g].rearrange("p n t -> p (n t)")
+                        )
+
+            counter = {"n": 0, "id": 0}
+
+            def product(dst, src, w, c, on_chip):
+                counter["n"] += 1
+                if c is not None:
+                    nc.scalar.activation(out=dst, in_=src, func=IDENT, scale=w, bias=c)
+                elif on_chip and counter["n"] % V_EVERY == 0:
+                    nc.vector.tensor_scalar(out=dst, in0=src, scalar1=w, scalar2=None, op0=MULT)
+                else:
+                    nc.scalar.activation(out=dst, in_=src, func=COPY, scale=w)
+
+            def group(units, s):
+                parts = []
+                for a, b, na, nb, w, k, c, on_chip in units:
+                    counter["id"] += 1
+                    ta = tmp.tile([P, HALF], F32, name="ta%d" % counter["id"], tag="ta" + s)
+                    tb = tmp.tile([P, HALF], F32, name="tb%d" % counter["id"], tag="tb" + s)
+                    product(ta[:], a, w[:, 4 * k : 4 * k + 1], None if c is None else c[:, k, 0:1], on_chip)
+                    product(tb[:], a, w[:, 4 * k + 2 : 4 * k + 3], None if c is None else c[:, k, 1:2], on_chip)
+                    parts.append((ta, tb))
+                for (a, b, na, nb, w, k, c, on_chip), (ta, tb) in zip(units, parts):
+                    nc.vector.scalar_tensor_tensor(out=na, in0=b, scalar=w[:, 4 * k + 1 : 4 * k + 2], in1=ta[:], op0=MULT, op1=ADD)
+                for (a, b, na, nb, w, k, c, on_chip), (ta, tb) in zip(units, parts):
+                    nc.vector.scalar_tensor_tensor(out=nb, in0=b, scalar=w[:, 4 * k + 3 : 4 * k + 4], in1=tb[:], op0=MULT, op1=ADD)
+
+            def free_stage(x, w, s_bit, pairs, s):
+                units = []
+                for k in pairs:
+                    i = (k // s_bit) * 2 * s_bit + k % s_bit
+                    j = i + s_bit
+                    units.append((x[:, i, :], x[:, j, :], x[:, i, :], x[:, j, :], w, k, None, True))
+                group(units, s)
+
+            ht_tiles = {}
+
+            def expand(i, order):
+                ht = head.tile([P, H], F32, name="ht%d" % i, tag="ht", bufs=2)
+                ht_tiles[i] = ht
+                for j in range(8):
+                    ps = psh.tile([P, 512], F32, name="mx%d_%d" % (i, j), tag="mx", bufs=3)
+                    for g in range(2):
+                        nc.tensor.matmul_mx(
+                            out=ps[:],
+                            lhsT=xq[:, g, i * P : (i + 1) * P].bitcast(FP8X4),
+                            lhsT_scale=xs[:, g, i * P : (i + 1) * P],
+                            rhs=we[:, g, 1024 * j : 1024 * (j + 1)].bitcast(FP4X4),
+                            rhs_scale=we_s[:, g, 512 * j : 512 * (j + 1)],
+                            start=(g == 0),
+                            stop=(g == 1),
+                        )
+                    if order == "q":
+                        dst = ht[:].rearrange("p (r q) -> p r q", r=32)[:, :, 16 * j : 16 * (j + 1)]
+                        src = ps[:].rearrange("p (q r) -> p r q", r=32)
+                    else:
+                        dst = ht[:, 512 * j : 512 * (j + 1)].rearrange("p (t q) -> p t q", t=4)
+                        src = ps[:].rearrange("p (q t) -> p t q", t=4)
+                    if order == "q" and j % 2 == 1:
+                        nc.vector.tensor_copy(out=dst, in_=src)
+                    else:
+                        nc.scalar.copy(out=dst, in_=src)
+
+            def turn(dst, i0, blk):
+                for ii in range(2):
+                    nc.tensor.transpose(dst[:, ii * P : (ii + 1) * P], ht_tiles[i0 + ii][:, blk * P : (blk + 1) * P], ident[:])
+
+            def bank(kind, tag):
+                counter["id"] += 1
+                ps = psf.tile([P, 2, HALF], F32, name="%s%d" % (kind, counter["id"]), tag=tag)
+                return ps
+
+            bit_of = const.tile([P, 7, 2], F32, name="bit_of")
+            for b in range(5):
+                nc.vector.tensor_reduce(
+                    out=bit_of[:, b, 1:2],
+                    in_=ident[:].rearrange("p (h b l) -> p b h l", b=2, l=2**b)[:, 1],
+                    axis=mybir.AxisListType.XY,
+                    op=ADD,
+                )
+                nc.vector.tensor_scalar(out=bit_of[:, b, 0:1], in0=bit_of[:, b, 1:2], scalar1=-1.0, scalar2=1.0, op0=MULT, op1=ADD)
+
+            def dense(w, name, scratch):
+                f6 = head.tile([P, 8, 16], BF16, name=name + "_f6", tag="f6")
+                for half in range(2):
+                    nc.sync.dma_start(out=f6[64 * half : 64 * half + 64, :, :], in_=w[8].rearrange("(g u t) r c -> u g (t r c)", g=8, u=64))
+                f5 = head.tile([P, 16, 16], BF16, name=name + "_f5", tag="f5")
+                for q in range(4):
+                    nc.sync.dma_start(out=f5[32 * q : 32 * q + 32, :, :], in_=w[7].rearrange("(g u t) r c -> u g (t r c)", g=16, u=32))
+                s6 = head.tile([P, 8, 4, 2], F32, name=name + "_s6", tag="s6")
+                for half in range(2):
+                    rows = slice(64 * half, 64 * half + 64)
+                    nc.vector.tensor_copy(
+                        out=s6[rows].rearrange("p g t c -> p (g t) c"),
+                        in_=f6[rows].rearrange("p g (t r c) -> p r (g t) c", r=2, c=2)[:, half],
+                    )
+                s5 = head.tile([P, 16, 4, 2], F32, name=name + "_s5", tag="s5")
+                for q in range(4):
+                    rows = slice(32 * q, 32 * q + 32)
+                    nc.vector.tensor_copy(
+                        out=s5[rows].rearrange("p g t c -> p (g t) c"),
+                        in_=f5[rows].rearrange("p g (t r c) -> p r (g t) c", r=2, c=2)[:, q % 2],
+                    )
+                rt = head.tile([P, 2, 2, 8, 4], F32, name=name + "_rt", tag="rt")
+                for i6 in range(2):
+                    for i5 in range(2):
+                        nc.vector.tensor_tensor(
+                            out=rt[:, i6, i5],
+                            in0=s6[:].rearrange("p g t c -> p c g t")[:, i6],
+                            in1=s5[:].rearrange("p (g x) t c -> p x c g t", x=2)[:, i6, i5],
+                            op=MULT,
+                        )
+                ps = psh.tile([P, 2, 2, P], F32, name=name + "_ps", tag="xt", bufs=1)
+                nc.tensor.transpose(ps[:, 0, 0, :], rt[:].rearrange("p x y g t -> p (x y g t)"), ident[:])
+                rows_sb = head.tile([P, P], F32, name=name + "_rows", tag="rows")
+                nc.vector.tensor_copy(out=rows_sb[:], in_=ps[:, 0, 0, :])
+                nc.sync.dma_start(out=scratch.rearrange("(p o) -> p o", p=P), in_=rows_sb[:])
+                mt = const.tile([P, 32 * P], F32, name=name)
+                for q in range(4):
+                    nc.sync.dma_start(
+                        out=mt[32 * q : 32 * q + 32, :], in_=scratch[32 * P * q : 32 * P * (q + 1)].partition_broadcast(32)
+                    )
+                low = None
+                for b in range(5):
+                    n = 2**b
+                    h = 2 ** (6 - b)
+                    rep = P // h
+                    f = head.tile([P, 8, 16 * n], BF16, name="%s_f%d" % (name, b), tag="f%d" % b)
+                    src = w[b + 2].rearrange("(g h e) r c -> h g (e r c)", g=8, h=h)
+                    if b < 3:
+                        for r in range(rep):
+                            nc.sync.dma_start(out=f[r:P:rep, :, :], in_=src)
+                    else:
+                        for hi in range(h):
+                            nc.sync.dma_start(out=f[hi * rep : (hi + 1) * rep, :, :], in_=src[hi].partition_broadcast(rep))
+                    parts = []
+                    for c in range(2):
+                        m = head.tile([P, 8, 8, n], F32, name="%s_m%d_%d" % (name, b, c), tag="msel%d" % c)
+                        nc.scalar.activation(
+                            out=m[:], in_=f[:].rearrange("p g (o x c) -> p c g x o", x=8, c=2)[:, c], func=COPY, scale=bit_of[:, b, c : c + 1]
+                        )
+                        parts.append(m)
+                    sel = head.tile([P, 32, 2, n], F32, name="%s_l%d" % (name, b), tag="l%d" % b)
+                    m0, m1 = [m[:].rearrange("p g x o -> p (g x o)") for m in parts]
+                    nc.vector.tensor_tensor(out=sel[:].rearrange("p k r o -> p (k r o)"), in0=m0, in1=m1, op=ADD)
+                    if b > 0:
+                        for r in range(2):
+                            nc.vector.tensor_tensor(
+                                out=sel[:, :, r, :], in0=sel[:, :, r, :], in1=low[:].rearrange("p k r o -> p k (r o)"), op=MULT
+                            )
+                    low = sel
+                mt4 = mt[:].rearrange("p (k h l) -> p h k l", h=4, l=32)
+                for hh in range(4):
+                    nc.vector.tensor_tensor(
+                        out=mt4[:, hh], in0=mt4[:, hh], in1=low[:].rearrange("p k r o -> p k (r o)"), op=MULT
+                    )
+                return mt
+
+            def stages_0_1(x, w, g, i0, c, s):
+                blk = 4 * g
+                if i0 is None:
+                    free_stage(x, w[:, 0, :], 1, (2 * g, 2 * g + 1), s)
+                else:
+                    pa = bank("fa", "fa")
+                    pb = bank("fb", "fb")
+                    for t in range(4):
+                        turn((pa, pb)[t % 2][:, t // 2, :], i0, blk + t)
+                    group(
+                        [
+                            (pa[:, n, :], pb[:, n, :], x[:, blk + 2 * n, :], x[:, blk + 2 * n + 1, :], w[:, 0, :], 2 * g + n, c, False)
+                            for n in range(2)
+                        ],
+                        s,
+                    )
+                free_stage(x, w[:, 1, :], 2, (2 * g, 2 * g + 1), s)
+
+            def stages_2_9(x, w, mt, h, s):
+                for t0 in (0, 2):
+                    pa = bank("fa", "fa")
+                    pb = bank("fb", "fb")
+                    for n in range(2):
+                        for side, ps in ((0, pa), (1, pb)):
+                            blk = 4 * (2 * h + side) + t0 + n
+                            nc.tensor.matmul(out=ps[:, n, :], lhsT=mt[:, blk * P : (blk + 1) * P], rhs=x[:, blk, :], start=True, stop=True)
+                    group(
+                        [
+                            (
+                                pa[:, n, :],
+                                pb[:, n, :],
+                                x[:, 8 * h + t0 + n, :],
+                                x[:, 8 * h + 4 + t0 + n, :],
+                                w[:, 2, :],
+                                4 * h + t0 + n,
+                                None,
+                                False,
+                            )
+                            for n in range(2)
+                        ],
+                        s,
+                    )
+
+            def stage_10(x, w, h2, g0, s):
+                free_stage(x, w[:, 3, :], 8, [8 * h2 + 4 * g0 + t for t in range(4)], s)
+
+            def stage_11(x, w, gg, s):
+                free_stage(x, w[:, 4, :], 16, [4 * gg + t for t in range(4)], s)
+
+            def gelu(x, blks):
+                for blk in blks:
+                    nc.scalar.activation(out=x[:, blk, :], in_=x[:, blk, :], func=GELU, bias=ub[:, blk : blk + 1])
+
+            prep_x(0)
+            prep_x(1)
+            expand(0, "q")
+            expand(1, "q")
+            mt_up = dense(up_w, "mt_up", out_flat[0 : P * P])
+            x1 = big.tile([P, 32, HALF], F32, name="x1", tag="x1")
+            for j in range(8):
+                pa = bank("fa", "fa")
+                pb = bank("fb", "fb")
+                for n in range(4):
+                    turn((pa, pb)[n % 2][:, n // 2, :], 0, 4 * j + n)
+                group(
+                    [
+                        (pa[:, n, :], pb[:, n, :], x1[:, 4 * j + 2 * n, :], x1[:, 4 * j + 2 * n + 1, :], wq[:, 0, :], 2 * j + n, cq, False)
+                        for n in range(2)
+                    ],
+                    "1",
+                )
+            for st in range(1, 4):
+                for j in range(4):
+                    free_stage(x1, wq[:, st, :], 2**st, range(4 * j, 4 * j + 4), "1")
+            prep_x(2)
+            prep_x(3)
+            expand(2, "p")
+            expand(3, "p")
+            mt_dn = dense(down_w, "mt_dn", out_flat[P * P : 2 * P * P])
+            xb_half = big.tile([P, 32, HALF], F32, name="xb_half", tag="xb_half")
+            for g in range(8):
+                stages_0_1(xb_half, wp_up, g, 2, cp, "2")
+
+        tail = ctx.enter_context(tc.tile_pool(name="tail", bufs=1))
+        psa = ctx.enter_context(tc.psum_pool(name="psa", bufs=1))
+        wr_raw = tail.tile([P, 5, 64], BF16, name="wr_raw")
+        for st in range(5):
+            for hi in range(4):
+                nc.sync.dma_start(
+                    out=wr_raw[32 * hi : 32 * hi + 32, st, :].rearrange("p (m e) -> p m e", m=16),
+                    in_=up_w[5 + st].rearrange("(h m p) r c -> h p m (r c)", h=4, m=16)[hi],
+                )
+        wr = const.tile([P, 5, 64], F32, name="wr")
+        nc.gpsimd.tensor_copy(out=wr[:], in_=wr_raw[:])
+        wc_s = tail.tile([P, 8, D], U8, name="wc_s", align_bytes=64)
+        nc.gpsimd.memset(wc_s[:].rearrange("p g n -> p (g n)").bitcast(I32), 0)
+
+        x2 = tail.tile([P, 32, HALF], F32, name="x2", tag="x2")
+        for c in range(4):
+            free_stage(x1, wq[:, 4, :], 16, (c, c + 4, c + 8, c + 12), "1")
+            reg = out_flat[(c % 2) * region : (c % 2 + 1) * region]
+            nc.sync.dma_start(out=reg.rearrange("(q r n) -> q r n", q=P, r=8), in_=x1[:, c:32:4, :])
+            for hi in range(4):
+                nc.sync.dma_start(
+                    out=x2[32 * hi + c : 32 * hi + 32 : 4, :, :], in_=reg.rearrange("(h m r n) -> h r m n", h=4, m=32, r=8)[hi]
+                )
+        for q in range(4):
+            nc.sync.dma_start(
+                out=wc_s[32 * q : 32 * q + 4, :, :].bitcast(I32),
+                in_=w_con_scales[:, 4 * q : 4 * q + 4, :].rearrange("g q n -> q g n").bitcast(I32),
+            )
+        wc = tail.tile([P, 8, 2 * D], U8, name="wc", align_bytes=64)
+        nc.sync.dma_start(out=wc[:].bitcast(I32), in_=w_con_words.rearrange("g p n -> p g n").bitcast(I32))
+        bias_raw = tail.tile([P, 2, D], BF16, name="bias_raw")
+        nc.sync.dma_start(out=bias_raw[:, 0, :], in_=b_con.partition_broadcast(P))
+        nc.sync.dma_start(out=bias_raw[:, 1, :], in_=down_bias.partition_broadcast(P))
+        bias = tail.tile([P, D], F32, name="bias")
+        nc.gpsimd.tensor_tensor(out=bias[:], in0=bias_raw[:, 0, :], in1=bias_raw[:, 1, :], op=ADD)
+
+        def up_tail(x, h):
+            stages_2_9(x, wp_up, mt_up, h, "2")
+
+        for h in range(4):
+            up_tail(xb_half, h)
+            if h % 2 == 1:
+                for g0 in range(2):
+                    stage_10(xb_half, wp_up, h // 2, g0, "2")
+        for gg in range(4):
+            stage_11(xb_half, wp_up, gg, "2")
+            gelu(xb_half, [4 * gg + t for t in range(4)])
+            gelu(xb_half, [16 + 4 * gg + t for t in range(4)])
+
+        def down(x, tok0, s):
+            for h in range(4):
+                for g in (2 * h, 2 * h + 1):
+                    stages_0_1(x, wp_dn, g, None, None, s)
+                stages_2_9(x, wp_dn, mt_dn, h, s)
+                if h % 2 == 1:
+                    for g0 in range(2):
+                        stage_10(x, wp_dn, h // 2, g0, s)
+            accs = {}
+            for i in range(2):
+                for d in range(2):
+                    acc = psa.tile([P, 512], F32, name="acc%d_%d_%d" % (tok0, i, d), tag="acc%d%d" % (i, d))
+                    accs[(i, d)] = acc
+            done = 0
+            for gg in range(4):
+                outs = []
+                for g in (gg, gg + 4):
+                    hb = tail.tile([P, 4, HALF], BF16, name="hb%d_%d" % (tok0, g), tag="hb", bufs=4)
+                    outs.append(hb)
+                units = []
+                for t in range(4):
+                    units.append((x[:, 4 * gg + t, :], x[:, 16 + 4 * gg + t, :], outs[0][:, t, :], outs[1][:, t, :], wp_dn[:, 4, :], 4 * gg + t, None, True))
+                group(units, s)
+                for g, hb in zip((gg, gg + 4), outs):
+                    hi = tail.tile([P, HALF, 4], BF16, name="hi%d_%d" % (tok0, g), tag="hi", bufs=2, align_bytes=64)
+                    nc.scalar.copy(out=hi[:], in_=hb[:].rearrange("p t n -> p n t"))
+                    hc = tail.tile([P, HALF], U32, name="hc%d_%d" % (tok0, g), tag="hc", bufs=2, align_bytes=64)
+                    hs = tail.tile([P, HALF], U8, name="hs%d_%d" % (tok0, g), tag="hs", bufs=2, align_bytes=64)
+                    nc.vector.quantize_mx(out=hc[:].bitcast(FP8X4), scales=hs[:], in_=hi[:].rearrange("p n t -> p (n t)"))
+                    for i in range(2):
+                        for d in range(2):
+                            nc.tensor.matmul_mx(
+                                out=accs[(i, d)][:],
+                                lhsT=hc[:, i * P : (i + 1) * P].bitcast(FP8X4),
+                                lhsT_scale=hs[:, i * P : (i + 1) * P],
+                                rhs=wc[:, g, 1024 * d : 1024 * (d + 1)].bitcast(FP4X4),
+                                rhs_scale=wc_s[:, g, 512 * d : 512 * (d + 1)],
+                                start=(done == 0),
+                                stop=(done == 7),
+                            )
+                    done += 1
+            for i in range(2):
+                for d in range(2):
+                    o = tail.tile([P, 512], F32, name="o%d_%d_%d" % (tok0, i, d), tag="o", bufs=4)
+                    nc.vector.tensor_tensor(out=o[:], in0=accs[(i, d)][:], in1=bias[:, 512 * d : 512 * (d + 1)], op=ADD)
+                    r0 = tok0 + i * P
+                    nc.sync.dma_start(out=out_rows[r0 : r0 + P, 512 * d : 512 * (d + 1)], in_=o[:])
+
+        for st in range(5):
+            for j in range(4):
+                if st < 4:
+                    free_stage(x2, wr[:, st, :], 2**st, range(4 * j, 4 * j + 4), "1")
+        x3 = big.tile([P, 8, 4 * HALF], F32, name="x3", tag="x1")
+        for c in range(4):
+            free_stage(x2, wr[:, 4, :], 16, range(4 * c, 4 * c + 4), "1")
+            reg = out_flat[(c % 2) * region : (c % 2 + 1) * region].rearrange("(v m z) -> v m z", v=2, m=4)
+            for v in range(2):
+                nc.sync.dma_start(
+                    out=reg[v].rearrange("m (z n) -> z m n", z=P), in_=x2[:, 16 * v + 4 * c : 16 * v + 4 * c + 4, :]
+                )
+            for m in range(4):
+                for v in range(2):
+                    p0 = (4 * c + m) * 8
+                    nc.sync.dma_start(
+                        out=x3[p0 : p0 + 8, v:8:2, :], in_=reg[v, m].rearrange("(h p n) -> p h n", h=4, p=8)
+                    )
+        down(xb_half, HALF, "2")
+        x3v = x3[:].rearrange("p g (t n) -> p (g t) n", t=4)
+        for h2 in range(2):
+            for g0 in range(2):
+                stage_10(x3v, wp_up, h2, g0, "1")
+        for gg in range(4):
+            stage_11(x3v, wp_up, gg, "1")
+            gelu(x3v, [4 * gg + t for t in range(4)])
+            gelu(x3v, [16 + 4 * gg + t for t in range(4)])
+        down(x3v, 0, "1")

@@ -21,8 +21,29 @@ P = 128
 D = 1024
 H = 4096
 HALF = 256
+NA = 208
+NB = 512 - NA
+REGION = NA * 1024
+BUFS_WIDE = 4
+BUFS_NARROW = 4
+SHARE_A = 0
+SHARE_B = 1
+SHARE_C = 0
+SHARE_C0 = 1
+SHARE_A3 = 1
+SHARE_4 = 4
+SIDE_FROM = 0.3
 FLOPS = 2 * 2 * 512 * D * H
-V_EVERY = 8
+
+
+def weave(*lists):
+    keyed = []
+    for n, (steps, lo, hi) in enumerate(lists):
+        for i, step in enumerate(steps):
+            keyed.append((lo + (hi - lo) * (i + 0.5) / len(steps), n, i, step))
+    keyed = sorted(keyed, key=lambda e: e[:3])
+    for e in keyed:
+        e[3]()
 
 
 def tile_butterflymlp_w4_kernel(
@@ -32,483 +53,715 @@ def tile_butterflymlp_w4_kernel(
     out_flat = out.rearrange("b s d -> (b s d)")
     out_rows = out.rearrange("b s d -> (b s) d")
     x_rows = x_bytes.rearrange("b s k -> (b s) k")
-    region = HALF * 1024
+    serial = {"n": 0}
+
+    def uid(prefix):
+        serial["n"] += 1
+        return "%s_%d" % (prefix, serial["n"])
 
     with ExitStack() as ctx:
+        ctx.enter_context(tc.manual_schedule())
         const = ctx.enter_context(tc.tile_pool(name="const", bufs=1))
         big = ctx.enter_context(tc.tile_pool(name="big", bufs=1))
-        tmp = ctx.enter_context(tc.tile_pool(name="tmp", bufs=4))
-        psf = ctx.enter_context(tc.psum_pool(name="psf", bufs=2))
-        with ExitStack() as head_ctx:
-            head = head_ctx.enter_context(tc.tile_pool(name="head", bufs=1))
-            psh = head_ctx.enter_context(tc.psum_pool(name="psh", bufs=1))
+        tmp = ctx.enter_context(tc.tile_pool(name="tmp", bufs=1))
 
-            ident = const.tile([P, P], F32, name="ident")
-            make_identity(nc, ident[:])
+        def product(dst, src, w, c, on_vector):
+            if c is not None:
+                nc.scalar.activation(out=dst, in_=src, func=IDENT, scale=w, bias=c)
+            elif on_vector:
+                nc.vector.tensor_scalar(out=dst, in0=src, scalar1=w, scalar2=None, op0=MULT)
+            else:
+                nc.scalar.activation(out=dst, in_=src, func=COPY, scale=w)
 
-            scale_row = head.tile([P, D], F32, name="scale_row")
-            nc.sync.dma_start(out=scale_row[:], in_=x_scale.rearrange("a b k -> (a b k)").partition_broadcast(P))
+        def group(units, vector_share=0, wide=False):
+            parts = []
+            n = 0
+            width = 512 if wide else NB
+            size = units[0][0].shape[-1]
+            for a, b, na, nb, w, k, c in units:
+                ta_full = tmp.tile([P, width], F32, name=uid("ta"), tag="taw" if wide else "ta", bufs=BUFS_WIDE if wide else BUFS_NARROW)
+                tb_full = tmp.tile([P, width], F32, name=uid("tb"), tag="tbw" if wide else "tb", bufs=BUFS_WIDE if wide else BUFS_NARROW)
+                ta = ta_full[:, 0:size]
+                tb = tb_full[:, 0:size]
+                product(ta, a, w[:, 4 * k : 4 * k + 1], None if c is None else c[:, k, 0:1], n >= 2 * len(units) - vector_share)
+                product(tb, a, w[:, 4 * k + 2 : 4 * k + 3], None if c is None else c[:, k, 1:2], n + 1 >= 2 * len(units) - vector_share)
+                n += 2
+                parts.append((ta, tb))
+            for (a, b, na, nb, w, k, c), (ta, tb) in zip(units, parts):
+                nc.vector.scalar_tensor_tensor(out=na, in0=b, scalar=w[:, 4 * k + 1 : 4 * k + 2], in1=ta, op0=MULT, op1=ADD)
+            for (a, b, na, nb, w, k, c), (ta, tb) in zip(units, parts):
+                nc.vector.scalar_tensor_tensor(out=nb, in0=b, scalar=w[:, 4 * k + 3 : 4 * k + 4], in1=tb, op0=MULT, op1=ADD)
+
+        def free_stage(view, w, bit, pairs, vector_share=0, wide=False, put=None):
+            put = view if put is None else put
+            units = []
+            for k in pairs:
+                i = (k // bit) * 2 * bit + k % bit
+                j = i + bit
+                units.append((view(i), view(j), put(i), put(j), w, k, None))
+            group(units, vector_share, wide)
+
+        ident = const.tile([P, P], F32, name="ident")
+        make_identity(nc, ident[:])
+        ident_b = const.tile([P, P], BF16, name="ident_b")
+        nc.gpsimd.tensor_copy(out=ident_b[:], in_=ident[:])
+        wq = const.tile([P, 5, 64], F32, name="wq")
+        wr = const.tile([P, 5, 64], F32, name="wr")
+        wp_up = const.tile([P, 5, 64], F32, name="wp_up")
+        wp_dn = const.tile([P, 5, 64], F32, name="wp_dn")
+        cq = const.tile([P, 16, 2], F32, name="cq")
+        cp = const.tile([P, 16, 2], F32, name="cp")
+        bp = const.tile([P, 32], F32, name="bp")
+        ub = const.tile([P, 32], F32, name="ub")
+        bit_of = const.tile([P, 5, 2], F32, name="bit_of")
+        mt = const.tile([P, 64 * P], F32, name="mt")
+        low = const.tile([P, 64, 2, 8], F32, name="low")
+        xq = const.tile([P, 2, 512], U32, name="xq", align_bytes=64)
+        xs = const.tile([P, 2, 512], U8, name="xs", align_bytes=64)
+        x1 = big.tile([P, 32, NA], F32, name="x1", tag="x1")
+
+        def load_w(words, scales, n, groups):
+            w = big.tile([P, 3 * groups * n], U8, name=uid("w"), tag="w", align_bytes=64)
+            codes = w[:, 0 : 2 * groups * n].rearrange("p (g n) -> p g n", g=groups)
+            planes = w[:, 2 * groups * n :].rearrange("p (g n) -> p g n", g=groups)
+            nc.gpsimd.memset(w[:, 2 * groups * n :].bitcast(I32), 0)
+            for q in range(4):
+                nc.sync.dma_start(
+                    out=planes[32 * q : 32 * q + 4, :, :].bitcast(I32),
+                    in_=scales[:, 4 * q : 4 * q + 4, :].rearrange("g q n -> q g n").bitcast(I32),
+                )
+            cuts = 4 if groups == 2 else 1
+            for c in range(cuts):
+                cols = slice(c * 2 * n // cuts, (c + 1) * 2 * n // cuts)
+                nc.sync.dma_start(out=codes[:, :, cols].bitcast(I32), in_=words[:, :, cols].rearrange("g p n -> p g n").bitcast(I32))
+            return codes, planes
+
+        with ExitStack() as front:
+            early = front.enter_context(tc.tile_pool(name="early", bufs=1))
+            psh = front.enter_context(tc.psum_pool(name="psh", bufs=1))
+            psf = front.enter_context(tc.psum_pool(name="psf", bufs=2))
+
+            scale_row = early.tile([P, D], F32, name="scale_row")
             x_bytes_tiles = {}
 
             def load_x(i):
-                xb = head.tile([P, D], U8, name="xb%d" % i, tag="xb", bufs=2)
+                xb = early.tile([P, D], U8, name="xb%d" % i, tag="xb", bufs=4)
                 nc.sync.dma_start(out=xb[:], in_=x_rows[i * P : (i + 1) * P, :])
                 x_bytes_tiles[i] = xb
 
+            pw = early.tile([P, 2048], BF16, name="pw")
+            nc.gpsimd.memset(pw[:].bitcast(I32), 0)
+            rw = early.tile([P, 512], BF16, name="rw")
+            nc.gpsimd.memset(rw[:].bitcast(I32), 0)
+            wq_raw = early.tile([P, 5, 64], BF16, name="wq_raw")
+            bq_raw = early.tile([P, 32], BF16, name="bq_raw")
+            nat_raw = early.tile([P, 1024], BF16, name="nat_raw")
+            nat = early.tile([P, 1024], F32, name="nat")
+
             load_x(0)
             load_x(1)
-
-            we_s = head.tile([P, 2, H], U8, name="we_s", align_bytes=64)
-            nc.gpsimd.memset(we_s[:].rearrange("p g n -> p (g n)").bitcast(I32), 0)
-            for q in range(4):
-                nc.sync.dma_start(
-                    out=we_s[32 * q : 32 * q + 4, :, :].bitcast(I32),
-                    in_=w_exp_scales[:, 4 * q : 4 * q + 4, :].rearrange("g q n -> q g n").bitcast(I32),
-                )
-            we = head.tile([P, 2, 2 * H], U8, name="we", align_bytes=64)
-            for c in range(4):
-                cols = slice(c * 2048, (c + 1) * 2048)
-                nc.sync.dma_start(
-                    out=we[:, :, cols].bitcast(I32), in_=w_exp_words[:, :, cols].rearrange("g p n -> p g n").bitcast(I32)
-                )
-
-            wq_raw = head.tile([P, 5, 64], BF16, name="wq_raw")
-            nc.sync.dma_start(out=wq_raw[:], in_=up_w[0:5].rearrange("s (q k) r c -> q s (k r c)", q=P))
-            wq = const.tile([P, 5, 64], F32, name="wq")
-            nc.gpsimd.tensor_copy(out=wq[:], in_=wq_raw[:])
-            bq_raw = head.tile([P, 32], BF16, name="bq_raw")
-            nc.sync.dma_start(out=bq_raw[:], in_=b_exp.rearrange("(q r) -> q r", q=P))
-
+            nc.sync.dma_start(out=scale_row[:], in_=x_scale.rearrange("a b k -> (a b k)").partition_broadcast(P))
+            we, we_s = load_w(w_exp_words, w_exp_scales, H, 2)
             load_x(2)
             load_x(3)
+            for st in range(7):
+                for n, w in enumerate((up_w, down_w)):
+                    at = 16 * st + 8 * n
+                    nc.sync.dma_start(out=nat_raw[at : at + 8, :], in_=w[2 + st].rearrange("(g k) r c -> g (k r c)", g=8))
+            nc.sync.dma_start(out=wq_raw[:], in_=up_w[0:5].rearrange("s (q k) r c -> q s (k r c)", q=P))
+            nc.sync.dma_start(out=bq_raw[:], in_=b_exp.rearrange("(q r) -> q r", q=P))
+            for n, w in enumerate((up_w, down_w)):
+                nc.sync.dma_start(out=pw[16 * n : 16 * n + 16, 0:1024], in_=w[0:2].rearrange("s (g k) r c -> (s g) (k r c)", g=8))
+                nc.sync.dma_start(out=pw[32 + 12 * n : 44 + 12 * n, :], in_=w[9:12].rearrange("s (h k) r c -> (s h) (k r c)", h=4))
+            nc.sync.dma_start(out=pw[64:72, 0:512], in_=b_exp.rearrange("(g e) -> g e", g=8))
+            nc.sync.dma_start(out=pw[72:80, 0:512], in_=up_bias.rearrange("(g e) -> g e", g=8))
+            for st in range(5):
+                nc.sync.dma_start(
+                    out=rw[16 * st : 16 * st + 16, :].rearrange("p (h e) -> p h e", h=4),
+                    in_=up_w[5 + st].rearrange("(h m p) r c -> m h (p r c)", h=4, m=16),
+                )
 
-            def load_wp(w, name):
-                raw = head.tile([P, 5, 64], BF16, name=name + "_raw")
-                for col, st in ((0, 0), (1, 1)):
-                    nc.sync.dma_start(
-                        out=raw[:, col, :].rearrange("p (g e) -> p g e", g=8), in_=w[st].rearrange("(g p e) r c -> p g (e r c)", g=8, p=P)
-                    )
-                for col, st in ((2, 9), (3, 10), (4, 11)):
-                    nc.sync.dma_start(
-                        out=raw[:, col, :].rearrange("p (g e) -> p g e", g=4), in_=w[st].rearrange("(g p e) r c -> p g (e r c)", g=4, p=P)
-                    )
-                full = const.tile([P, 5, 64], F32, name=name)
-                nc.gpsimd.tensor_copy(out=full[:], in_=raw[:])
-                return full
-
-            def load_vec_p(v, name):
-                raw = head.tile([P, 8, 4], BF16, name=name + "_raw")
-                nc.sync.dma_start(out=raw[:], in_=v.rearrange("(g p t) -> p g t", g=8, p=P))
-                return raw
-
-            wp_up = load_wp(up_w, "wp_up")
-            bp_raw = load_vec_p(b_exp, "bp")
-            ub_raw = load_vec_p(up_bias, "ub")
-            ub = const.tile([P, 32], F32, name="ub")
-            nc.gpsimd.tensor_copy(out=ub[:], in_=ub_raw[:].rearrange("p g t -> p (g t)"))
-
-            def stage0_bias(w, b_raw, name):
-                b32 = head.tile([P, 16, 2], F32, name=name + "_b32")
-                nc.gpsimd.tensor_copy(out=b32[:].rearrange("p k c -> p (k c)"), in_=b_raw)
-                prod = head.tile([P, 2, 16, 2], F32, name=name + "_prod")
-                res = const.tile([P, 16, 2], F32, name=name)
-                w4 = w[:, 0, :].rearrange("p (k r c) -> p r k c", r=2, c=2)
-                for r in range(2):
-                    nc.gpsimd.tensor_tensor(out=prod[:, r], in0=w4[:, r], in1=b32[:], op=MULT)
-                    nc.gpsimd.tensor_tensor(out=res[:, :, r], in0=prod[:, r, :, 0], in1=prod[:, r, :, 1], op=ADD)
-                return res
-
-            cq = stage0_bias(wq, bq_raw[:], "cq")
-            cp = stage0_bias(wp_up, bp_raw[:].rearrange("p g t -> p (g t)"), "cp")
-            wp_dn = load_wp(down_w, "wp_dn")
-
-            xq = const.tile([P, 2, 512], U32, name="xq", align_bytes=64)
-            xs = const.tile([P, 2, 512], U8, name="xs", align_bytes=64)
             xg_tiles = {}
 
             def prep_x(i):
-                xw = head.tile([P, D], BF16, name="xw%d" % i, tag="xw", bufs=2)
+                xw = early.tile([P, D], BF16, name="xw%d" % i, tag="xw", bufs=2)
                 nc.vector.tensor_tensor(out=xw[:], in0=x_bytes_tiles[i][:].bitcast(FP8), in1=scale_row[:], op=MULT)
                 words = xw[:].bitcast(F32)
-                xt = psh.tile([P, 2, 2, P], F32, name="xt%d" % i, tag="xt", bufs=1)
+                xt = psh.tile([P, 2, 2, P], F32, name="xt%d" % i, tag="xt", bufs=2)
                 for g in range(2):
                     for u in range(2):
                         nc.tensor.transpose(xt[:, g, u, :], words[:, 256 * g + u : 256 * (g + 1) : 2], ident[:])
                 if i % 2 == 0:
-                    xg_new = head.tile([P, 2, HALF, 4], BF16, name="xg%d" % i, tag="xg", bufs=1, align_bytes=64)
+                    xg_new = early.tile([P, 2, HALF, 4], BF16, name="xg%d" % i, tag="xg", bufs=1, align_bytes=64)
                     xg_tiles[i // 2] = xg_new
                 xg = xg_tiles[i // 2]
                 for g in range(2):
                     dst = xg[:, g, (i % 2) * P : (i % 2 + 1) * P, :].rearrange("p n t -> p (n t)").bitcast(F32)
                     nc.vector.tensor_copy(out=dst.rearrange("p (n u) -> p n u", u=2), in_=xt[:, g].rearrange("p u n -> p n u"))
-                if i % 2 == 1:
-                    tok = slice((i // 2) * HALF, (i // 2 + 1) * HALF)
-                    for g in range(2):
-                        nc.vector.quantize_mx(
-                            out=xq[:, g, tok].bitcast(FP8X4), scales=xs[:, g, tok], in_=xg[:, g].rearrange("p n t -> p (n t)")
-                        )
 
-            counter = {"n": 0, "id": 0}
+            def quantize_x(half):
+                tok = slice(half * HALF, (half + 1) * HALF)
+                for g in range(2):
+                    nc.vector.quantize_mx(
+                        out=xq[:, g, tok].bitcast(FP8X4), scales=xs[:, g, tok], in_=xg_tiles[half][:, g].rearrange("p n t -> p (n t)")
+                    )
 
-            def product(dst, src, w, c, on_chip):
-                counter["n"] += 1
-                if c is not None:
-                    nc.scalar.activation(out=dst, in_=src, func=IDENT, scale=w, bias=c)
-                elif on_chip and counter["n"] % V_EVERY == 0:
-                    nc.vector.tensor_scalar(out=dst, in0=src, scalar1=w, scalar2=None, op0=MULT)
+            def expand(ps, i, j):
+                tok = slice(i * P, (i + 1) * P)
+                for g in range(2):
+                    nc.tensor.matmul_mx(
+                        out=ps,
+                        lhsT=xq[:, g, tok].bitcast(FP8X4),
+                        lhsT_scale=xs[:, g, tok],
+                        rhs=we[:, g, 1024 * j : 1024 * (j + 1)].bitcast(FP4X4),
+                        rhs_scale=we_s[:, g, 512 * j : 512 * (j + 1)],
+                        start=(g == 0),
+                        stop=(g == 1),
+                    )
+
+            ht = big.tile([P, 2, H], F32, name="ht", tag="t32")
+
+            def a_expand(i, j, on_vector):
+                ps = psh.tile([P, 512], F32, name=uid("mx"), tag="mx", bufs=2)
+                expand(ps[:], i, j)
+                dst = ht[:, i].rearrange("p (r q) -> p r q", r=32)[:, :, 16 * j : 16 * (j + 1)]
+                src = ps[:].rearrange("p (q r) -> p r q", r=32)
+                if on_vector:
+                    nc.vector.tensor_copy(out=dst, in_=src)
                 else:
-                    nc.scalar.activation(out=dst, in_=src, func=COPY, scale=w)
+                    nc.scalar.copy(out=dst, in_=src)
 
-            def group(units, s):
-                parts = []
-                for a, b, na, nb, w, k, c, on_chip in units:
-                    counter["id"] += 1
-                    ta = tmp.tile([P, HALF], F32, name="ta%d" % counter["id"], tag="ta" + s)
-                    tb = tmp.tile([P, HALF], F32, name="tb%d" % counter["id"], tag="tb" + s)
-                    product(ta[:], a, w[:, 4 * k : 4 * k + 1], None if c is None else c[:, k, 0:1], on_chip)
-                    product(tb[:], a, w[:, 4 * k + 2 : 4 * k + 3], None if c is None else c[:, k, 1:2], on_chip)
-                    parts.append((ta, tb))
-                for (a, b, na, nb, w, k, c, on_chip), (ta, tb) in zip(units, parts):
-                    nc.vector.scalar_tensor_tensor(out=na, in0=b, scalar=w[:, 4 * k + 1 : 4 * k + 2], in1=ta[:], op0=MULT, op1=ADD)
-                for (a, b, na, nb, w, k, c, on_chip), (ta, tb) in zip(units, parts):
-                    nc.vector.scalar_tensor_tensor(out=nb, in0=b, scalar=w[:, 4 * k + 3 : 4 * k + 4], in1=tb[:], op0=MULT, op1=ADD)
+            def banks():
+                pa = psf.tile([P, 2, HALF], F32, name=uid("fa"), tag="fa")
+                pb = psf.tile([P, 2, HALF], F32, name=uid("fb"), tag="fb")
+                return pa, pb
 
-            def free_stage(x, w, s_bit, pairs, s):
-                units = []
-                for k in pairs:
-                    i = (k // s_bit) * 2 * s_bit + k % s_bit
-                    j = i + s_bit
-                    units.append((x[:, i, :], x[:, j, :], x[:, i, :], x[:, j, :], w, k, None, True))
-                group(units, s)
+            def spread_weights():
+                def turns(src, n, step):
+                    ps = psh.tile([P, 8, P], BF16, name=uid("wt"), tag="xt", bufs=2)
+                    for j, at in n:
+                        nc.tensor.transpose(ps[:, j, :], src[:, at : P * step : step], ident_b[:])
+                    return ps
 
-            ht_tiles = {}
-
-            def expand(i, order):
-                ht = head.tile([P, H], F32, name="ht%d" % i, tag="ht", bufs=2)
-                ht_tiles[i] = ht
-                for j in range(8):
-                    ps = psh.tile([P, 512], F32, name="mx%d_%d" % (i, j), tag="mx", bufs=3)
-                    for g in range(2):
-                        nc.tensor.matmul_mx(
-                            out=ps[:],
-                            lhsT=xq[:, g, i * P : (i + 1) * P].bitcast(FP8X4),
-                            lhsT_scale=xs[:, g, i * P : (i + 1) * P],
-                            rhs=we[:, g, 1024 * j : 1024 * (j + 1)].bitcast(FP4X4),
-                            rhs_scale=we_s[:, g, 512 * j : 512 * (j + 1)],
-                            start=(g == 0),
-                            stop=(g == 1),
-                        )
-                    if order == "q":
-                        dst = ht[:].rearrange("p (r q) -> p r q", r=32)[:, :, 16 * j : 16 * (j + 1)]
-                        src = ps[:].rearrange("p (q r) -> p r q", r=32)
-                    else:
-                        dst = ht[:, 512 * j : 512 * (j + 1)].rearrange("p (t q) -> p t q", t=4)
-                        src = ps[:].rearrange("p (q t) -> p t q", t=4)
-                    if order == "q" and j % 2 == 1:
-                        nc.vector.tensor_copy(out=dst, in_=src)
-                    else:
-                        nc.scalar.copy(out=dst, in_=src)
-
-            def turn(dst, i0, blk):
-                for ii in range(2):
-                    nc.tensor.transpose(dst[:, ii * P : (ii + 1) * P], ht_tiles[i0 + ii][:, blk * P : (blk + 1) * P], ident[:])
-
-            def bank(kind, tag):
-                counter["id"] += 1
-                ps = psf.tile([P, 2, HALF], F32, name="%s%d" % (kind, counter["id"]), tag=tag)
-                return ps
-
-            bit_of = const.tile([P, 7, 2], F32, name="bit_of")
-            for b in range(5):
-                nc.vector.tensor_reduce(
-                    out=bit_of[:, b, 1:2],
-                    in_=ident[:].rearrange("p (h b l) -> p b h l", b=2, l=2**b)[:, 1],
-                    axis=mybir.AxisListType.XY,
-                    op=ADD,
-                )
-                nc.vector.tensor_scalar(out=bit_of[:, b, 0:1], in0=bit_of[:, b, 1:2], scalar1=-1.0, scalar2=1.0, op0=MULT, op1=ADD)
-
-            def dense(w, name, scratch):
-                f6 = head.tile([P, 8, 16], BF16, name=name + "_f6", tag="f6")
-                for half in range(2):
-                    nc.sync.dma_start(out=f6[64 * half : 64 * half + 64, :, :], in_=w[8].rearrange("(g u t) r c -> u g (t r c)", g=8, u=64))
-                f5 = head.tile([P, 16, 16], BF16, name=name + "_f5", tag="f5")
-                for q in range(4):
-                    nc.sync.dma_start(out=f5[32 * q : 32 * q + 32, :, :], in_=w[7].rearrange("(g u t) r c -> u g (t r c)", g=16, u=32))
-                s6 = head.tile([P, 8, 4, 2], F32, name=name + "_s6", tag="s6")
-                for half in range(2):
-                    rows = slice(64 * half, 64 * half + 64)
+                ps = turns(pw, [(j, j) for j in range(8)], 8)
+                for n, wp in enumerate((wp_up, wp_dn)):
                     nc.vector.tensor_copy(
-                        out=s6[rows].rearrange("p g t c -> p (g t) c"),
-                        in_=f6[rows].rearrange("p g (t r c) -> p r (g t) c", r=2, c=2)[:, half],
+                        out=wp[:, 0:2, :].rearrange("p s (g j) -> p (s g) j", j=8), in_=ps[:, :, 16 * n : 16 * n + 16].rearrange("p j s -> p s j")
                     )
-                s5 = head.tile([P, 16, 4, 2], F32, name=name + "_s5", tag="s5")
-                for q in range(4):
-                    rows = slice(32 * q, 32 * q + 32)
-                    nc.vector.tensor_copy(
-                        out=s5[rows].rearrange("p g t c -> p (g t) c"),
-                        in_=f5[rows].rearrange("p g (t r c) -> p r (g t) c", r=2, c=2)[:, q % 2],
-                    )
-                rt = head.tile([P, 2, 2, 8, 4], F32, name=name + "_rt", tag="rt")
-                for i6 in range(2):
-                    for i5 in range(2):
-                        nc.vector.tensor_tensor(
-                            out=rt[:, i6, i5],
-                            in0=s6[:].rearrange("p g t c -> p c g t")[:, i6],
-                            in1=s5[:].rearrange("p (g x) t c -> p x c g t", x=2)[:, i6, i5],
-                            op=MULT,
+                for hf in range(2):
+                    ps = turns(pw, [(j, 8 * hf + j) for j in range(8)], 16)
+                    for n, wp in enumerate((wp_up, wp_dn)):
+                        nc.vector.tensor_copy(
+                            out=wp[:, 2:5, :].rearrange("p s (h j) -> p (s h) j", j=16)[:, :, 8 * hf : 8 * hf + 8],
+                            in_=ps[:, :, 32 + 12 * n : 44 + 12 * n].rearrange("p j s -> p s j"),
                         )
-                ps = psh.tile([P, 2, 2, P], F32, name=name + "_ps", tag="xt", bufs=1)
-                nc.tensor.transpose(ps[:, 0, 0, :], rt[:].rearrange("p x y g t -> p (x y g t)"), ident[:])
-                rows_sb = head.tile([P, P], F32, name=name + "_rows", tag="rows")
-                nc.vector.tensor_copy(out=rows_sb[:], in_=ps[:, 0, 0, :])
-                nc.sync.dma_start(out=scratch.rearrange("(p o) -> p o", p=P), in_=rows_sb[:])
-                mt = const.tile([P, 32 * P], F32, name=name)
-                for q in range(4):
-                    nc.sync.dma_start(
-                        out=mt[32 * q : 32 * q + 32, :], in_=scratch[32 * P * q : 32 * P * (q + 1)].partition_broadcast(32)
-                    )
-                low = None
+                ps = turns(pw, [(j, j) for j in range(4)], 4)
+                nc.vector.tensor_copy(out=bp[:].rearrange("p (g t) -> p g t", t=4), in_=ps[:, 0:4, 64:72].rearrange("p t g -> p g t"))
+                nc.vector.tensor_copy(out=ub[:].rearrange("p (g t) -> p g t", t=4), in_=ps[:, 0:4, 72:80].rearrange("p t g -> p g t"))
+                ps = turns(rw, [(j, j) for j in range(4)], 4)
+                nc.vector.tensor_copy(out=wr[:].rearrange("p s (m c) -> p (s m) c", c=4), in_=ps[:, 0:4, 0:80].rearrange("p c s -> p s c"))
+
+            def stage0_bias(w, b32, res):
+                prod = early.tile([P, 2, 16, 2], F32, name=uid("prod"), tag="prod", bufs=2)
+                w4 = w[:, 0, :].rearrange("p (k r c) -> p r k c", r=2, c=2)
+                for r in range(2):
+                    nc.gpsimd.tensor_tensor(out=prod[:, r], in0=w4[:, r], in1=b32, op=MULT)
+                    nc.gpsimd.tensor_tensor(out=res[:, :, r], in0=prod[:, r, :, 0], in1=prod[:, r, :, 1], op=ADD)
+
+            def q_weights():
+                bq = early.tile([P, 16, 2], F32, name="bq")
+                nc.gpsimd.tensor_copy(out=wq[:], in_=wq_raw[:])
+                nc.gpsimd.tensor_copy(out=bq[:].rearrange("p k c -> p (k c)"), in_=bq_raw[:])
+                stage0_bias(wq, bq[:], cq)
+
+            def bit_columns():
                 for b in range(5):
-                    n = 2**b
+                    nc.vector.tensor_reduce(
+                        out=bit_of[:, b, 1:2],
+                        in_=ident[:].rearrange("p (h b l) -> p b h l", b=2, l=2**b)[:, 1],
+                        axis=mybir.AxisListType.XY,
+                        op=ADD,
+                    )
+                nc.vector.tensor_scalar(out=bit_of[:, :, 0], in0=bit_of[:, :, 1], scalar1=-1.0, scalar2=1.0, op0=MULT, op1=ADD)
+
+            def scratch(b):
+                return out_flat[b * 16384 : (b + 1) * 16384]
+
+            def park_factors():
+                for b in range(7):
+                    rows = nat[16 * b : 16 * b + 16, :]
+                    if b < 4:
+                        nc.sync.dma_start(
+                            out=scratch(b).rearrange("(h g e) -> g h e", g=16, h=2 ** (6 - b)),
+                            in_=rows.rearrange("g (h e) -> g h e", h=2 ** (6 - b)),
+                        )
+                    else:
+                        for x in range(2 ** (6 - b)):
+                            nc.sync.dma_start(
+                                out=scratch(b).rearrange("(x u g e) -> x g u e", u=2**b, g=16, e=16)[x],
+                                in_=rows.rearrange("g (x u e) -> x g u e", u=2**b, e=16)[x],
+                            )
+
+            factors = {}
+
+            def fetch_factors(b):
+                if b < 4:
                     h = 2 ** (6 - b)
                     rep = P // h
-                    f = head.tile([P, 8, 16 * n], BF16, name="%s_f%d" % (name, b), tag="f%d" % b)
-                    src = w[b + 2].rearrange("(g h e) r c -> h g (e r c)", g=8, h=h)
+                    f = early.tile([P, 16, 16 * 2**b], F32, name="f%d" % b)
+                    flat = f[:].rearrange("p g e -> p (g e)")
+                    src = scratch(b).rearrange("(h z) -> h z", h=h)
                     if b < 3:
                         for r in range(rep):
-                            nc.sync.dma_start(out=f[r:P:rep, :, :], in_=src)
+                            nc.sync.dma_start(out=flat[r:P:rep, :], in_=src)
                     else:
-                        for hi in range(h):
-                            nc.sync.dma_start(out=f[hi * rep : (hi + 1) * rep, :, :], in_=src[hi].partition_broadcast(rep))
-                    parts = []
-                    for c in range(2):
-                        m = head.tile([P, 8, 8, n], F32, name="%s_m%d_%d" % (name, b, c), tag="msel%d" % c)
-                        nc.scalar.activation(
-                            out=m[:], in_=f[:].rearrange("p g (o x c) -> p c g x o", x=8, c=2)[:, c], func=COPY, scale=bit_of[:, b, c : c + 1]
-                        )
-                        parts.append(m)
-                    sel = head.tile([P, 32, 2, n], F32, name="%s_l%d" % (name, b), tag="l%d" % b)
-                    m0, m1 = [m[:].rearrange("p g x o -> p (g x o)") for m in parts]
-                    nc.vector.tensor_tensor(out=sel[:].rearrange("p k r o -> p (k r o)"), in0=m0, in1=m1, op=ADD)
-                    if b > 0:
-                        for r in range(2):
-                            nc.vector.tensor_tensor(
-                                out=sel[:, :, r, :], in0=sel[:, :, r, :], in1=low[:].rearrange("p k r o -> p k (r o)"), op=MULT
-                            )
-                    low = sel
-                mt4 = mt[:].rearrange("p (k h l) -> p h k l", h=4, l=32)
-                for hh in range(4):
-                    nc.vector.tensor_tensor(
-                        out=mt4[:, hh], in0=mt4[:, hh], in1=low[:].rearrange("p k r o -> p k (r o)"), op=MULT
-                    )
-                return mt
-
-            def stages_0_1(x, w, g, i0, c, s):
-                blk = 4 * g
-                if i0 is None:
-                    free_stage(x, w[:, 0, :], 1, (2 * g, 2 * g + 1), s)
+                        for top in range(h):
+                            nc.sync.dma_start(out=flat[top * rep : (top + 1) * rep, :], in_=src[top].partition_broadcast(rep))
                 else:
-                    pa = bank("fa", "fa")
-                    pb = bank("fb", "fb")
-                    for t in range(4):
-                        turn((pa, pb)[t % 2][:, t // 2, :], i0, blk + t)
-                    group(
-                        [
-                            (pa[:, n, :], pb[:, n, :], x[:, blk + 2 * n, :], x[:, blk + 2 * n + 1, :], w[:, 0, :], 2 * g + n, c, False)
-                            for n in range(2)
-                        ],
-                        s,
+                    f = early.tile([P, 2 ** (6 - b) * 16, 16], F32, name="f%d" % b)
+                    rows = 2**b
+                    for r in range(P // rows):
+                        nc.sync.dma_start(
+                            out=f[r * rows : (r + 1) * rows].rearrange("p (x g) e -> p x (g e)", g=16),
+                            in_=scratch(b).rearrange("(x u z) -> u x z", u=rows, z=256),
+                        )
+                factors[b] = f
+
+            def high_a():
+                s6 = early.tile([P, 64, 2], F32, name="s6")
+                for hf in range(2):
+                    rows = slice(64 * hf, 64 * hf + 64)
+                    nc.vector.tensor_copy(out=s6[rows], in_=factors[6][rows].rearrange("p g (t r c) -> p r (g t) c", r=2, c=2)[:, hf])
+                s5 = early.tile([P, 128, 2], F32, name="s5")
+                for q in range(4):
+                    rows = slice(32 * q, 32 * q + 32)
+                    nc.vector.tensor_copy(out=s5[rows], in_=factors[5][rows].rearrange("p g (t r c) -> p r (g t) c", r=2, c=2)[:, q % 2])
+                factors["s6"] = s6
+                factors["s5"] = s5
+
+            def high_b():
+                parts = []
+                for r in range(2):
+                    m = early.tile([P, 256, 2], F32, name="s4_%d" % r, tag="msel%d" % r)
+                    nc.scalar.activation(
+                        out=m[:],
+                        in_=factors[4][:].rearrange("p g (t r c) -> p r (g t) c", r=2, c=2)[:, r],
+                        func=COPY,
+                        scale=bit_of[:, 4, r : r + 1],
                     )
-                free_stage(x, w[:, 1, :], 2, (2 * g, 2 * g + 1), s)
+                    parts.append(m)
+                s4 = early.tile([P, 256, 2], F32, name="s4")
+                nc.vector.tensor_tensor(out=s4[:], in0=parts[0][:], in1=parts[1][:], op=ADD)
+                factors["s4"] = s4
 
-            def stages_2_9(x, w, mt, h, s):
-                for t0 in (0, 2):
-                    pa = bank("fa", "fa")
-                    pb = bank("fb", "fb")
-                    for n in range(2):
-                        for side, ps in ((0, pa), (1, pb)):
-                            blk = 4 * (2 * h + side) + t0 + n
-                            nc.tensor.matmul(out=ps[:, n, :], lhsT=mt[:, blk * P : (blk + 1) * P], rhs=x[:, blk, :], start=True, stop=True)
-                    group(
-                        [
-                            (
-                                pa[:, n, :],
-                                pb[:, n, :],
-                                x[:, 8 * h + t0 + n, :],
-                                x[:, 8 * h + 4 + t0 + n, :],
-                                w[:, 2, :],
-                                4 * h + t0 + n,
-                                None,
-                                False,
-                            )
-                            for n in range(2)
-                        ],
-                        s,
+            def high_c():
+                t5 = early.tile([P, 2, 2, 16, 4], F32, name="t5")
+                for x in range(2):
+                    for y in range(2):
+                        nc.vector.tensor_tensor(
+                            out=t5[:, x, y],
+                            in0=factors["s6"][:].rearrange("p (g t) c -> p c g t", t=4)[:, x],
+                            in1=factors["s5"][:].rearrange("p (x g t) c -> p x c g t", x=2, t=4)[:, x, y],
+                            op=MULT,
+                        )
+                rt = early.tile([P, 8, 16, 4], F32, name="rt")
+                for x in range(4):
+                    for z in range(2):
+                        nc.vector.tensor_tensor(
+                            out=rt[:, 2 * x + z],
+                            in0=t5[:, x // 2, x % 2],
+                            in1=factors["s4"][:].rearrange("p (x g t) c -> p x c g t", x=4, t=4)[:, x, z],
+                            op=MULT,
+                        )
+                factors["rt"] = rt
+
+            def high_d():
+                ps = psh.tile([P, 4, P], F32, name="rows_ps", tag="xt", bufs=2)
+                flat = factors["rt"][:].rearrange("p x g t -> p (x g t)")
+                for x in range(4):
+                    nc.tensor.transpose(ps[:, x, :], flat[:, x * P : (x + 1) * P], ident[:])
+                rows_sb = early.tile([P, 4, P], F32, name="rows_sb")
+                nc.vector.tensor_copy(out=rows_sb[:], in_=ps[:])
+                area = out_flat[131072 : 131072 + 65536]
+                nc.sync.dma_start(out=area.rearrange("(x p o) -> p x o", x=4, p=P), in_=rows_sb[:])
+                for q in range(8):
+                    nc.sync.dma_start(out=mt[16 * q : 16 * q + 16, :], in_=area[8192 * q : 8192 * (q + 1)].partition_broadcast(16))
+
+            def low_part(b):
+                f = factors[b]
+                k = 2**b
+                pair = []
+                for c in range(2):
+                    m = early.tile([P, 16, 8, k], F32, name="m%d_%d" % (b, c), tag="msel%d" % c)
+                    nc.scalar.activation(
+                        out=m[:], in_=f[:].rearrange("p g (o x c) -> p c g x o", x=8, c=2)[:, c], func=COPY, scale=bit_of[:, b, c : c + 1]
                     )
+                    pair.append(m)
+                if b == 3:
+                    sel = low
+                else:
+                    sel = early.tile([P, 64, 2, k], F32, name="l%d" % b)
+                nc.vector.tensor_tensor(
+                    out=sel[:].rearrange("p k r o -> p (k r o)"),
+                    in0=pair[0][:].rearrange("p g x o -> p (g x o)"),
+                    in1=pair[1][:].rearrange("p g x o -> p (g x o)"),
+                    op=ADD,
+                )
+                if b > 0:
+                    for r in range(2):
+                        nc.vector.tensor_tensor(
+                            out=sel[:, :, r, :],
+                            in0=sel[:, :, r, :],
+                            in1=factors[("low", b - 1)][:].rearrange("p k r o -> p k (r o)"),
+                            op=MULT,
+                        )
+                factors[("low", b)] = sel
 
-            def stage_10(x, w, h2, g0, s):
-                free_stage(x, w[:, 3, :], 8, [8 * h2 + 4 * g0 + t for t in range(4)], s)
-
-            def stage_11(x, w, gg, s):
-                free_stage(x, w[:, 4, :], 16, [4 * gg + t for t in range(4)], s)
-
-            def gelu(x, blks):
-                for blk in blks:
-                    nc.scalar.activation(out=x[:, blk, :], in_=x[:, blk, :], func=GELU, bias=ub[:, blk : blk + 1])
-
+            bit_columns()
+            q_weights()
             prep_x(0)
             prep_x(1)
-            expand(0, "q")
-            expand(1, "q")
-            mt_up = dense(up_w, "mt_up", out_flat[0 : P * P])
-            x1 = big.tile([P, 32, HALF], F32, name="x1", tag="x1")
+            quantize_x(0)
             for j in range(8):
-                pa = bank("fa", "fa")
-                pb = bank("fb", "fb")
+                for i in range(2):
+                    a_expand(i, j, i == 1)
+                if j == 4:
+                    prep_x(2)
+                if j == 5:
+                    prep_x(3)
+                    nc.scalar.copy(out=nat[0:112, :], in_=nat_raw[0:112, :])
+            quantize_x(1)
+            park_factors()
+            for b in (0, 1, 6, 5, 4, 2, 3):
+                fetch_factors(b)
+            def a_stage0(j):
+                pa, pb = banks()
                 for n in range(4):
-                    turn((pa, pb)[n % 2][:, n // 2, :], 0, 4 * j + n)
+                    blk = 4 * j + n
+                    for i in range(2):
+                        nc.tensor.transpose((pa, pb)[n % 2][:, n // 2, i * P : (i + 1) * P], ht[:, i, blk * P : (blk + 1) * P], ident[:])
                 group(
                     [
-                        (pa[:, n, :], pb[:, n, :], x1[:, 4 * j + 2 * n, :], x1[:, 4 * j + 2 * n + 1, :], wq[:, 0, :], 2 * j + n, cq, False)
+                        (pa[:, n, 0:NA], pb[:, n, 0:NA], x1[:, 4 * j + 2 * n, :], x1[:, 4 * j + 2 * n + 1, :], wq[:, 0, :], 2 * j + n, cq)
                         for n in range(2)
-                    ],
-                    "1",
+                    ]
                 )
-            for st in range(1, 4):
-                for j in range(4):
-                    free_stage(x1, wq[:, st, :], 2**st, range(4 * j, 4 * j + 4), "1")
-            prep_x(2)
-            prep_x(3)
-            expand(2, "p")
-            expand(3, "p")
-            mt_dn = dense(down_w, "mt_dn", out_flat[P * P : 2 * P * P])
-            xb_half = big.tile([P, 32, HALF], F32, name="xb_half", tag="xb_half")
-            for g in range(8):
-                stages_0_1(xb_half, wp_up, g, 2, cp, "2")
 
-        tail = ctx.enter_context(tc.tile_pool(name="tail", bufs=1))
-        psa = ctx.enter_context(tc.psum_pool(name="psa", bufs=1))
-        wr_raw = tail.tile([P, 5, 64], BF16, name="wr_raw")
-        for st in range(5):
-            for hi in range(4):
-                nc.sync.dma_start(
-                    out=wr_raw[32 * hi : 32 * hi + 32, st, :].rearrange("p (m e) -> p m e", m=16),
-                    in_=up_w[5 + st].rearrange("(h m p) r c -> h p m (r c)", h=4, m=16)[hi],
-                )
-        wr = const.tile([P, 5, 64], F32, name="wr")
-        nc.gpsimd.tensor_copy(out=wr[:], in_=wr_raw[:])
-        wc_s = tail.tile([P, 8, D], U8, name="wc_s", align_bytes=64)
-        nc.gpsimd.memset(wc_s[:].rearrange("p g n -> p (g n)").bitcast(I32), 0)
+            def a_stage(st, j, share=0):
+                free_stage(lambda i: x1[:, i, :], wq[:, st, :], 2**st, range(4 * j, 4 * j + 4), share)
 
-        x2 = tail.tile([P, 32, HALF], F32, name="x2", tag="x2")
-        for c in range(4):
-            free_stage(x1, wq[:, 4, :], 16, (c, c + 4, c + 8, c + 12), "1")
-            reg = out_flat[(c % 2) * region : (c % 2 + 1) * region]
-            nc.sync.dma_start(out=reg.rearrange("(q r n) -> q r n", q=P, r=8), in_=x1[:, c:32:4, :])
-            for hi in range(4):
-                nc.sync.dma_start(
-                    out=x2[32 * hi + c : 32 * hi + 32 : 4, :, :], in_=reg.rearrange("(h m r n) -> h r m n", h=4, m=32, r=8)[hi]
-                )
-        for q in range(4):
-            nc.sync.dma_start(
-                out=wc_s[32 * q : 32 * q + 4, :, :].bitcast(I32),
-                in_=w_con_scales[:, 4 * q : 4 * q + 4, :].rearrange("g q n -> q g n").bitcast(I32),
-            )
-        wc = tail.tile([P, 8, 2 * D], U8, name="wc", align_bytes=64)
-        nc.sync.dma_start(out=wc[:].bitcast(I32), in_=w_con_words.rearrange("g p n -> p g n").bitcast(I32))
-        bias_raw = tail.tile([P, 2, D], BF16, name="bias_raw")
-        nc.sync.dma_start(out=bias_raw[:, 0, :], in_=b_con.partition_broadcast(P))
-        nc.sync.dma_start(out=bias_raw[:, 1, :], in_=down_bias.partition_broadcast(P))
-        bias = tail.tile([P, D], F32, name="bias")
-        nc.gpsimd.tensor_tensor(out=bias[:], in0=bias_raw[:, 0, :], in1=bias_raw[:, 1, :], op=ADD)
+            for j in range(8):
+                a_stage0(j)
+            a_stage(1, 0, SHARE_A)
+            a_stage(1, 1, SHARE_A)
+            spread_weights()
+            stage0_bias(wp_up, bp[:].rearrange("p (k c) -> p k c", c=2), cp)
+            rest = [lambda st=st, j=j: a_stage(st, j, SHARE_A) for st in range(1, 4) for j in range(4)][2:]
+            side = [lambda: low_part(0), high_a, lambda: low_part(1), high_b, high_c, lambda: low_part(2), high_d, lambda: low_part(3)]
+            weave((rest, 0, 1), (side, SIDE_FROM, 1))
 
-        def up_tail(x, h):
-            stages_2_9(x, wp_up, mt_up, h, "2")
+        xpool = ctx.enter_context(tc.tile_pool(name="xpool", bufs=1))
+        x = xpool.tile([P, 32, 512], F32, name="x")
 
-        for h in range(4):
-            up_tail(xb_half, h)
-            if h % 2 == 1:
-                for g0 in range(2):
-                    stage_10(xb_half, wp_up, h // 2, g0, "2")
-        for gg in range(4):
-            stage_11(xb_half, wp_up, gg, "2")
-            gelu(xb_half, [4 * gg + t for t in range(4)])
-            gelu(xb_half, [16 + 4 * gg + t for t in range(4)])
+        def xb(i):
+            return x[:, i, NA:512]
 
-        def down(x, tok0, s):
-            for h in range(4):
-                for g in (2 * h, 2 * h + 1):
-                    stages_0_1(x, wp_dn, g, None, None, s)
-                stages_2_9(x, wp_dn, mt_dn, h, s)
-                if h % 2 == 1:
-                    for g0 in range(2):
-                        stage_10(x, wp_dn, h // 2, g0, s)
-            accs = {}
-            for i in range(2):
-                for d in range(2):
-                    acc = psa.tile([P, 512], F32, name="acc%d_%d_%d" % (tok0, i, d), tag="acc%d%d" % (i, d))
-                    accs[(i, d)] = acc
-            done = 0
-            for gg in range(4):
-                outs = []
-                for g in (gg, gg + 4):
-                    hb = tail.tile([P, 4, HALF], BF16, name="hb%d_%d" % (tok0, g), tag="hb", bufs=4)
-                    outs.append(hb)
+        def xw(i):
+            return x[:, i, :]
+
+        with ExitStack() as middle:
+            ps0 = middle.enter_context(tc.psum_pool(name="ps0", bufs=2))
+            turned = middle.enter_context(tc.tile_pool(name="turned", bufs=2))
+
+            turned_tiles = {}
+
+            def b_expand(g):
+                hg = turned.tile([P, 3, 4, P], F32, name=uid("hg"), tag="hg")
+                for i in range(3):
+                    ps = ps0.tile([P, 512], F32, name=uid("mx"), tag="mx", bufs=4)
+                    expand(ps[:], i + 1, g)
+                    src = ps[:].rearrange("p (q t) -> p t q", t=4)
+                    if i == 0 and g % 2 == 0:
+                        nc.vector.tensor_copy(out=hg[:, i], in_=src)
+                    else:
+                        nc.scalar.copy(out=hg[:, i], in_=src)
+                turned_tiles[g] = hg
+
+            def b_stage0(g):
+                hg = turned_tiles[g]
                 units = []
-                for t in range(4):
-                    units.append((x[:, 4 * gg + t, :], x[:, 16 + 4 * gg + t, :], outs[0][:, t, :], outs[1][:, t, :], wp_dn[:, 4, :], 4 * gg + t, None, True))
-                group(units, s)
-                for g, hb in zip((gg, gg + 4), outs):
-                    hi = tail.tile([P, HALF, 4], BF16, name="hi%d_%d" % (tok0, g), tag="hi", bufs=2, align_bytes=64)
-                    nc.scalar.copy(out=hi[:], in_=hb[:].rearrange("p t n -> p n t"))
-                    hc = tail.tile([P, HALF], U32, name="hc%d_%d" % (tok0, g), tag="hc", bufs=2, align_bytes=64)
-                    hs = tail.tile([P, HALF], U8, name="hs%d_%d" % (tok0, g), tag="hs", bufs=2, align_bytes=64)
-                    nc.vector.quantize_mx(out=hc[:].bitcast(FP8X4), scales=hs[:], in_=hi[:].rearrange("p n t -> p (n t)"))
-                    for i in range(2):
-                        for d in range(2):
-                            nc.tensor.matmul_mx(
-                                out=accs[(i, d)][:],
-                                lhsT=hc[:, i * P : (i + 1) * P].bitcast(FP8X4),
-                                lhsT_scale=hs[:, i * P : (i + 1) * P],
-                                rhs=wc[:, g, 1024 * d : 1024 * (d + 1)].bitcast(FP4X4),
-                                rhs_scale=wc_s[:, g, 512 * d : 512 * (d + 1)],
-                                start=(done == 0),
-                                stop=(done == 7),
-                            )
-                    done += 1
-            for i in range(2):
-                for d in range(2):
-                    o = tail.tile([P, 512], F32, name="o%d_%d_%d" % (tok0, i, d), tag="o", bufs=4)
-                    nc.vector.tensor_tensor(out=o[:], in0=accs[(i, d)][:], in1=bias[:, 512 * d : 512 * (d + 1)], op=ADD)
-                    r0 = tok0 + i * P
-                    nc.sync.dma_start(out=out_rows[r0 : r0 + P, 512 * d : 512 * (d + 1)], in_=o[:])
+                for n in range(2):
+                    pair = []
+                    for t in (2 * n, 2 * n + 1):
+                        ps = ps0.tile([P, 512], F32, name=uid("b"), tag="fa" if t % 2 == 0 else "fb")
+                        for i in range(3):
+                            nc.tensor.transpose(ps[:, i * P : (i + 1) * P], hg[:, i, t, :], ident[:])
+                        pair.append(ps[:, 384 - NB : 384])
+                    i = 4 * g + 2 * n
+                    units.append((pair[0], pair[1], xb(i), xb(i + 1), wp_up[:, 0, :], 2 * g + n, cp))
+                group(units)
 
-        for st in range(5):
-            for j in range(4):
-                if st < 4:
-                    free_stage(x2, wr[:, st, :], 2**st, range(4 * j, 4 * j + 4), "1")
-        x3 = big.tile([P, 8, 4 * HALF], F32, name="x3", tag="x1")
-        for c in range(4):
-            free_stage(x2, wr[:, 4, :], 16, range(4 * c, 4 * c + 4), "1")
-            reg = out_flat[(c % 2) * region : (c % 2 + 1) * region].rearrange("(v m z) -> v m z", v=2, m=4)
-            for v in range(2):
-                nc.sync.dma_start(
-                    out=reg[v].rearrange("m (z n) -> z m n", z=P), in_=x2[:, 16 * v + 4 * c : 16 * v + 4 * c + 4, :]
-                )
-            for m in range(4):
-                for v in range(2):
-                    p0 = (4 * c + m) * 8
+            def b_stage1(j):
+                free_stage(xb, wp_up[:, 1, :], 2, range(4 * j, 4 * j + 4), SHARE_B)
+
+            def finish_dense(n, h):
+                view = mt[:, n * 4096 : (n + 1) * 4096].rearrange("p (k h l) -> p h k l", h=8, l=16)[:, h]
+                nc.vector.tensor_tensor(out=view, in0=view, in1=low[:, 32 * n : 32 * n + 32].rearrange("p k r o -> p k (r o)"), op=MULT)
+
+            def b_stage9(h, t0):
+                units = []
+                for t in (t0, t0 + 1):
+                    pair = []
+                    for side_ in range(2):
+                        blk = 4 * (2 * h + side_) + t
+                        ps = psg.tile([P, 512], F32, name=uid("b"), tag="fa" if side_ == 0 else "fb")
+                        nc.tensor.matmul(out=ps[:, 0:NB], lhsT=mt[:, blk * P : (blk + 1) * P], rhs=xb(blk), start=True, stop=True)
+                        pair.append(ps[:, 0:NB])
+                    i = 8 * h + t
+                    units.append((pair[0], pair[1], xb(i), xb(i + 4), wp_up[:, 2, :], 4 * h + t, None))
+                group(units)
+
+            def region(c):
+                return out_flat[(c % 2) * REGION : (c % 2 + 1) * REGION]
+
+            def q_store(c):
+                for h in range(4):
                     nc.sync.dma_start(
-                        out=x3[p0 : p0 + 8, v:8:2, :], in_=reg[v, m].rearrange("(h p n) -> p h n", h=4, p=8)
+                        out=region(c).rearrange("(h r m n) -> h m r n", h=4, r=8, m=32)[h], in_=x1[32 * h : 32 * h + 32, c:32:4, :]
                     )
-        down(xb_half, HALF, "2")
-        x3v = x3[:].rearrange("p g (t n) -> p (g t) n", t=4)
-        for h2 in range(2):
-            for g0 in range(2):
-                stage_10(x3v, wp_up, h2, g0, "1")
-        for gg in range(4):
-            stage_11(x3v, wp_up, gg, "1")
-            gelu(x3v, [4 * gg + t for t in range(4)])
-            gelu(x3v, [16 + 4 * gg + t for t in range(4)])
-        down(x3v, 0, "1")
+
+            def r_load(c):
+                nc.sync.dma_start(out=x2[c:P:4].rearrange("p m n -> p (m n)"), in_=region(c).rearrange("(z e) -> z e", z=32))
+
+            x2 = big.tile([P, 32, NA], F32, name="x2", tag="t32")
+
+            def a_stage4(c, hf):
+                free_stage(lambda i: x1[:, i, :], wq[:, 4, :], 16, (c + 8 * hf, c + 4 + 8 * hf), SHARE_4)
+                if hf == 1:
+                    q_store(c)
+                    if c > 0:
+                        r_load(c - 1)
+
+            b_expand(0)
+            first_b = []
+            for g in range(8):
+                if g < 7:
+                    first_b.append(lambda g=g: b_expand(g + 1))
+                first_b.append(lambda g=g: b_stage0(g))
+            weave(
+                (first_b, 0, 1),
+                ([lambda c=c, hf=hf: a_stage4(c, hf) for c in range(4) for hf in range(2)], 0, 1),
+            )
+            r_load(3)
+
+        with ExitStack() as middle:
+            psg = middle.enter_context(tc.psum_pool(name="psg", bufs=4))
+            wc, wc_s = load_w(w_con_words, w_con_scales, D, 8)
+            bias_parts = []
+            for n, vec in enumerate((b_con, down_bias)):
+                raw = tmp.tile([P, D], BF16, name="bias_raw%d" % n, tag="taw" if n == 0 else "tbw", bufs=BUFS_WIDE)
+                nc.sync.dma_start(out=raw[:], in_=vec.partition_broadcast(P))
+                bias_parts.append(raw)
+            bias = const.tile([P, D], F32, name="bias")
+            nc.gpsimd.tensor_tensor(out=bias[:], in0=bias_parts[0][:], in1=bias_parts[1][:], op=ADD)
+            x3 = big.tile([P, 32, NA], F32, name="x3", tag="x1")
+            weave(
+                ([lambda j=j: b_stage1(j) for j in range(4)], 0, 1),
+                ([lambda h=h, n=n: finish_dense(n, h) for n in range(2) for h in range(8)], 0, 1),
+            )
+
+            def r_store(c):
+                reg = region(c).rearrange("(v m z) -> v m z", v=2, m=4)
+                for v in range(2):
+                    nc.sync.dma_start(
+                        out=reg[v].rearrange("m (z n) -> z m n", z=P), in_=x2[:, 16 * v + 4 * c : 16 * v + 4 * c + 4, :]
+                    )
+
+            def p_load(c):
+                reg = region(c).rearrange("(v m z) -> v m z", v=2, m=4)
+                for m in range(4):
+                    for v in range(2):
+                        p0 = (4 * c + m) * 8
+                        nc.sync.dma_start(
+                            out=x3[p0 : p0 + 8].rearrange("p (g t) n -> p g (t n)", t=4)[:, v:8:2, :],
+                            in_=reg[v, m].rearrange("(h p n) -> p h n", h=4, p=8),
+                        )
+
+            def r_stage(st, j):
+                free_stage(lambda i: x2[:, i, :], wr[:, st, :], 2**st, range(4 * j, 4 * j + 4), SHARE_A)
+
+            def r_last(c):
+                r_stage(4, c)
+                r_store(c)
+                if c > 0:
+                    p_load(c - 1)
+                if c == 3:
+                    p_load(3)
+
+            for st in range(3):
+                for j in range(4):
+                    r_stage(st, j)
+            weave(
+                ([lambda j=j: r_stage(3, j) for j in range(4)] + [lambda c=c: r_last(c) for c in range(4)], 0, 1),
+                ([lambda h=h, t0=t0: b_stage9(h, t0) for h in range(4) for t0 in (0, 2)], 0, 1),
+            )
+
+            def b_stage10(h2, g0):
+                free_stage(xb, wp_up[:, 3, :], 8, [8 * h2 + 4 * g0 + t for t in range(4)], SHARE_B)
+
+            def b_stage11(gg):
+                free_stage(xb, wp_up[:, 4, :], 16, [4 * gg + t for t in range(4)], SHARE_B)
+
+            for h2 in range(2):
+                for g0 in range(2):
+                    b_stage10(h2, g0)
+            for gg in range(4):
+                b_stage11(gg)
+
+        def a_stage10(h2, g0):
+            free_stage(lambda i: x3[:, i, :], wp_up[:, 3, :], 8, [8 * h2 + 4 * g0 + t for t in range(4)], SHARE_A)
+
+        def a_stage11(gg):
+            free_stage(lambda i: x3[:, i, :], wp_up[:, 4, :], 16, [4 * gg + t for t in range(4)], SHARE_A3, put=lambda i: x[:, i, 0:NA])
+
+        with ExitStack() as down:
+            psc = down.enter_context(tc.psum_pool(name="psc", bufs=4))
+
+            def c_gelu(g):
+                for t in range(4):
+                    blk = 4 * g + t
+                    nc.scalar.activation(out=xw(blk), in_=xw(blk), func=GELU, bias=ub[:, blk : blk + 1])
+
+            def c_stage0(g):
+                free_stage(xw, wp_dn[:, 0, :], 1, (2 * g, 2 * g + 1), SHARE_C0, wide=True)
+
+            def c_stage1(g):
+                free_stage(xw, wp_dn[:, 1, :], 2, (2 * g, 2 * g + 1), SHARE_C0, wide=True)
+
+            def c_stage9(h, t0):
+                units = []
+                for t in (t0, t0 + 1):
+                    pair = []
+                    for side_ in range(2):
+                        blk = 4 * (2 * h + side_) + t
+                        ps = psc.tile([P, 512], F32, name=uid("c"), tag="ca" if side_ == 0 else "cb")
+                        nc.tensor.matmul(out=ps[:], lhsT=mt[:, (32 + blk) * P : (33 + blk) * P], rhs=xw(blk), start=True, stop=True)
+                        pair.append(ps)
+                    i = 8 * h + t
+                    units.append((pair[0][:], pair[1][:], xw(i), xw(i + 4), wp_dn[:, 2, :], 4 * h + t, None))
+                group(units, 0, wide=True)
+
+            def c_stage10(h2, g0):
+                for t in (0, 2):
+                    free_stage(xw, wp_dn[:, 3, :], 8, [8 * h2 + 4 * g0 + t, 8 * h2 + 4 * g0 + t + 1], SHARE_C, wide=True)
+
+            a_stage10(0, 0)
+            a_stage10(1, 0)
+            a_stage10(0, 1)
+            a_stage11(0)
+            c_gelu(0)
+            a_stage10(1, 1)
+            c_gelu(4)
+            a_stage11(1)
+            c_stage0(0)
+            c_gelu(1)
+            a_stage11(2)
+            c_stage1(0)
+            c_stage0(1)
+            c_gelu(5)
+            c_stage0(4)
+            c_stage1(1)
+            c_gelu(2)
+            c_stage0(5)
+            c_stage1(4)
+            c_stage9(0, 0)
+            a_stage11(3)
+            c_gelu(3)
+            c_stage1(5)
+            c_stage9(0, 2)
+            c_stage0(2)
+            c_gelu(6)
+            c_stage9(2, 0)
+            c_stage0(3)
+            c_stage1(2)
+            c_stage9(2, 2)
+            c_gelu(7)
+            c_stage1(3)
+            c_stage0(6)
+            c_stage9(1, 0)
+            c_stage0(7)
+            c_stage1(6)
+            c_stage9(1, 2)
+            c_stage1(7)
+            c_stage10(0, 0)
+            c_stage9(3, 0)
+            c_stage10(0, 1)
+            c_stage9(3, 2)
+            c_stage10(1, 0)
+            c_stage10(1, 1)
+
+        psa = ctx.enter_context(tc.psum_pool(name="psa", bufs=1))
+        fin = big.tile([P, 12288], BF16, name="fin", tag="x1")
+        accs = {}
+        for i in range(4):
+            for d in range(2):
+                acc = psa.tile([P, 512], F32, name="acc%d_%d" % (i, d), tag="acc%d_%d" % (i, d))
+                accs[(i, d)] = acc
+        hc = const.tile([P, 2, 512], U32, name="hc", tag="xq", align_bytes=64)
+        hs = const.tile([P, 2, 512], U8, name="hs", tag="xs", align_bytes=64)
+
+        def hb(g):
+            at = 2048 * (2 * (g % 2) + g // 4)
+            return fin[:, at : at + 2048].rearrange("p (t n) -> p t n", t=4)
+
+        def hi(slot):
+            at = 8192 + 2048 * slot
+            return fin[:, at : at + 2048].rearrange("p (n t) -> p n t", t=4)
+
+        def last_stage(gg):
+            for t0 in (0, 2):
+                units = []
+                for t in (t0, t0 + 1):
+                    k = 4 * gg + t
+                    units.append((xw(k), xw(k + 16), hb(gg)[:, t, :], hb(gg + 4)[:, t, :], wp_dn[:, 4, :], k, None))
+                group(units, SHARE_C, wide=True)
+
+        def lay(g):
+            if g < 4:
+                nc.vector.tensor_copy(out=hi(g // 4), in_=hb(g).rearrange("p t n -> p n t"))
+            else:
+                nc.scalar.copy(out=hi(g // 4), in_=hb(g).rearrange("p t n -> p n t"))
+
+        def quantize_h(g):
+            slot = g // 4
+            nc.vector.quantize_mx(out=hc[:, slot].bitcast(FP8X4), scales=hs[:, slot], in_=hi(slot).rearrange("p n t -> p (n t)"))
+
+        def contract(g, first_pass, last_pass):
+            slot = g // 4
+            for i in range(4):
+                for d in range(2):
+                    nc.tensor.matmul_mx(
+                        out=accs[(i, d)][:],
+                        lhsT=hc[:, slot, i * P : (i + 1) * P].bitcast(FP8X4),
+                        lhsT_scale=hs[:, slot, i * P : (i + 1) * P],
+                        rhs=wc[:, g, 1024 * d : 1024 * (d + 1)].bitcast(FP4X4),
+                        rhs_scale=wc_s[:, g, 512 * d : 512 * (d + 1)],
+                        start=first_pass,
+                        stop=last_pass,
+                    )
+
+        for gg in range(6):
+            if gg < 4:
+                last_stage(gg)
+            if gg > 1:
+                for g in (gg - 2, gg + 2):
+                    quantize_h(g)
+                    contract(g, g == 0, g == 7)
+            if 0 < gg < 5:
+                for g in (gg - 1, gg + 3):
+                    lay(g)
+        for i in range(4):
+            for d in range(2):
+                o = tmp.tile([P, 512], F32, name=uid("o"), tag="taw" if d == 0 else "tbw", bufs=BUFS_WIDE)
+                nc.vector.tensor_tensor(out=o[:], in0=accs[(i, d)][:], in1=bias[:, 512 * d : 512 * (d + 1)], op=ADD)
+                nc.sync.dma_start(out=out_rows[i * P : (i + 1) * P, 512 * d : 512 * (d + 1)], in_=o[:])

@@ -24,16 +24,21 @@ HALF = 256
 NA = 208
 NB = 512 - NA
 REGION = NA * 1024
-BUFS_WIDE = 4
-BUFS_NARROW = 4
-SHARE_A = 0
-SHARE_B = 1
-SHARE_C = 0
-SHARE_C0 = 1
-SHARE_A3 = 1
-SHARE_4 = 4
-SIDE_FROM = 0.3
 FLOPS = 2 * 2 * 512 * D * H
+BUFS_T_WIDE = 5
+BUFS_T = 7
+BUFS_U = 1
+BUFS_U_WIDE = 1
+SIDE_FROM = 0.25
+A4_TO = 0.75
+R9_TO = 0.85
+GP_FACTORS = (0, 1, 2, 3)
+SPLIT = {"A0":0,"A":0,"A4":0,"A3":0,"B0":0,"B":0,"B9":0,"C0":0,"C1":0,"C9":0,"C10":0,"C11":0}
+ON_VECTOR = {"A0":0,"A":0,"A4":2,"A3":0,"B0":0,"B":0,"B9":0,"C0":1,"C1":1,"C9":0,"C10":0,"C11":0}
+
+
+def share(table, phase, turn):
+    return int(table[phase] * (turn + 1)) - int(table[phase] * turn)
 
 
 def weave(*lists):
@@ -64,42 +69,57 @@ def tile_butterflymlp_w4_kernel(
         const = ctx.enter_context(tc.tile_pool(name="const", bufs=1))
         big = ctx.enter_context(tc.tile_pool(name="big", bufs=1))
         tmp = ctx.enter_context(tc.tile_pool(name="tmp", bufs=1))
+        wide_pool = {}
 
-        def product(dst, src, w, c, on_vector):
-            if c is not None:
-                nc.scalar.activation(out=dst, in_=src, func=IDENT, scale=w, bias=c)
-            elif on_vector:
-                nc.vector.tensor_scalar(out=dst, in0=src, scalar1=w, scalar2=None, op0=MULT)
-            else:
-                nc.scalar.activation(out=dst, in_=src, func=COPY, scale=w)
-
-        def group(units, vector_share=0, wide=False):
-            parts = []
-            n = 0
-            width = 512 if wide else NB
+        def group(units, phase, turn):
+            n_split = share(SPLIT, phase, turn)
+            n_vector = share(ON_VECTOR, phase, turn)
+            wide = units[0][0].shape[-1] == 512
             size = units[0][0].shape[-1]
-            for a, b, na, nb, w, k, c in units:
-                ta_full = tmp.tile([P, width], F32, name=uid("ta"), tag="taw" if wide else "ta", bufs=BUFS_WIDE if wide else BUFS_NARROW)
-                tb_full = tmp.tile([P, width], F32, name=uid("tb"), tag="tbw" if wide else "tb", bufs=BUFS_WIDE if wide else BUFS_NARROW)
-                ta = ta_full[:, 0:size]
-                tb = tb_full[:, 0:size]
-                product(ta, a, w[:, 4 * k : 4 * k + 1], None if c is None else c[:, k, 0:1], n >= 2 * len(units) - vector_share)
-                product(tb, a, w[:, 4 * k + 2 : 4 * k + 3], None if c is None else c[:, k, 1:2], n + 1 >= 2 * len(units) - vector_share)
-                n += 2
-                parts.append((ta, tb))
-            for (a, b, na, nb, w, k, c), (ta, tb) in zip(units, parts):
-                nc.vector.scalar_tensor_tensor(out=na, in0=b, scalar=w[:, 4 * k + 1 : 4 * k + 2], in1=ta, op0=MULT, op1=ADD)
-            for (a, b, na, nb, w, k, c), (ta, tb) in zip(units, parts):
-                nc.vector.scalar_tensor_tensor(out=nb, in0=b, scalar=w[:, 4 * k + 3 : 4 * k + 4], in1=tb, op0=MULT, op1=ADD)
+            where = wide_pool["tmp"] if wide else tmp
+            parts = []
 
-        def free_stage(view, w, bit, pairs, vector_share=0, wide=False, put=None):
-            put = view if put is None else put
+            def product(dst, src, w, c, on_vector=False):
+                if on_vector:
+                    nc.vector.tensor_scalar(out=dst, in0=src, scalar1=w, scalar2=None, op0=MULT)
+                elif c is not None:
+                    nc.scalar.activation(out=dst, in_=src, func=IDENT, scale=w, bias=c)
+                else:
+                    nc.scalar.activation(out=dst, in_=src, func=COPY, scale=w)
+
+            def temp(tag, bufs):
+                full = where.tile([P, 2, 512 if wide else NB], F32, name=uid(tag), tag=tag, bufs=bufs)
+                return full[:, :, 0:size]
+
+            for n, (a, b, na, nb, both, w, k, c) in enumerate(units):
+                split = n >= len(units) - n_split
+                ta = temp("t", BUFS_T_WIDE if wide else BUFS_T)
+                for r in range(2):
+                    product(ta[:, r], a, w[:, 4 * k + 2 * r : 4 * k + 2 * r + 1], None if c is None else c[:, k, r : r + 1], 2 * n + r < n_vector)
+                tb = None
+                if split:
+                    tb = temp("u", BUFS_U_WIDE if wide else BUFS_U)
+                    for r in range(2):
+                        product(tb[:, r], b, w[:, 4 * k + 2 * r + 1 : 4 * k + 2 * r + 2], None)
+                parts.append((ta, tb))
+            for r in range(2):
+                for (a, b, na, nb, both, w, k, c), (ta, tb) in zip(units, parts):
+                    if tb is None:
+                        nc.vector.scalar_tensor_tensor(
+                            out=(na, nb)[r], in0=b, scalar=w[:, 4 * k + 2 * r + 1 : 4 * k + 2 * r + 2], in1=ta[:, r], op0=MULT, op1=ADD
+                        )
+            for (a, b, na, nb, both, w, k, c), (ta, tb) in zip(units, parts):
+                if tb is not None:
+                    nc.vector.tensor_tensor(out=both, in0=ta, in1=tb, op=ADD)
+
+        def free_stage(src, w, bit, pairs, phase, turn, dst=None):
+            dst = src if dst is None else dst
             units = []
             for k in pairs:
                 i = (k // bit) * 2 * bit + k % bit
                 j = i + bit
-                units.append((view(i), view(j), put(i), put(j), w, k, None))
-            group(units, vector_share, wide)
+                units.append((src[:, i, :], src[:, j, :], dst[:, i, :], dst[:, j, :], dst[:, i : j + 1 : bit, :], w, k, None))
+            group(units, phase, turn)
 
         ident = const.tile([P, P], F32, name="ident")
         make_identity(nc, ident[:])
@@ -125,13 +145,16 @@ def tile_butterflymlp_w4_kernel(
             codes = w[:, 0 : 2 * groups * n].rearrange("p (g n) -> p g n", g=groups)
             planes = w[:, 2 * groups * n :].rearrange("p (g n) -> p g n", g=groups)
             nc.gpsimd.memset(w[:, 2 * groups * n :].bitcast(I32), 0)
-            for q in range(4):
-                nc.sync.dma_start(
-                    out=planes[32 * q : 32 * q + 4, :, :].bitcast(I32),
-                    in_=scales[:, 4 * q : 4 * q + 4, :].rearrange("g q n -> q g n").bitcast(I32),
-                )
             cuts = 4 if groups == 2 else 1
             for c in range(cuts):
+                if c % 2 == 0:
+                    span = n // max(cuts // 2, 1)
+                    part = slice(c // 2 * span, (c // 2 + 1) * span)
+                    for j in range(4):
+                        nc.sync.dma_start(
+                            out=planes[j:P:32, :, part].bitcast(I32),
+                            in_=scales[:, :, part].rearrange("g (q j) n -> j q g n", j=4)[j].bitcast(I32),
+                        )
                 cols = slice(c * 2 * n // cuts, (c + 1) * 2 * n // cuts)
                 nc.sync.dma_start(out=codes[:, :, cols].bitcast(I32), in_=words[:, :, cols].rearrange("g p n -> p g n").bitcast(I32))
             return codes, planes
@@ -236,6 +259,8 @@ def tile_butterflymlp_w4_kernel(
                 pb = psf.tile([P, 2, HALF], F32, name=uid("fb"), tag="fb")
                 return pa, pb
 
+            rw_turned = early.tile([P, 512], BF16, name="rw_turned")
+
             def spread_weights():
                 def turns(src, n, step):
                     ps = psh.tile([P, 8, P], BF16, name=uid("wt"), tag="xt", bufs=2)
@@ -258,7 +283,10 @@ def tile_butterflymlp_w4_kernel(
                 ps = turns(pw, [(j, j) for j in range(4)], 4)
                 nc.vector.tensor_copy(out=bp[:].rearrange("p (g t) -> p g t", t=4), in_=ps[:, 0:4, 64:72].rearrange("p t g -> p g t"))
                 nc.vector.tensor_copy(out=ub[:].rearrange("p (g t) -> p g t", t=4), in_=ps[:, 0:4, 72:80].rearrange("p t g -> p g t"))
-                ps = turns(rw, [(j, j) for j in range(4)], 4)
+                nc.gpsimd.tensor_copy(
+                    out=rw_turned[:].rearrange("p (x h e) -> p x h e", x=8, h=4), in_=rw[:].rearrange("p (h x e) -> p x h e", x=8, h=4)
+                )
+                ps = turns(rw_turned, [(j, j) for j in range(4)], 4)
                 nc.vector.tensor_copy(out=wr[:].rearrange("p s (m c) -> p (s m) c", c=4), in_=ps[:, 0:4, 0:80].rearrange("p c s -> p s c"))
 
             def stage0_bias(w, b32, res):
@@ -304,7 +332,7 @@ def tile_butterflymlp_w4_kernel(
 
             factors = {}
 
-            def fetch_factors(b):
+            def fetch_factors(b, queue):
                 if b < 4:
                     h = 2 ** (6 - b)
                     rep = P // h
@@ -313,15 +341,15 @@ def tile_butterflymlp_w4_kernel(
                     src = scratch(b).rearrange("(h z) -> h z", h=h)
                     if b < 3:
                         for r in range(rep):
-                            nc.sync.dma_start(out=flat[r:P:rep, :], in_=src)
+                            queue.dma_start(out=flat[r:P:rep, :], in_=src)
                     else:
                         for top in range(h):
-                            nc.sync.dma_start(out=flat[top * rep : (top + 1) * rep, :], in_=src[top].partition_broadcast(rep))
+                            queue.dma_start(out=flat[top * rep : (top + 1) * rep, :], in_=src[top].partition_broadcast(rep))
                 else:
                     f = early.tile([P, 2 ** (6 - b) * 16, 16], F32, name="f%d" % b)
                     rows = 2**b
                     for r in range(P // rows):
-                        nc.sync.dma_start(
+                        queue.dma_start(
                             out=f[r * rows : (r + 1) * rows].rearrange("p (x g) e -> p x (g e)", g=16),
                             in_=scratch(b).rearrange("(x u z) -> u x z", u=rows, z=256),
                         )
@@ -376,16 +404,23 @@ def tile_butterflymlp_w4_kernel(
                 factors["rt"] = rt
 
             def high_d():
+                area = out_flat[2 * REGION : 2 * REGION + 65536]
                 ps = psh.tile([P, 4, P], F32, name="rows_ps", tag="xt", bufs=2)
                 flat = factors["rt"][:].rearrange("p x g t -> p (x g t)")
                 for x in range(4):
                     nc.tensor.transpose(ps[:, x, :], flat[:, x * P : (x + 1) * P], ident[:])
                 rows_sb = early.tile([P, 4, P], F32, name="rows_sb")
                 nc.vector.tensor_copy(out=rows_sb[:], in_=ps[:])
-                area = out_flat[131072 : 131072 + 65536]
                 nc.sync.dma_start(out=area.rearrange("(x p o) -> p x o", x=4, p=P), in_=rows_sb[:])
+                spread_rows(0)
+
+            def spread_rows(n):
+                area = out_flat[2 * REGION : 2 * REGION + 65536]
                 for q in range(8):
-                    nc.sync.dma_start(out=mt[16 * q : 16 * q + 16, :], in_=area[8192 * q : 8192 * (q + 1)].partition_broadcast(16))
+                    nc.sync.dma_start(
+                        out=mt[16 * q : 16 * q + 16, 4096 * n : 4096 * (n + 1)],
+                        in_=area[8192 * q + 4096 * n : 8192 * q + 4096 * (n + 1)].partition_broadcast(16),
+                    )
 
             def low_part(b):
                 f = factors[b]
@@ -432,8 +467,8 @@ def tile_butterflymlp_w4_kernel(
                     nc.scalar.copy(out=nat[0:112, :], in_=nat_raw[0:112, :])
             quantize_x(1)
             park_factors()
-            for b in (0, 1, 6, 5, 4, 2, 3):
-                fetch_factors(b)
+            for b in (4, 5, 6, 0, 1, 2, 3):
+                fetch_factors(b, nc.gpsimd if b in GP_FACTORS else nc.sync)
             def a_stage0(j):
                 pa, pb = banks()
                 for n in range(4):
@@ -442,26 +477,38 @@ def tile_butterflymlp_w4_kernel(
                         nc.tensor.transpose((pa, pb)[n % 2][:, n // 2, i * P : (i + 1) * P], ht[:, i, blk * P : (blk + 1) * P], ident[:])
                 group(
                     [
-                        (pa[:, n, 0:NA], pb[:, n, 0:NA], x1[:, 4 * j + 2 * n, :], x1[:, 4 * j + 2 * n + 1, :], wq[:, 0, :], 2 * j + n, cq)
+                        (
+                            pa[:, n, 0:NA],
+                            pb[:, n, 0:NA],
+                            x1[:, 4 * j + 2 * n, :],
+                            x1[:, 4 * j + 2 * n + 1, :],
+                            x1[:, 4 * j + 2 * n : 4 * j + 2 * n + 2, :],
+                            wq[:, 0, :],
+                            2 * j + n,
+                            cq,
+                        )
                         for n in range(2)
-                    ]
+                    ],
+                    "A0", j,
                 )
 
-            def a_stage(st, j, share=0):
-                free_stage(lambda i: x1[:, i, :], wq[:, st, :], 2**st, range(4 * j, 4 * j + 4), share)
+            def a_stage(st, j):
+                free_stage(x1, wq[:, st, :], 2**st, range(4 * j, 4 * j + 4), "A", j)
 
             for j in range(8):
                 a_stage0(j)
-            a_stage(1, 0, SHARE_A)
-            a_stage(1, 1, SHARE_A)
+            a_stage(1, 0)
+            a_stage(1, 1)
             spread_weights()
             stage0_bias(wp_up, bp[:].rearrange("p (k c) -> p k c", c=2), cp)
-            rest = [lambda st=st, j=j: a_stage(st, j, SHARE_A) for st in range(1, 4) for j in range(4)][2:]
-            side = [lambda: low_part(0), high_a, lambda: low_part(1), high_b, high_c, lambda: low_part(2), high_d, lambda: low_part(3)]
+            rest = [lambda st=st, j=j: a_stage(st, j) for st in range(1, 4) for j in range(4)][2:]
+            side = [high_a, high_b, high_c, high_d] + [lambda b=b: low_part(b) for b in range(4)]
             weave((rest, 0, 1), (side, SIDE_FROM, 1))
 
         xpool = ctx.enter_context(tc.tile_pool(name="xpool", bufs=1))
         x = xpool.tile([P, 32, 512], F32, name="x")
+
+        xb_all = x[:, :, NA:512]
 
         def xb(i):
             return x[:, i, NA:512]
@@ -498,11 +545,11 @@ def tile_butterflymlp_w4_kernel(
                             nc.tensor.transpose(ps[:, i * P : (i + 1) * P], hg[:, i, t, :], ident[:])
                         pair.append(ps[:, 384 - NB : 384])
                     i = 4 * g + 2 * n
-                    units.append((pair[0], pair[1], xb(i), xb(i + 1), wp_up[:, 0, :], 2 * g + n, cp))
-                group(units)
+                    units.append((pair[0], pair[1], xb(i), xb(i + 1), xb_all[:, i : i + 2, :], wp_up[:, 0, :], 2 * g + n, cp))
+                group(units, "B0", g)
 
             def b_stage1(j):
-                free_stage(xb, wp_up[:, 1, :], 2, range(4 * j, 4 * j + 4), SHARE_B)
+                free_stage(xb_all, wp_up[:, 1, :], 2, range(4 * j, 4 * j + 4), "B", j)
 
             def finish_dense(n, h):
                 view = mt[:, n * 4096 : (n + 1) * 4096].rearrange("p (k h l) -> p h k l", h=8, l=16)[:, h]
@@ -518,17 +565,14 @@ def tile_butterflymlp_w4_kernel(
                         nc.tensor.matmul(out=ps[:, 0:NB], lhsT=mt[:, blk * P : (blk + 1) * P], rhs=xb(blk), start=True, stop=True)
                         pair.append(ps[:, 0:NB])
                     i = 8 * h + t
-                    units.append((pair[0], pair[1], xb(i), xb(i + 4), wp_up[:, 2, :], 4 * h + t, None))
-                group(units)
+                    units.append((pair[0], pair[1], xb(i), xb(i + 4), xb_all[:, i : i + 5 : 4, :], wp_up[:, 2, :], 4 * h + t, None))
+                group(units, "B9", 2 * h + t0 // 2)
 
             def region(c):
                 return out_flat[(c % 2) * REGION : (c % 2 + 1) * REGION]
 
             def q_store(c):
-                for h in range(4):
-                    nc.sync.dma_start(
-                        out=region(c).rearrange("(h r m n) -> h m r n", h=4, r=8, m=32)[h], in_=x1[32 * h : 32 * h + 32, c:32:4, :]
-                    )
+                nc.sync.dma_start(out=region(c).rearrange("(x q n) -> q x n", x=8, q=P), in_=x1[:, c:32:4, :])
 
             def r_load(c):
                 nc.sync.dma_start(out=x2[c:P:4].rearrange("p m n -> p (m n)"), in_=region(c).rearrange("(z e) -> z e", z=32))
@@ -536,7 +580,7 @@ def tile_butterflymlp_w4_kernel(
             x2 = big.tile([P, 32, NA], F32, name="x2", tag="t32")
 
             def a_stage4(c, hf):
-                free_stage(lambda i: x1[:, i, :], wq[:, 4, :], 16, (c + 8 * hf, c + 4 + 8 * hf), SHARE_4)
+                free_stage(x1, wq[:, 4, :], 16, (c + 8 * hf, c + 4 + 8 * hf), "A4", 2 * c + hf)
                 if hf == 1:
                     q_store(c)
                     if c > 0:
@@ -550,16 +594,18 @@ def tile_butterflymlp_w4_kernel(
                 first_b.append(lambda g=g: b_stage0(g))
             weave(
                 (first_b, 0, 1),
-                ([lambda c=c, hf=hf: a_stage4(c, hf) for c in range(4) for hf in range(2)], 0, 1),
+                ([lambda c=c, hf=hf: a_stage4(c, hf) for c in range(4) for hf in range(2)], 0, A4_TO),
             )
             r_load(3)
 
         with ExitStack() as middle:
             psg = middle.enter_context(tc.psum_pool(name="psg", bufs=4))
+            spread_rows(1)
+            late = middle.enter_context(tc.tile_pool(name="late", bufs=1))
             wc, wc_s = load_w(w_con_words, w_con_scales, D, 8)
             bias_parts = []
             for n, vec in enumerate((b_con, down_bias)):
-                raw = tmp.tile([P, D], BF16, name="bias_raw%d" % n, tag="taw" if n == 0 else "tbw", bufs=BUFS_WIDE)
+                raw = late.tile([P, D], BF16, name="bias_raw%d" % n)
                 nc.sync.dma_start(out=raw[:], in_=vec.partition_broadcast(P))
                 bias_parts.append(raw)
             bias = const.tile([P, D], F32, name="bias")
@@ -567,8 +613,10 @@ def tile_butterflymlp_w4_kernel(
             x3 = big.tile([P, 32, NA], F32, name="x3", tag="x1")
             weave(
                 ([lambda j=j: b_stage1(j) for j in range(4)], 0, 1),
-                ([lambda h=h, n=n: finish_dense(n, h) for n in range(2) for h in range(8)], 0, 1),
+                ([lambda h=h: finish_dense(0, h) for h in range(8)], 0, 1),
             )
+            for t0 in (0, 2):
+                b_stage9(0, t0)
 
             def r_store(c):
                 reg = region(c).rearrange("(v m z) -> v m z", v=2, m=4)
@@ -579,16 +627,14 @@ def tile_butterflymlp_w4_kernel(
 
             def p_load(c):
                 reg = region(c).rearrange("(v m z) -> v m z", v=2, m=4)
-                for m in range(4):
-                    for v in range(2):
-                        p0 = (4 * c + m) * 8
-                        nc.sync.dma_start(
-                            out=x3[p0 : p0 + 8].rearrange("p (g t) n -> p g (t n)", t=4)[:, v:8:2, :],
-                            in_=reg[v, m].rearrange("(h p n) -> p h n", h=4, p=8),
-                        )
+                for v in range(2):
+                    nc.sync.dma_start(
+                        out=x3[32 * c : 32 * c + 32].rearrange("p (g t) n -> p g (t n)", t=4)[:, v:8:2, :],
+                        in_=reg[v].rearrange("m (x h n) -> (m x) h n", x=8, h=4),
+                    )
 
             def r_stage(st, j):
-                free_stage(lambda i: x2[:, i, :], wr[:, st, :], 2**st, range(4 * j, 4 * j + 4), SHARE_A)
+                free_stage(x2, wr[:, st, :], 2**st, range(4 * j, 4 * j + 4), "A", j)
 
             def r_last(c):
                 r_stage(4, c)
@@ -602,27 +648,33 @@ def tile_butterflymlp_w4_kernel(
                 for j in range(4):
                     r_stage(st, j)
             weave(
-                ([lambda j=j: r_stage(3, j) for j in range(4)] + [lambda c=c: r_last(c) for c in range(4)], 0, 1),
-                ([lambda h=h, t0=t0: b_stage9(h, t0) for h in range(4) for t0 in (0, 2)], 0, 1),
+                ([lambda j=j: r_stage(3, j) for j in range(4)] + [lambda c=c: r_last(c) for c in range(4)], 0, R9_TO),
+                ([lambda h=h, t0=t0: b_stage9(h, t0) for h in range(1, 4) for t0 in (0, 2)], 0.1, 1),
             )
 
             def b_stage10(h2, g0):
-                free_stage(xb, wp_up[:, 3, :], 8, [8 * h2 + 4 * g0 + t for t in range(4)], SHARE_B)
+                free_stage(xb_all, wp_up[:, 3, :], 8, [8 * h2 + 4 * g0 + t for t in range(4)], "B", 2 * h2 + g0)
 
             def b_stage11(gg):
-                free_stage(xb, wp_up[:, 4, :], 16, [4 * gg + t for t in range(4)], SHARE_B)
+                free_stage(xb_all, wp_up[:, 4, :], 16, [4 * gg + t for t in range(4)], "B", gg)
 
-            for h2 in range(2):
-                for g0 in range(2):
-                    b_stage10(h2, g0)
-            for gg in range(4):
-                b_stage11(gg)
+            weave(
+                (
+                    [lambda h2=h2, g0=g0: b_stage10(h2, g0) for h2 in range(2) for g0 in range(2)]
+                    + [lambda gg=gg: b_stage11(gg) for gg in range(4)],
+                    0,
+                    1,
+                ),
+                ([lambda h=h: finish_dense(1, h) for h in range(8)], 0, 1),
+            )
+
+        wide_pool["tmp"] = ctx.enter_context(tc.tile_pool(name="tmpw", bufs=1))
 
         def a_stage10(h2, g0):
-            free_stage(lambda i: x3[:, i, :], wp_up[:, 3, :], 8, [8 * h2 + 4 * g0 + t for t in range(4)], SHARE_A)
+            free_stage(x3, wp_up[:, 3, :], 8, [8 * h2 + 4 * g0 + t for t in range(4)], "A3", 2 * h2 + g0)
 
         def a_stage11(gg):
-            free_stage(lambda i: x3[:, i, :], wp_up[:, 4, :], 16, [4 * gg + t for t in range(4)], SHARE_A3, put=lambda i: x[:, i, 0:NA])
+            free_stage(x3, wp_up[:, 4, :], 16, [4 * gg + t for t in range(4)], "A3", gg, dst=x[:, :, 0:NA])
 
         with ExitStack() as down:
             psc = down.enter_context(tc.psum_pool(name="psc", bufs=4))
@@ -633,10 +685,10 @@ def tile_butterflymlp_w4_kernel(
                     nc.scalar.activation(out=xw(blk), in_=xw(blk), func=GELU, bias=ub[:, blk : blk + 1])
 
             def c_stage0(g):
-                free_stage(xw, wp_dn[:, 0, :], 1, (2 * g, 2 * g + 1), SHARE_C0, wide=True)
+                free_stage(x, wp_dn[:, 0, :], 1, (2 * g, 2 * g + 1), "C0", g)
 
             def c_stage1(g):
-                free_stage(xw, wp_dn[:, 1, :], 2, (2 * g, 2 * g + 1), SHARE_C0, wide=True)
+                free_stage(x, wp_dn[:, 1, :], 2, (2 * g, 2 * g + 1), "C1", g)
 
             def c_stage9(h, t0):
                 units = []
@@ -648,12 +700,12 @@ def tile_butterflymlp_w4_kernel(
                         nc.tensor.matmul(out=ps[:], lhsT=mt[:, (32 + blk) * P : (33 + blk) * P], rhs=xw(blk), start=True, stop=True)
                         pair.append(ps)
                     i = 8 * h + t
-                    units.append((pair[0][:], pair[1][:], xw(i), xw(i + 4), wp_dn[:, 2, :], 4 * h + t, None))
-                group(units, 0, wide=True)
+                    units.append((pair[0][:], pair[1][:], xw(i), xw(i + 4), x[:, i : i + 5 : 4, :], wp_dn[:, 2, :], 4 * h + t, None))
+                group(units, "C9", 2 * h + t0 // 2)
 
             def c_stage10(h2, g0):
                 for t in (0, 2):
-                    free_stage(xw, wp_dn[:, 3, :], 8, [8 * h2 + 4 * g0 + t, 8 * h2 + 4 * g0 + t + 1], SHARE_C, wide=True)
+                    free_stage(x, wp_dn[:, 3, :], 8, [8 * h2 + 4 * g0 + t, 8 * h2 + 4 * g0 + t + 1], "C10", 4 * h2 + 2 * g0 + t // 2)
 
             a_stage10(0, 0)
             a_stage10(1, 0)
@@ -714,6 +766,10 @@ def tile_butterflymlp_w4_kernel(
             at = 2048 * (2 * (g % 2) + g // 4)
             return fin[:, at : at + 2048].rearrange("p (t n) -> p t n", t=4)
 
+        def fin_pair(gg, t):
+            at = 4096 * (gg % 2)
+            return fin[:, at : at + 4096].rearrange("p (v t n) -> p v t n", v=2, t=4)[:, :, t, :]
+
         def hi(slot):
             at = 8192 + 2048 * slot
             return fin[:, at : at + 2048].rearrange("p (n t) -> p n t", t=4)
@@ -723,8 +779,8 @@ def tile_butterflymlp_w4_kernel(
                 units = []
                 for t in (t0, t0 + 1):
                     k = 4 * gg + t
-                    units.append((xw(k), xw(k + 16), hb(gg)[:, t, :], hb(gg + 4)[:, t, :], wp_dn[:, 4, :], k, None))
-                group(units, SHARE_C, wide=True)
+                    units.append((xw(k), xw(k + 16), hb(gg)[:, t, :], hb(gg + 4)[:, t, :], fin_pair(gg, t), wp_dn[:, 4, :], k, None))
+                group(units, "C11", 2 * gg + t0 // 2)
 
         def lay(g):
             if g < 4:
@@ -762,6 +818,6 @@ def tile_butterflymlp_w4_kernel(
                     lay(g)
         for i in range(4):
             for d in range(2):
-                o = tmp.tile([P, 512], F32, name=uid("o"), tag="taw" if d == 0 else "tbw", bufs=BUFS_WIDE)
+                o = wide_pool["tmp"].tile([P, 512], F32, name=uid("o"), tag="t", bufs=BUFS_T_WIDE)
                 nc.vector.tensor_tensor(out=o[:], in0=accs[(i, d)][:], in1=bias[:, 512 * d : 512 * (d + 1)], op=ADD)
                 nc.sync.dma_start(out=out_rows[i * P : (i + 1) * P, 512 * d : 512 * (d + 1)], in_=o[:])

@@ -29,12 +29,14 @@ BUFS_T_WIDE = 5
 BUFS_T = 7
 BUFS_U = 1
 BUFS_U_WIDE = 1
-SIDE_FROM = 0.25
-A4_TO = 0.75
+SIDE_FROM = 0.15
+A4_TO = 0.85
 R9_TO = 0.85
-GP_FACTORS = (0, 1, 2, 3)
+GP_FACTORS = (9,)
+FIN_TO = 0.5
+EVAC_MOD = 2
 SPLIT = {"A0":0,"A":0,"A4":0,"A3":0,"B0":0,"B":0,"B9":0,"C0":0,"C1":0,"C9":0,"C10":0,"C11":0}
-ON_VECTOR = {"A0":0,"A":0,"A4":2,"A3":0,"B0":0,"B":0,"B9":0,"C0":1,"C1":1,"C9":0,"C10":0,"C11":0}
+ON_VECTOR = {"A0":0,"A":0,"A4":1,"A3":2,"B0":0,"B":0,"B9":0,"C0":0.5,"C1":0,"C9":0,"C10":0,"C11":0}
 
 
 def share(table, phase, turn):
@@ -144,7 +146,7 @@ def tile_butterflymlp_w4_kernel(
             w = big.tile([P, 3 * groups * n], U8, name=uid("w"), tag="w", align_bytes=64)
             codes = w[:, 0 : 2 * groups * n].rearrange("p (g n) -> p g n", g=groups)
             planes = w[:, 2 * groups * n :].rearrange("p (g n) -> p g n", g=groups)
-            nc.gpsimd.memset(w[:, 2 * groups * n :].bitcast(I32), 0)
+            (nc.vector if groups == 2 else nc.gpsimd).memset(w[:, 2 * groups * n :].bitcast(I32), 0)
             cuts = 4 if groups == 2 else 1
             for c in range(cuts):
                 if c % 2 == 0:
@@ -162,7 +164,7 @@ def tile_butterflymlp_w4_kernel(
         with ExitStack() as front:
             early = front.enter_context(tc.tile_pool(name="early", bufs=1))
             psh = front.enter_context(tc.psum_pool(name="psh", bufs=1))
-            psf = front.enter_context(tc.psum_pool(name="psf", bufs=2))
+            psf = front.enter_context(tc.psum_pool(name="psf", bufs=3))
 
             scale_row = early.tile([P, D], F32, name="scale_row")
             x_bytes_tiles = {}
@@ -206,10 +208,15 @@ def tile_butterflymlp_w4_kernel(
 
             xg_tiles = {}
 
-            def prep_x(i):
+            xw_tiles = {}
+
+            def widen_x(i):
                 xw = early.tile([P, D], BF16, name="xw%d" % i, tag="xw", bufs=2)
                 nc.vector.tensor_tensor(out=xw[:], in0=x_bytes_tiles[i][:].bitcast(FP8), in1=scale_row[:], op=MULT)
-                words = xw[:].bitcast(F32)
+                xw_tiles[i] = xw
+
+            def turn_x(i):
+                words = xw_tiles[i][:].bitcast(F32)
                 xt = psh.tile([P, 2, 2, P], F32, name="xt%d" % i, tag="xt", bufs=2)
                 for g in range(2):
                     for u in range(2):
@@ -222,11 +229,12 @@ def tile_butterflymlp_w4_kernel(
                     dst = xg[:, g, (i % 2) * P : (i % 2 + 1) * P, :].rearrange("p n t -> p (n t)").bitcast(F32)
                     nc.vector.tensor_copy(out=dst.rearrange("p (n u) -> p n u", u=2), in_=xt[:, g].rearrange("p u n -> p n u"))
 
-            def quantize_x(half):
-                tok = slice(half * HALF, (half + 1) * HALF)
+            def quantize_x(i):
+                tok = slice(i * P, (i + 1) * P)
+                at = slice((i % 2) * P, (i % 2 + 1) * P)
                 for g in range(2):
                     nc.vector.quantize_mx(
-                        out=xq[:, g, tok].bitcast(FP8X4), scales=xs[:, g, tok], in_=xg_tiles[half][:, g].rearrange("p n t -> p (n t)")
+                        out=xq[:, g, tok].bitcast(FP8X4), scales=xs[:, g, tok], in_=xg_tiles[i // 2][:, g, at].rearrange("p n t -> p (n t)")
                     )
 
             def expand(ps, i, j):
@@ -245,7 +253,7 @@ def tile_butterflymlp_w4_kernel(
             ht = big.tile([P, 2, H], F32, name="ht", tag="t32")
 
             def a_expand(i, j, on_vector):
-                ps = psh.tile([P, 512], F32, name=uid("mx"), tag="mx", bufs=2)
+                ps = psf.tile([P, 512], F32, name=uid("mx"), tag="fa" if i == 0 else "fb")
                 expand(ps[:], i, j)
                 dst = ht[:, i].rearrange("p (r q) -> p r q", r=32)[:, :, 16 * j : 16 * (j + 1)]
                 src = ps[:].rearrange("p (q r) -> p r q", r=32)
@@ -283,7 +291,7 @@ def tile_butterflymlp_w4_kernel(
                 ps = turns(pw, [(j, j) for j in range(4)], 4)
                 nc.vector.tensor_copy(out=bp[:].rearrange("p (g t) -> p g t", t=4), in_=ps[:, 0:4, 64:72].rearrange("p t g -> p g t"))
                 nc.vector.tensor_copy(out=ub[:].rearrange("p (g t) -> p g t", t=4), in_=ps[:, 0:4, 72:80].rearrange("p t g -> p g t"))
-                nc.gpsimd.tensor_copy(
+                nc.vector.tensor_copy(
                     out=rw_turned[:].rearrange("p (x h e) -> p x h e", x=8, h=4), in_=rw[:].rearrange("p (h x e) -> p x h e", x=8, h=4)
                 )
                 ps = turns(rw_turned, [(j, j) for j in range(4)], 4)
@@ -378,11 +386,13 @@ def tile_butterflymlp_w4_kernel(
                         scale=bit_of[:, 4, r : r + 1],
                     )
                     parts.append(m)
+                factors["s4_parts"] = parts
+
+            def high_c():
+                parts = factors["s4_parts"]
                 s4 = early.tile([P, 256, 2], F32, name="s4")
                 nc.vector.tensor_tensor(out=s4[:], in0=parts[0][:], in1=parts[1][:], op=ADD)
                 factors["s4"] = s4
-
-            def high_c():
                 t5 = early.tile([P, 2, 2, 16, 4], F32, name="t5")
                 for x in range(2):
                     for y in range(2):
@@ -392,23 +402,30 @@ def tile_butterflymlp_w4_kernel(
                             in1=factors["s5"][:].rearrange("p (x g t) c -> p x c g t", x=2, t=4)[:, x, y],
                             op=MULT,
                         )
+                factors["t5"] = t5
+
+            def high_d():
                 rt = early.tile([P, 8, 16, 4], F32, name="rt")
                 for x in range(4):
                     for z in range(2):
                         nc.vector.tensor_tensor(
                             out=rt[:, 2 * x + z],
-                            in0=t5[:, x // 2, x % 2],
+                            in0=factors["t5"][:, x // 2, x % 2],
                             in1=factors["s4"][:].rearrange("p (x g t) c -> p x c g t", x=4, t=4)[:, x, z],
                             op=MULT,
                         )
                 factors["rt"] = rt
 
-            def high_d():
-                area = out_flat[2 * REGION : 2 * REGION + 65536]
+            def high_e():
                 ps = psh.tile([P, 4, P], F32, name="rows_ps", tag="xt", bufs=2)
                 flat = factors["rt"][:].rearrange("p x g t -> p (x g t)")
                 for x in range(4):
                     nc.tensor.transpose(ps[:, x, :], flat[:, x * P : (x + 1) * P], ident[:])
+                factors["ps"] = ps
+
+            def high_f():
+                area = out_flat[2 * REGION : 2 * REGION + 65536]
+                ps = factors["ps"]
                 rows_sb = early.tile([P, 4, P], F32, name="rows_sb")
                 nc.vector.tensor_copy(out=rows_sb[:], in_=ps[:])
                 nc.sync.dma_start(out=area.rearrange("(x p o) -> p x o", x=4, p=P), in_=rows_sb[:])
@@ -422,7 +439,7 @@ def tile_butterflymlp_w4_kernel(
                         in_=area[8192 * q + 4096 * n : 8192 * q + 4096 * (n + 1)].partition_broadcast(16),
                     )
 
-            def low_part(b):
+            def low_a(b):
                 f = factors[b]
                 k = 2**b
                 pair = []
@@ -432,6 +449,11 @@ def tile_butterflymlp_w4_kernel(
                         out=m[:], in_=f[:].rearrange("p g (o x c) -> p c g x o", x=8, c=2)[:, c], func=COPY, scale=bit_of[:, b, c : c + 1]
                     )
                     pair.append(m)
+                factors[("pair", b)] = pair
+
+            def low_b(b):
+                k = 2**b
+                pair = factors[("pair", b)]
                 if b == 3:
                     sel = low
                 else:
@@ -442,6 +464,10 @@ def tile_butterflymlp_w4_kernel(
                     in1=pair[1][:].rearrange("p g x o -> p (g x o)"),
                     op=ADD,
                 )
+                factors[("low", b)] = sel
+
+            def low_c(b):
+                sel = factors[("low", b)]
                 if b > 0:
                     for r in range(2):
                         nc.vector.tensor_tensor(
@@ -450,22 +476,23 @@ def tile_butterflymlp_w4_kernel(
                             in1=factors[("low", b - 1)][:].rearrange("p k r o -> p k (r o)"),
                             op=MULT,
                         )
-                factors[("low", b)] = sel
 
-            bit_columns()
             q_weights()
-            prep_x(0)
-            prep_x(1)
+            widen_x(0)
+            widen_x(1)
+            turn_x(0)
+            turn_x(1)
             quantize_x(0)
+            quantize_x(1)
             for j in range(8):
                 for i in range(2):
                     a_expand(i, j, i == 1)
-                if j == 4:
-                    prep_x(2)
                 if j == 5:
-                    prep_x(3)
+                    widen_x(2)
                     nc.scalar.copy(out=nat[0:112, :], in_=nat_raw[0:112, :])
-            quantize_x(1)
+                if j == 6:
+                    widen_x(3)
+            bit_columns()
             park_factors()
             for b in (4, 5, 6, 0, 1, 2, 3):
                 fetch_factors(b, nc.gpsimd if b in GP_FACTORS else nc.sync)
@@ -497,12 +524,18 @@ def tile_butterflymlp_w4_kernel(
 
             for j in range(8):
                 a_stage0(j)
+                if j in (1, 3):
+                    turn_x(2 + j // 2)
+            quantize_x(2)
+            quantize_x(3)
             a_stage(1, 0)
             a_stage(1, 1)
             spread_weights()
             stage0_bias(wp_up, bp[:].rearrange("p (k c) -> p k c", c=2), cp)
-            rest = [lambda st=st, j=j: a_stage(st, j) for st in range(1, 4) for j in range(4)][2:]
-            side = [high_a, high_b, high_c, high_d] + [lambda b=b: low_part(b) for b in range(4)]
+            rest = [lambda st=st, j=j: a_stage(st, j) for st in range(1, 4) for j in range(4)][2:9]
+            side = [high_b, high_a, high_c, high_d, high_e, high_f]
+            side += [lambda: low_a(0), lambda: low_b(0), lambda: low_a(1), lambda: low_b(1), lambda: low_a(2), lambda: low_c(1)]
+            side += [lambda: low_b(2), lambda: low_a(3), lambda: low_c(2), lambda: low_b(3), lambda: low_c(3)]
             weave((rest, 0, 1), (side, SIDE_FROM, 1))
 
         xpool = ctx.enter_context(tc.tile_pool(name="xpool", bufs=1))
@@ -528,7 +561,7 @@ def tile_butterflymlp_w4_kernel(
                     ps = ps0.tile([P, 512], F32, name=uid("mx"), tag="mx", bufs=4)
                     expand(ps[:], i + 1, g)
                     src = ps[:].rearrange("p (q t) -> p t q", t=4)
-                    if i == 0 and g % 2 == 0:
+                    if i == 0 and g % EVAC_MOD == 0:
                         nc.vector.tensor_copy(out=hg[:, i], in_=src)
                     else:
                         nc.scalar.copy(out=hg[:, i], in_=src)
@@ -586,6 +619,8 @@ def tile_butterflymlp_w4_kernel(
                     if c > 0:
                         r_load(c - 1)
 
+            a_stage(3, 1)
+            a_stage(3, 2)
             b_expand(0)
             first_b = []
             for g in range(8):
@@ -594,7 +629,11 @@ def tile_butterflymlp_w4_kernel(
                 first_b.append(lambda g=g: b_stage0(g))
             weave(
                 (first_b, 0, 1),
-                ([lambda c=c, hf=hf: a_stage4(c, hf) for c in range(4) for hf in range(2)], 0, A4_TO),
+                (
+                    [lambda: a_stage(3, 3)] + [lambda c=c, hf=hf: a_stage4(c, hf) for c in range(4) for hf in range(2)],
+                    0,
+                    A4_TO,
+                ),
             )
             r_load(3)
 
@@ -613,7 +652,7 @@ def tile_butterflymlp_w4_kernel(
             x3 = big.tile([P, 32, NA], F32, name="x3", tag="x1")
             weave(
                 ([lambda j=j: b_stage1(j) for j in range(4)], 0, 1),
-                ([lambda h=h: finish_dense(0, h) for h in range(8)], 0, 1),
+                ([lambda h=h: finish_dense(0, h) for h in range(8)], 0, FIN_TO),
             )
             for t0 in (0, 2):
                 b_stage9(0, t0)
@@ -658,10 +697,17 @@ def tile_butterflymlp_w4_kernel(
             def b_stage11(gg):
                 free_stage(xb_all, wp_up[:, 4, :], 16, [4 * gg + t for t in range(4)], "B", gg)
 
+            def gelu(gg, first, last):
+                for g in (gg, gg + 4):
+                    for blk in range(4 * g, 4 * g + 4):
+                        part = x[:, blk, first:last]
+                        nc.scalar.activation(out=part, in_=part, func=GELU, bias=ub[:, blk : blk + 1])
+
             weave(
                 (
                     [lambda h2=h2, g0=g0: b_stage10(h2, g0) for h2 in range(2) for g0 in range(2)]
-                    + [lambda gg=gg: b_stage11(gg) for gg in range(4)],
+                    + [lambda: b_stage11(0), lambda: b_stage11(1), lambda: gelu(0, NA, 512), lambda: b_stage11(2)]
+                    + [lambda: gelu(1, NA, 512), lambda: b_stage11(3), lambda: gelu(2, NA, 512)],
                     0,
                     1,
                 ),
@@ -680,9 +726,9 @@ def tile_butterflymlp_w4_kernel(
             psc = down.enter_context(tc.psum_pool(name="psc", bufs=4))
 
             def c_gelu(g):
-                for t in range(4):
-                    blk = 4 * g + t
-                    nc.scalar.activation(out=xw(blk), in_=xw(blk), func=GELU, bias=ub[:, blk : blk + 1])
+                for blk in range(4 * g, 4 * g + 4):
+                    part = x[:, blk, 0:NA]
+                    nc.scalar.activation(out=part, in_=part, func=GELU, bias=ub[:, blk : blk + 1])
 
             def c_stage0(g):
                 free_stage(x, wp_dn[:, 0, :], 1, (2 * g, 2 * g + 1), "C0", g)
@@ -709,10 +755,11 @@ def tile_butterflymlp_w4_kernel(
 
             a_stage10(0, 0)
             a_stage10(1, 0)
+            gelu(3, NA, 512)
             a_stage10(0, 1)
             a_stage11(0)
-            c_gelu(0)
             a_stage10(1, 1)
+            c_gelu(0)
             c_gelu(4)
             a_stage11(1)
             c_stage0(0)
@@ -774,27 +821,29 @@ def tile_butterflymlp_w4_kernel(
             at = 8192 + 2048 * slot
             return fin[:, at : at + 2048].rearrange("p (n t) -> p n t", t=4)
 
-        def last_stage(gg):
-            for t0 in (0, 2):
-                units = []
-                for t in (t0, t0 + 1):
-                    k = 4 * gg + t
-                    units.append((xw(k), xw(k + 16), hb(gg)[:, t, :], hb(gg + 4)[:, t, :], fin_pair(gg, t), wp_dn[:, 4, :], k, None))
-                group(units, "C11", 2 * gg + t0 // 2)
+        def last_stage(gg, t0):
+            units = []
+            for t in (t0, t0 + 1):
+                k = 4 * gg + t
+                units.append((xw(k), xw(k + 16), hb(gg)[:, t, :], hb(gg + 4)[:, t, :], fin_pair(gg, t), wp_dn[:, 4, :], k, None))
+            group(units, "C11", 2 * gg + t0 // 2)
 
-        def lay(g):
+        def lay(g, tok):
+            src = hb(g)[:, :, tok].rearrange("p t n -> p n t")
             if g < 4:
-                nc.vector.tensor_copy(out=hi(g // 4), in_=hb(g).rearrange("p t n -> p n t"))
+                nc.vector.tensor_copy(out=hi(g // 4)[:, tok, :], in_=src)
             else:
-                nc.scalar.copy(out=hi(g // 4), in_=hb(g).rearrange("p t n -> p n t"))
+                nc.scalar.copy(out=hi(g // 4)[:, tok, :], in_=src)
 
-        def quantize_h(g):
+        def quantize_h(g, tok):
             slot = g // 4
-            nc.vector.quantize_mx(out=hc[:, slot].bitcast(FP8X4), scales=hs[:, slot], in_=hi(slot).rearrange("p n t -> p (n t)"))
+            nc.vector.quantize_mx(
+                out=hc[:, slot, tok].bitcast(FP8X4), scales=hs[:, slot, tok], in_=hi(slot)[:, tok, :].rearrange("p n t -> p (n t)")
+            )
 
-        def contract(g, first_pass, last_pass):
+        def contract(g, tiles, first_pass, last_pass):
             slot = g // 4
-            for i in range(4):
+            for i in tiles:
                 for d in range(2):
                     nc.tensor.matmul_mx(
                         out=accs[(i, d)][:],
@@ -806,18 +855,36 @@ def tile_butterflymlp_w4_kernel(
                         stop=last_pass,
                     )
 
-        for gg in range(6):
-            if gg < 4:
-                last_stage(gg)
-            if gg > 1:
-                for g in (gg - 2, gg + 2):
-                    quantize_h(g)
-                    contract(g, g == 0, g == 7)
-            if 0 < gg < 5:
+        def finish(tiles):
+            for i in tiles:
+                for d in range(2):
+                    o = wide_pool["tmp"].tile([P, 512], F32, name=uid("o"), tag="t", bufs=BUFS_T_WIDE)
+                    nc.vector.tensor_tensor(out=o[:], in0=accs[(i, d)][:], in1=bias[:, 512 * d : 512 * (d + 1)], op=ADD)
+                    nc.sync.dma_start(out=out_rows[i * P : (i + 1) * P, 512 * d : 512 * (d + 1)], in_=o[:])
+
+        whole = slice(0, 512)
+        for gg in range(4):
+            last_stage(gg, 0)
+            if gg > 0:
                 for g in (gg - 1, gg + 3):
-                    lay(g)
-        for i in range(4):
-            for d in range(2):
-                o = wide_pool["tmp"].tile([P, 512], F32, name=uid("o"), tag="t", bufs=BUFS_T_WIDE)
-                nc.vector.tensor_tensor(out=o[:], in0=accs[(i, d)][:], in1=bias[:, 512 * d : 512 * (d + 1)], op=ADD)
-                nc.sync.dma_start(out=out_rows[i * P : (i + 1) * P, 512 * d : 512 * (d + 1)], in_=o[:])
+                    lay(g, whole)
+            last_stage(gg, 2)
+            if gg > 0:
+                for g in (gg - 1, gg + 3):
+                    quantize_h(g, whole)
+                    contract(g, range(4), g == 0, False)
+        halves = [slice(0, 256), slice(256, 512)]
+        for g in (3, 7):
+            lay(g, halves[0])
+        for g in (3, 7):
+            quantize_h(g, halves[0])
+        for g in (3, 7):
+            lay(g, halves[1])
+        contract(3, (0, 1), False, False)
+        contract(7, (0, 1), False, True)
+        for g in (3, 7):
+            quantize_h(g, halves[1])
+        contract(3, (2, 3), False, False)
+        contract(7, (2, 3), False, True)
+        finish((0, 1))
+        finish((2, 3))

@@ -14,52 +14,42 @@ FP4X4 = mybir.dt.float4_e2m1fn_x4
 ADD = mybir.AluOpType.add
 MULT = mybir.AluOpType.mult
 COPY = mybir.ActivationFunctionType.Copy
-IDENT = mybir.ActivationFunctionType.Identity
+IDENTITY = mybir.ActivationFunctionType.Identity
 GELU = mybir.ActivationFunctionType.Gelu
 
 P = 128
 D = 1024
 H = 4096
-HALF = 256
-NA = 208
-NB = 512 - NA
-REGION = NA * 1024
-FLOPS = 2 * 2 * 512 * D * H
-BUFS_T_WIDE = 5
-BUFS_T = 7
-BUFS_U = 1
-BUFS_U_WIDE = 1
-SIDE_FROM = 0.15
-A4_TO = 0.85
-R9_TO = 0.85
-GP_FACTORS = (9,)
-FIN_TO = 0.5
-EVAC_MOD = 2
-SPLIT = {"A0":0,"A":0,"A4":0,"A3":0,"B0":0,"B":0,"B9":0,"C0":0,"C1":0,"C9":0,"C10":0,"C11":0}
-ON_VECTOR = {"A0":0,"A":0,"A4":1,"A3":2,"B0":0,"B":0,"B9":0,"C0":0.5,"C1":0,"C9":0,"C10":0,"C11":0}
+TOKENS = 512
+BLOCKS = 32
+BANK = 512
+N_PAIRS = 208
+N_DENSE = TOKENS - N_PAIRS
+QUARTER = N_PAIRS * H // 4
+FACTOR = 16 * D
+TEMPS = 7
+TEMPS_ALL = 5
 
-
-def share(table, phase, turn):
-    return int(table[phase] * (turn + 1)) - int(table[phase] * turn)
+FLOPS = 2 * 2 * TOKENS * D * H
 
 
 def weave(*lists):
     keyed = []
-    for n, (steps, lo, hi) in enumerate(lists):
+    for n, (steps, first, last) in enumerate(lists):
         for i, step in enumerate(steps):
-            keyed.append((lo + (hi - lo) * (i + 0.5) / len(steps), n, i, step))
-    keyed = sorted(keyed, key=lambda e: e[:3])
-    for e in keyed:
-        e[3]()
+            keyed.append((first + (last - first) * (i + 0.5) / len(steps), n, i, step))
+    for entry in sorted(keyed, key=lambda e: e[:3]):
+        entry[3]()
 
 
 def tile_butterflymlp_w4_kernel(
     tc, x_bytes, x_scale, w_exp_words, w_exp_scales, b_exp, up_w, up_bias, down_w, w_con_words, w_con_scales, b_con, down_bias, out
 ):
     nc = tc.nc
-    out_flat = out.rearrange("b s d -> (b s d)")
+    hbm = out.rearrange("b s d -> (b s d)")
     out_rows = out.rearrange("b s d -> (b s) d")
     x_rows = x_bytes.rearrange("b s k -> (b s) k")
+    row_area = hbm[2 * QUARTER : 2 * QUARTER + 65536]
     serial = {"n": 0}
 
     def uid(prefix):
@@ -70,58 +60,46 @@ def tile_butterflymlp_w4_kernel(
         ctx.enter_context(tc.manual_schedule())
         const = ctx.enter_context(tc.tile_pool(name="const", bufs=1))
         big = ctx.enter_context(tc.tile_pool(name="big", bufs=1))
-        tmp = ctx.enter_context(tc.tile_pool(name="tmp", bufs=1))
-        wide_pool = {}
+        temps = ctx.enter_context(tc.tile_pool(name="temps", bufs=1))
+        temps_all = {}
 
-        def group(units, phase, turn):
-            n_split = share(SPLIT, phase, turn)
-            n_vector = share(ON_VECTOR, phase, turn)
-            wide = units[0][0].shape[-1] == 512
+        def copy(on_vector, dst, src):
+            if on_vector:
+                nc.vector.tensor_copy(out=dst, in_=src)
+            else:
+                nc.scalar.copy(out=dst, in_=src)
+
+        def group(units, n_vector=0):
             size = units[0][0].shape[-1]
-            where = wide_pool["tmp"] if wide else tmp
-            parts = []
-
-            def product(dst, src, w, c, on_vector=False):
-                if on_vector:
-                    nc.vector.tensor_scalar(out=dst, in0=src, scalar1=w, scalar2=None, op0=MULT)
-                elif c is not None:
-                    nc.scalar.activation(out=dst, in_=src, func=IDENT, scale=w, bias=c)
+            products = []
+            for n, (a, b, new_a, new_b, w, k, c) in enumerate(units):
+                if size == TOKENS:
+                    full = temps_all["pool"].tile([P, 2, TOKENS], F32, name=uid("t"), tag="t", bufs=TEMPS_ALL)
                 else:
-                    nc.scalar.activation(out=dst, in_=src, func=COPY, scale=w)
-
-            def temp(tag, bufs):
-                full = where.tile([P, 2, 512 if wide else NB], F32, name=uid(tag), tag=tag, bufs=bufs)
-                return full[:, :, 0:size]
-
-            for n, (a, b, na, nb, both, w, k, c) in enumerate(units):
-                split = n >= len(units) - n_split
-                ta = temp("t", BUFS_T_WIDE if wide else BUFS_T)
+                    full = temps.tile([P, 2, N_DENSE], F32, name=uid("t"), tag="t", bufs=TEMPS)
+                t = full[:, :, 0:size]
                 for r in range(2):
-                    product(ta[:, r], a, w[:, 4 * k + 2 * r : 4 * k + 2 * r + 1], None if c is None else c[:, k, r : r + 1], 2 * n + r < n_vector)
-                tb = None
-                if split:
-                    tb = temp("u", BUFS_U_WIDE if wide else BUFS_U)
-                    for r in range(2):
-                        product(tb[:, r], b, w[:, 4 * k + 2 * r + 1 : 4 * k + 2 * r + 2], None)
-                parts.append((ta, tb))
+                    w_a = w[:, 4 * k + 2 * r : 4 * k + 2 * r + 1]
+                    if 2 * n + r < n_vector:
+                        nc.vector.tensor_scalar(out=t[:, r], in0=a, scalar1=w_a, scalar2=None, op0=MULT)
+                    elif c is not None:
+                        nc.scalar.activation(out=t[:, r], in_=a, func=IDENTITY, scale=w_a, bias=c[:, k, r : r + 1])
+                    else:
+                        nc.scalar.activation(out=t[:, r], in_=a, func=COPY, scale=w_a)
+                products.append(t)
             for r in range(2):
-                for (a, b, na, nb, both, w, k, c), (ta, tb) in zip(units, parts):
-                    if tb is None:
-                        nc.vector.scalar_tensor_tensor(
-                            out=(na, nb)[r], in0=b, scalar=w[:, 4 * k + 2 * r + 1 : 4 * k + 2 * r + 2], in1=ta[:, r], op0=MULT, op1=ADD
-                        )
-            for (a, b, na, nb, both, w, k, c), (ta, tb) in zip(units, parts):
-                if tb is not None:
-                    nc.vector.tensor_tensor(out=both, in0=ta, in1=tb, op=ADD)
+                for (a, b, new_a, new_b, w, k, c), t in zip(units, products):
+                    w_b = w[:, 4 * k + 2 * r + 1 : 4 * k + 2 * r + 2]
+                    nc.vector.scalar_tensor_tensor(out=(new_a, new_b)[r], in0=b, scalar=w_b, in1=t[:, r], op0=MULT, op1=ADD)
 
-        def free_stage(src, w, bit, pairs, phase, turn, dst=None):
+        def block_stage(src, w, bit, pairs, n_vector=0, dst=None):
             dst = src if dst is None else dst
             units = []
             for k in pairs:
                 i = (k // bit) * 2 * bit + k % bit
                 j = i + bit
-                units.append((src[:, i, :], src[:, j, :], dst[:, i, :], dst[:, j, :], dst[:, i : j + 1 : bit, :], w, k, None))
-            group(units, phase, turn)
+                units.append((src[:, i, :], src[:, j, :], dst[:, i, :], dst[:, j, :], w, k, None))
+            group(units, n_vector)
 
         ident = const.tile([P, P], F32, name="ident")
         make_identity(nc, ident[:])
@@ -130,354 +108,358 @@ def tile_butterflymlp_w4_kernel(
         wq = const.tile([P, 5, 64], F32, name="wq")
         wr = const.tile([P, 5, 64], F32, name="wr")
         wp_up = const.tile([P, 5, 64], F32, name="wp_up")
-        wp_dn = const.tile([P, 5, 64], F32, name="wp_dn")
-        cq = const.tile([P, 16, 2], F32, name="cq")
-        cp = const.tile([P, 16, 2], F32, name="cp")
-        bp = const.tile([P, 32], F32, name="bp")
-        ub = const.tile([P, 32], F32, name="ub")
-        bit_of = const.tile([P, 5, 2], F32, name="bit_of")
-        mt = const.tile([P, 64 * P], F32, name="mt")
-        low = const.tile([P, 64, 2, 8], F32, name="low")
-        xq = const.tile([P, 2, 512], U32, name="xq", align_bytes=64)
-        xs = const.tile([P, 2, 512], U8, name="xs", align_bytes=64)
-        x1 = big.tile([P, 32, NA], F32, name="x1", tag="x1")
+        wp_down = const.tile([P, 5, 64], F32, name="wp_down")
+        bias_q = const.tile([P, 16, 2], F32, name="bias_q")
+        bias_p = const.tile([P, 16, 2], F32, name="bias_p")
+        b_exp_p = const.tile([P, BLOCKS], F32, name="b_exp_p")
+        up_bias_p = const.tile([P, BLOCKS], F32, name="up_bias_p")
+        bit4 = const.tile([P, 2], F32, name="bit4")
+        dense = const.tile([P, 2 * BLOCKS * P], F32, name="dense")
+        low = const.tile([P, 2 * BLOCKS, 2, 8], F32, name="low")
+        x_codes = const.tile([P, 2, TOKENS], U32, name="x_codes", tag="codes", align_bytes=64)
+        x_planes = const.tile([P, 2, TOKENS], U8, name="x_planes", tag="planes", align_bytes=64)
+        q_data = big.tile([P, BLOCKS, N_PAIRS], F32, name="q_data", tag="pairs")
 
-        def load_w(words, scales, n, groups):
-            w = big.tile([P, 3 * groups * n], U8, name=uid("w"), tag="w", align_bytes=64)
-            codes = w[:, 0 : 2 * groups * n].rearrange("p (g n) -> p g n", g=groups)
-            planes = w[:, 2 * groups * n :].rearrange("p (g n) -> p g n", g=groups)
-            (nc.vector if groups == 2 else nc.gpsimd).memset(w[:, 2 * groups * n :].bitcast(I32), 0)
-            cuts = 4 if groups == 2 else 1
-            for c in range(cuts):
-                if c % 2 == 0:
-                    span = n // max(cuts // 2, 1)
-                    part = slice(c // 2 * span, (c // 2 + 1) * span)
+        def load_weight(words, scales, passes, n, cuts, zeroing):
+            w = big.tile([P, 3 * passes * n], U8, name=uid("w"), tag="w", align_bytes=64)
+            codes = w[:, 0 : 2 * passes * n].rearrange("p (g n) -> p g n", g=passes)
+            planes = w[:, 2 * passes * n :].rearrange("p (g n) -> p g n", g=passes)
+            zeroing.memset(w[:, 2 * passes * n :].bitcast(I32), 0)
+            plane_cuts = (cuts + 1) // 2
+            for cut in range(cuts):
+                if cut % 2 == 0:
+                    cols = slice(cut // 2 * n // plane_cuts, (cut // 2 + 1) * n // plane_cuts)
                     for j in range(4):
                         nc.sync.dma_start(
-                            out=planes[j:P:32, :, part].bitcast(I32),
-                            in_=scales[:, :, part].rearrange("g (q j) n -> j q g n", j=4)[j].bitcast(I32),
+                            out=planes[j:P:32, :, cols].bitcast(I32),
+                            in_=scales[:, :, cols].rearrange("g (q j) n -> j q g n", j=4)[j].bitcast(I32),
                         )
-                cols = slice(c * 2 * n // cuts, (c + 1) * 2 * n // cuts)
+                cols = slice(cut * 2 * n // cuts, (cut + 1) * 2 * n // cuts)
                 nc.sync.dma_start(out=codes[:, :, cols].bitcast(I32), in_=words[:, :, cols].rearrange("g p n -> p g n").bitcast(I32))
             return codes, planes
 
         with ExitStack() as front:
             early = front.enter_context(tc.tile_pool(name="early", bufs=1))
-            psh = front.enter_context(tc.psum_pool(name="psh", bufs=1))
-            psf = front.enter_context(tc.psum_pool(name="psf", bufs=3))
+            ps_turn = front.enter_context(tc.psum_pool(name="ps_turn", bufs=2))
+            ps_front = front.enter_context(tc.psum_pool(name="ps_front", bufs=3))
 
             scale_row = early.tile([P, D], F32, name="scale_row")
-            x_bytes_tiles = {}
+            p_rows = early.tile([P, 2048], BF16, name="p_rows")
+            nc.gpsimd.memset(p_rows[:].bitcast(I32), 0)
+            r_rows = early.tile([P, 512], BF16, name="r_rows")
+            nc.gpsimd.memset(r_rows[:].bitcast(I32), 0)
+            wq_raw = early.tile([P, 5, 64], BF16, name="wq_raw")
+            b_exp_q_raw = early.tile([P, BLOCKS], BF16, name="b_exp_q_raw")
+            factor_raw = early.tile([P, D], BF16, name="factor_raw")
+            x_byte_tiles = {}
 
             def load_x(i):
-                xb = early.tile([P, D], U8, name="xb%d" % i, tag="xb", bufs=4)
-                nc.sync.dma_start(out=xb[:], in_=x_rows[i * P : (i + 1) * P, :])
-                x_bytes_tiles[i] = xb
-
-            pw = early.tile([P, 2048], BF16, name="pw")
-            nc.gpsimd.memset(pw[:].bitcast(I32), 0)
-            rw = early.tile([P, 512], BF16, name="rw")
-            nc.gpsimd.memset(rw[:].bitcast(I32), 0)
-            wq_raw = early.tile([P, 5, 64], BF16, name="wq_raw")
-            bq_raw = early.tile([P, 32], BF16, name="bq_raw")
-            nat_raw = early.tile([P, 1024], BF16, name="nat_raw")
-            nat = early.tile([P, 1024], F32, name="nat")
+                byte_tile = early.tile([P, D], U8, name="x_bytes_%d" % i, tag="x_bytes", bufs=4)
+                nc.sync.dma_start(out=byte_tile[:], in_=x_rows[i * P : (i + 1) * P, :])
+                x_byte_tiles[i] = byte_tile
 
             load_x(0)
             load_x(1)
             nc.sync.dma_start(out=scale_row[:], in_=x_scale.rearrange("a b k -> (a b k)").partition_broadcast(P))
-            we, we_s = load_w(w_exp_words, w_exp_scales, H, 2)
+            exp_codes, exp_planes = load_weight(w_exp_words, w_exp_scales, 2, H, 4, nc.vector)
+            for b in range(7):
+                for n, w in enumerate((up_w, down_w)):
+                    row = 16 * b + 8 * n
+                    nc.sync.dma_start(out=factor_raw[row : row + 8, :], in_=w[2 + b].rearrange("(g k) r c -> g (k r c)", g=8))
             load_x(2)
             load_x(3)
-            for st in range(7):
-                for n, w in enumerate((up_w, down_w)):
-                    at = 16 * st + 8 * n
-                    nc.sync.dma_start(out=nat_raw[at : at + 8, :], in_=w[2 + st].rearrange("(g k) r c -> g (k r c)", g=8))
             nc.sync.dma_start(out=wq_raw[:], in_=up_w[0:5].rearrange("s (q k) r c -> q s (k r c)", q=P))
-            nc.sync.dma_start(out=bq_raw[:], in_=b_exp.rearrange("(q r) -> q r", q=P))
+            nc.sync.dma_start(out=b_exp_q_raw[:], in_=b_exp.rearrange("(q r) -> q r", q=P))
             for n, w in enumerate((up_w, down_w)):
-                nc.sync.dma_start(out=pw[16 * n : 16 * n + 16, 0:1024], in_=w[0:2].rearrange("s (g k) r c -> (s g) (k r c)", g=8))
-                nc.sync.dma_start(out=pw[32 + 12 * n : 44 + 12 * n, :], in_=w[9:12].rearrange("s (h k) r c -> (s h) (k r c)", h=4))
-            nc.sync.dma_start(out=pw[64:72, 0:512], in_=b_exp.rearrange("(g e) -> g e", g=8))
-            nc.sync.dma_start(out=pw[72:80, 0:512], in_=up_bias.rearrange("(g e) -> g e", g=8))
-            for st in range(5):
+                nc.sync.dma_start(out=p_rows[16 * n : 16 * n + 16, 0:1024], in_=w[0:2].rearrange("s (g k) r c -> (s g) (k r c)", g=8))
+                nc.sync.dma_start(out=p_rows[32 + 12 * n : 44 + 12 * n, :], in_=w[9:12].rearrange("s (h k) r c -> (s h) (k r c)", h=4))
+            nc.sync.dma_start(out=p_rows[64:72, 0:512], in_=b_exp.rearrange("(g e) -> g e", g=8))
+            nc.sync.dma_start(out=p_rows[72:80, 0:512], in_=up_bias.rearrange("(g e) -> g e", g=8))
+            for s in range(5):
                 nc.sync.dma_start(
-                    out=rw[16 * st : 16 * st + 16, :].rearrange("p (h e) -> p h e", h=4),
-                    in_=up_w[5 + st].rearrange("(h m p) r c -> m h (p r c)", h=4, m=16),
+                    out=r_rows[16 * s : 16 * s + 16, :].rearrange("p (h e) -> p h e", h=4),
+                    in_=up_w[5 + s].rearrange("(h m r) a c -> m h (r a c)", h=4, m=16),
                 )
 
-            xg_tiles = {}
-
-            xw_tiles = {}
+            x_rounded = {}
+            x_grouped = {}
 
             def widen_x(i):
-                xw = early.tile([P, D], BF16, name="xw%d" % i, tag="xw", bufs=2)
-                nc.vector.tensor_tensor(out=xw[:], in0=x_bytes_tiles[i][:].bitcast(FP8), in1=scale_row[:], op=MULT)
-                xw_tiles[i] = xw
+                rounded = early.tile([P, D], BF16, name="x_rounded_%d" % i, tag="x_rounded", bufs=2)
+                nc.vector.tensor_tensor(out=rounded[:], in0=x_byte_tiles[i][:].bitcast(FP8), in1=scale_row[:], op=MULT)
+                x_rounded[i] = rounded
 
             def turn_x(i):
-                words = xw_tiles[i][:].bitcast(F32)
-                xt = psh.tile([P, 2, 2, P], F32, name="xt%d" % i, tag="xt", bufs=2)
+                words = x_rounded[i][:].bitcast(F32)
+                bank = ps_turn.tile([P, 2, 2, P], F32, name="x_bank_%d" % i, tag="turn")
                 for g in range(2):
                     for u in range(2):
-                        nc.tensor.transpose(xt[:, g, u, :], words[:, 256 * g + u : 256 * (g + 1) : 2], ident[:])
-                if i % 2 == 0:
-                    xg_new = early.tile([P, 2, HALF, 4], BF16, name="xg%d" % i, tag="xg", bufs=1, align_bytes=64)
-                    xg_tiles[i // 2] = xg_new
-                xg = xg_tiles[i // 2]
+                        nc.tensor.transpose(bank[:, g, u, :], words[:, 256 * g + u : 256 * (g + 1) : 2], ident[:])
+                grouped = early.tile([P, 2, P, 4], BF16, name="x_grouped_%d" % i, tag="x_grouped", bufs=2, align_bytes=64)
                 for g in range(2):
-                    dst = xg[:, g, (i % 2) * P : (i % 2 + 1) * P, :].rearrange("p n t -> p (n t)").bitcast(F32)
-                    nc.vector.tensor_copy(out=dst.rearrange("p (n u) -> p n u", u=2), in_=xt[:, g].rearrange("p u n -> p n u"))
+                    dst = grouped[:, g].rearrange("p n t -> p (n t)").bitcast(F32)
+                    copy(i < 2, dst.rearrange("p (n u) -> p n u", u=2), bank[:, g].rearrange("p u n -> p n u"))
+                x_grouped[i] = grouped
 
             def quantize_x(i):
-                tok = slice(i * P, (i + 1) * P)
-                at = slice((i % 2) * P, (i % 2 + 1) * P)
+                tokens = slice(i * P, (i + 1) * P)
                 for g in range(2):
                     nc.vector.quantize_mx(
-                        out=xq[:, g, tok].bitcast(FP8X4), scales=xs[:, g, tok], in_=xg_tiles[i // 2][:, g, at].rearrange("p n t -> p (n t)")
+                        out=x_codes[:, g, tokens].bitcast(FP8X4),
+                        scales=x_planes[:, g, tokens],
+                        in_=x_grouped[i][:, g].rearrange("p n t -> p (n t)"),
                     )
 
-            def expand(ps, i, j):
-                tok = slice(i * P, (i + 1) * P)
+            def expand(bank, i, j):
+                tokens = slice(i * P, (i + 1) * P)
                 for g in range(2):
                     nc.tensor.matmul_mx(
-                        out=ps,
-                        lhsT=xq[:, g, tok].bitcast(FP8X4),
-                        lhsT_scale=xs[:, g, tok],
-                        rhs=we[:, g, 1024 * j : 1024 * (j + 1)].bitcast(FP4X4),
-                        rhs_scale=we_s[:, g, 512 * j : 512 * (j + 1)],
+                        out=bank,
+                        lhsT=x_codes[:, g, tokens].bitcast(FP8X4),
+                        lhsT_scale=x_planes[:, g, tokens],
+                        rhs=exp_codes[:, g, 1024 * j : 1024 * (j + 1)].bitcast(FP4X4),
+                        rhs_scale=exp_planes[:, g, 512 * j : 512 * (j + 1)],
                         start=(g == 0),
                         stop=(g == 1),
                     )
 
-            ht = big.tile([P, 2, H], F32, name="ht", tag="t32")
+            expanded = big.tile([P, 2, H], F32, name="expanded", tag="wide")
 
-            def a_expand(i, j, on_vector):
-                ps = psf.tile([P, 512], F32, name=uid("mx"), tag="fa" if i == 0 else "fb")
-                expand(ps[:], i, j)
-                dst = ht[:, i].rearrange("p (r q) -> p r q", r=32)[:, :, 16 * j : 16 * (j + 1)]
-                src = ps[:].rearrange("p (q r) -> p r q", r=32)
-                if on_vector:
-                    nc.vector.tensor_copy(out=dst, in_=src)
-                else:
-                    nc.scalar.copy(out=dst, in_=src)
-
-            def banks():
-                pa = psf.tile([P, 2, HALF], F32, name=uid("fa"), tag="fa")
-                pb = psf.tile([P, 2, HALF], F32, name=uid("fb"), tag="fb")
-                return pa, pb
-
-            rw_turned = early.tile([P, 512], BF16, name="rw_turned")
-
-            def spread_weights():
-                def turns(src, n, step):
-                    ps = psh.tile([P, 8, P], BF16, name=uid("wt"), tag="xt", bufs=2)
-                    for j, at in n:
-                        nc.tensor.transpose(ps[:, j, :], src[:, at : P * step : step], ident_b[:])
-                    return ps
-
-                ps = turns(pw, [(j, j) for j in range(8)], 8)
-                for n, wp in enumerate((wp_up, wp_dn)):
-                    nc.vector.tensor_copy(
-                        out=wp[:, 0:2, :].rearrange("p s (g j) -> p (s g) j", j=8), in_=ps[:, :, 16 * n : 16 * n + 16].rearrange("p j s -> p s j")
-                    )
-                for hf in range(2):
-                    ps = turns(pw, [(j, 8 * hf + j) for j in range(8)], 16)
-                    for n, wp in enumerate((wp_up, wp_dn)):
-                        nc.vector.tensor_copy(
-                            out=wp[:, 2:5, :].rearrange("p s (h j) -> p (s h) j", j=16)[:, :, 8 * hf : 8 * hf + 8],
-                            in_=ps[:, :, 32 + 12 * n : 44 + 12 * n].rearrange("p j s -> p s j"),
-                        )
-                ps = turns(pw, [(j, j) for j in range(4)], 4)
-                nc.vector.tensor_copy(out=bp[:].rearrange("p (g t) -> p g t", t=4), in_=ps[:, 0:4, 64:72].rearrange("p t g -> p g t"))
-                nc.vector.tensor_copy(out=ub[:].rearrange("p (g t) -> p g t", t=4), in_=ps[:, 0:4, 72:80].rearrange("p t g -> p g t"))
-                nc.vector.tensor_copy(
-                    out=rw_turned[:].rearrange("p (x h e) -> p x h e", x=8, h=4), in_=rw[:].rearrange("p (h x e) -> p x h e", x=8, h=4)
+            def expand_pairs(i, j):
+                bank = ps_front.tile([P, BANK], F32, name=uid("mx"), tag="even" if i == 0 else "odd")
+                expand(bank[:], i, j)
+                copy(
+                    i == 1,
+                    expanded[:, i].rearrange("p (r q) -> p r q", r=BLOCKS)[:, :, 16 * j : 16 * (j + 1)],
+                    bank[:].rearrange("p (q r) -> p r q", r=BLOCKS),
                 )
-                ps = turns(rw_turned, [(j, j) for j in range(4)], 4)
-                nc.vector.tensor_copy(out=wr[:].rearrange("p s (m c) -> p (s m) c", c=4), in_=ps[:, 0:4, 0:80].rearrange("p c s -> p s c"))
 
-            def stage0_bias(w, b32, res):
-                prod = early.tile([P, 2, 16, 2], F32, name=uid("prod"), tag="prod", bufs=2)
-                w4 = w[:, 0, :].rearrange("p (k r c) -> p r k c", r=2, c=2)
-                for r in range(2):
-                    nc.gpsimd.tensor_tensor(out=prod[:, r], in0=w4[:, r], in1=b32, op=MULT)
-                    nc.gpsimd.tensor_tensor(out=res[:, :, r], in0=prod[:, r, :, 0], in1=prod[:, r, :, 1], op=ADD)
+            r_rows_turned = early.tile([P, 512], BF16, name="r_rows_turned")
+            spread_banks = {}
 
-            def q_weights():
-                bq = early.tile([P, 16, 2], F32, name="bq")
-                nc.gpsimd.tensor_copy(out=wq[:], in_=wq_raw[:])
-                nc.gpsimd.tensor_copy(out=bq[:].rearrange("p k c -> p (k c)"), in_=bq_raw[:])
-                stage0_bias(wq, bq[:], cq)
+            def turn_r_rows():
+                nc.gpsimd.tensor_copy(
+                    out=r_rows_turned[:].rearrange("p (x h e) -> p x h e", x=8, h=4),
+                    in_=r_rows[:].rearrange("p (h x e) -> p x h e", x=8, h=4),
+                )
 
-            def bit_columns():
-                for b in range(5):
-                    nc.vector.tensor_reduce(
-                        out=bit_of[:, b, 1:2],
-                        in_=ident[:].rearrange("p (h b l) -> p b h l", b=2, l=2**b)[:, 1],
-                        axis=mybir.AxisListType.XY,
-                        op=ADD,
+            def spread_turns(step):
+                rows, count, first, stride = (
+                    (p_rows, 8, 0, 8),
+                    (p_rows, 8, 0, 16),
+                    (p_rows, 8, 8, 16),
+                    (p_rows, 4, 0, 4),
+                    (r_rows_turned, 4, 0, 4),
+                )[step]
+                bank = ps_turn.tile([P, 8, P], BF16, name=uid("spread"), tag="turn")
+                for j in range(count):
+                    nc.tensor.transpose(bank[:, j, :], rows[:, first + j : P * stride : stride], ident_b[:])
+                spread_banks[step] = bank
+
+            def spread_copies(step):
+                bank = spread_banks[step]
+                if step == 0:
+                    for n, wp in enumerate((wp_up, wp_down)):
+                        nc.scalar.copy(
+                            out=wp[:, 0:2, :].rearrange("p s (g j) -> p (s g) j", j=8),
+                            in_=bank[:, :, 16 * n : 16 * n + 16].rearrange("p j s -> p s j"),
+                        )
+                elif step < 3:
+                    at = 8 * (step - 1)
+                    for n, wp in enumerate((wp_up, wp_down)):
+                        nc.scalar.copy(
+                            out=wp[:, 2:5, :].rearrange("p s (h j) -> p (s h) j", j=16)[:, :, at : at + 8],
+                            in_=bank[:, :, 32 + 12 * n : 44 + 12 * n].rearrange("p j s -> p s j"),
+                        )
+                elif step == 3:
+                    for row, vec in ((64, b_exp_p), (72, up_bias_p)):
+                        nc.scalar.copy(
+                            out=vec[:].rearrange("p (g t) -> p g t", t=4), in_=bank[:, 0:4, row : row + 8].rearrange("p t g -> p g t")
+                        )
+                    first_stage_bias(wp_up, b_exp_p[:].rearrange("p (k c) -> p k c", c=2), bias_p)
+                else:
+                    nc.scalar.copy(
+                        out=wr[:].rearrange("p s (m j) -> p (s m) j", j=4), in_=bank[:, 0:4, 0:80].rearrange("p j s -> p s j")
                     )
-                nc.vector.tensor_scalar(out=bit_of[:, :, 0], in0=bit_of[:, :, 1], scalar1=-1.0, scalar2=1.0, op0=MULT, op1=ADD)
 
-            def scratch(b):
-                return out_flat[b * 16384 : (b + 1) * 16384]
+            def spread(step):
+                if step < 5:
+                    spread_turns(step)
+                if step > 0:
+                    spread_copies(step - 1)
+
+            def first_stage_bias(w, b_pairs, bias):
+                prod = early.tile([P, 2, 16, 2], F32, name=uid("prod"), tag="prod", bufs=2)
+                w_pairs = w[:, 0, :].rearrange("p (k r c) -> p r k c", r=2, c=2)
+                for r in range(2):
+                    nc.gpsimd.tensor_tensor(out=prod[:, r], in0=w_pairs[:, r], in1=b_pairs, op=MULT)
+                    nc.gpsimd.tensor_tensor(out=bias[:, :, r], in0=prod[:, r, :, 0], in1=prod[:, r, :, 1], op=ADD)
+
+            def widen_q_weights():
+                b_exp_q = early.tile([P, 16, 2], F32, name="b_exp_q")
+                nc.gpsimd.tensor_copy(out=wq[:], in_=wq_raw[:])
+                nc.gpsimd.tensor_copy(out=b_exp_q[:].rearrange("p k c -> p (k c)"), in_=b_exp_q_raw[:])
+                first_stage_bias(wq, b_exp_q[:], bias_q)
+
+            def factor_area(b):
+                return hbm[b * FACTOR : (b + 1) * FACTOR]
+
+            factor_all = early.tile([P, D], F32, name="factor_all")
+            factor_by_input = early.tile([P, 2, D // 2], F32, name="factor_by_input")
+            factors = {}
+
+            def widen_factors():
+                nc.scalar.copy(out=factor_all[0:112, :], in_=factor_raw[0:112, :])
+                nc.scalar.copy(out=factor_by_input[0:112], in_=factor_raw[0:112, :].rearrange("p (e c) -> p c e", c=2))
 
             def park_factors():
-                for b in range(7):
-                    rows = nat[16 * b : 16 * b + 16, :]
+                for b in (4, 5, 6, 3, 2, 1, 0):
                     if b < 4:
-                        nc.sync.dma_start(
-                            out=scratch(b).rearrange("(h g e) -> g h e", g=16, h=2 ** (6 - b)),
-                            in_=rows.rearrange("g (h e) -> g h e", h=2 ** (6 - b)),
-                        )
+                        for c in range(2):
+                            nc.sync.dma_start(
+                                out=factor_area(b).rearrange("(h c g e) -> c g h e", c=2, g=16, h=2 ** (6 - b))[c],
+                                in_=factor_by_input[16 * b : 16 * b + 16, c].rearrange("g (h e) -> g h e", h=2 ** (6 - b)),
+                            )
                     else:
                         for x in range(2 ** (6 - b)):
                             nc.sync.dma_start(
-                                out=scratch(b).rearrange("(x u g e) -> x g u e", u=2**b, g=16, e=16)[x],
-                                in_=rows.rearrange("g (x u e) -> x g u e", u=2**b, e=16)[x],
+                                out=factor_area(b).rearrange("(x u g e) -> x g u e", u=2**b, g=16, e=16)[x],
+                                in_=factor_all[16 * b : 16 * b + 16, :].rearrange("g (x u e) -> x g u e", u=2**b, e=16)[x],
                             )
 
-            factors = {}
-
-            def fetch_factors(b, queue):
+            def fetch_factors(b):
                 if b < 4:
-                    h = 2 ** (6 - b)
-                    rep = P // h
-                    f = early.tile([P, 16, 16 * 2**b], F32, name="f%d" % b)
-                    flat = f[:].rearrange("p g e -> p (g e)")
-                    src = scratch(b).rearrange("(h z) -> h z", h=h)
-                    if b < 3:
-                        for r in range(rep):
-                            queue.dma_start(out=flat[r:P:rep, :], in_=src)
-                    else:
-                        for top in range(h):
-                            queue.dma_start(out=flat[top * rep : (top + 1) * rep, :], in_=src[top].partition_broadcast(rep))
+                    f = early.tile([P, 16, 8 * 2**b], F32, name="factor_%d" % b)
+                    for r in range(2**b):
+                        nc.sync.dma_start(
+                            out=f[:].rearrange("p g e -> p (g e)")[r : P : 2**b, :],
+                            in_=factor_area(b).rearrange("(j z) -> j z", j=2 ** (7 - b)),
+                        )
                 else:
-                    f = early.tile([P, 2 ** (6 - b) * 16, 16], F32, name="f%d" % b)
                     rows = 2**b
+                    f = early.tile([P, 16 * 2 ** (6 - b), 16], F32, name="factor_%d" % b)
                     for r in range(P // rows):
-                        queue.dma_start(
+                        nc.sync.dma_start(
                             out=f[r * rows : (r + 1) * rows].rearrange("p (x g) e -> p x (g e)", g=16),
-                            in_=scratch(b).rearrange("(x u z) -> u x z", u=rows, z=256),
+                            in_=factor_area(b).rearrange("(x u z) -> u x z", u=rows, z=256),
                         )
                 factors[b] = f
 
-            def high_a():
-                s6 = early.tile([P, 64, 2], F32, name="s6")
-                for hf in range(2):
-                    rows = slice(64 * hf, 64 * hf + 64)
-                    nc.vector.tensor_copy(out=s6[rows], in_=factors[6][rows].rearrange("p g (t r c) -> p r (g t) c", r=2, c=2)[:, hf])
-                s5 = early.tile([P, 128, 2], F32, name="s5")
-                for q in range(4):
-                    rows = slice(32 * q, 32 * q + 32)
-                    nc.vector.tensor_copy(out=s5[rows], in_=factors[5][rows].rearrange("p g (t r c) -> p r (g t) c", r=2, c=2)[:, q % 2])
-                factors["s6"] = s6
-                factors["s5"] = s5
+            def bit4_columns():
+                nc.vector.tensor_reduce(
+                    out=bit4[:, 1:2],
+                    in_=ident[:].rearrange("p (h v l) -> p v h l", v=2, l=16)[:, 1],
+                    axis=mybir.AxisListType.XY,
+                    op=ADD,
+                )
+                nc.vector.tensor_scalar(out=bit4[:, 0:1], in0=bit4[:, 1:2], scalar1=-1.0, scalar2=1.0, op0=MULT, op1=ADD)
 
-            def high_b():
-                parts = []
+            def high_masks():
                 for r in range(2):
-                    m = early.tile([P, 256, 2], F32, name="s4_%d" % r, tag="msel%d" % r)
+                    m = early.tile([P, 256, 2], F32, name="masked_%d" % r)
                     nc.scalar.activation(
                         out=m[:],
                         in_=factors[4][:].rearrange("p g (t r c) -> p r (g t) c", r=2, c=2)[:, r],
                         func=COPY,
-                        scale=bit_of[:, 4, r : r + 1],
+                        scale=bit4[:, r : r + 1],
                     )
-                    parts.append(m)
-                factors["s4_parts"] = parts
+                    factors[("masked", r)] = m
 
-            def high_c():
-                parts = factors["s4_parts"]
-                s4 = early.tile([P, 256, 2], F32, name="s4")
-                nc.vector.tensor_tensor(out=s4[:], in0=parts[0][:], in1=parts[1][:], op=ADD)
-                factors["s4"] = s4
-                t5 = early.tile([P, 2, 2, 16, 4], F32, name="t5")
-                for x in range(2):
-                    for y in range(2):
+            def high_rows():
+                row6 = early.tile([P, 64, 2], F32, name="row6")
+                for half in range(2):
+                    rows = slice(64 * half, 64 * half + 64)
+                    nc.scalar.copy(out=row6[rows], in_=factors[6][rows].rearrange("p g (t r c) -> p r (g t) c", r=2, c=2)[:, half])
+                row5 = early.tile([P, 128, 2], F32, name="row5")
+                for q in range(4):
+                    rows = slice(32 * q, 32 * q + 32)
+                    nc.scalar.copy(out=row5[rows], in_=factors[5][rows].rearrange("p g (t r c) -> p r (g t) c", r=2, c=2)[:, q % 2])
+                factors["row6"] = row6
+                factors["row5"] = row5
+
+            def high_products():
+                row4 = early.tile([P, 256, 2], F32, name="row4")
+                nc.vector.tensor_tensor(out=row4[:], in0=factors[("masked", 0)][:], in1=factors[("masked", 1)][:], op=ADD)
+                bits56 = early.tile([P, 2, 2, 16, 4], F32, name="bits56")
+                for i6 in range(2):
+                    for i5 in range(2):
                         nc.vector.tensor_tensor(
-                            out=t5[:, x, y],
-                            in0=factors["s6"][:].rearrange("p (g t) c -> p c g t", t=4)[:, x],
-                            in1=factors["s5"][:].rearrange("p (x g t) c -> p x c g t", x=2, t=4)[:, x, y],
+                            out=bits56[:, i6, i5],
+                            in0=factors["row6"][:].rearrange("p (g t) c -> p c g t", t=4)[:, i6],
+                            in1=factors["row5"][:].rearrange("p (x g t) c -> p x c g t", x=2, t=4)[:, i6, i5],
                             op=MULT,
                         )
-                factors["t5"] = t5
+                factors["row4"] = row4
+                factors["bits56"] = bits56
 
-            def high_d():
-                rt = early.tile([P, 8, 16, 4], F32, name="rt")
+            def high_last_products():
+                high = early.tile([P, 8, 16, 4], F32, name="high")
                 for x in range(4):
-                    for z in range(2):
+                    for i4 in range(2):
                         nc.vector.tensor_tensor(
-                            out=rt[:, 2 * x + z],
-                            in0=factors["t5"][:, x // 2, x % 2],
-                            in1=factors["s4"][:].rearrange("p (x g t) c -> p x c g t", x=4, t=4)[:, x, z],
+                            out=high[:, 2 * x + i4],
+                            in0=factors["bits56"][:, x // 2, x % 2],
+                            in1=factors["row4"][:].rearrange("p (x g t) c -> p x c g t", x=4, t=4)[:, x, i4],
                             op=MULT,
                         )
-                factors["rt"] = rt
+                factors["high"] = high
 
-            def high_e():
-                ps = psh.tile([P, 4, P], F32, name="rows_ps", tag="xt", bufs=2)
-                flat = factors["rt"][:].rearrange("p x g t -> p (x g t)")
+            def high_turns():
+                bank = ps_turn.tile([P, 4, P], F32, name="high_bank", tag="turn")
+                columns = factors["high"][:].rearrange("p x g t -> p (x g t)")
                 for x in range(4):
-                    nc.tensor.transpose(ps[:, x, :], flat[:, x * P : (x + 1) * P], ident[:])
-                factors["ps"] = ps
+                    nc.tensor.transpose(bank[:, x, :], columns[:, x * P : (x + 1) * P], ident[:])
+                factors["bank"] = bank
 
-            def high_f():
-                area = out_flat[2 * REGION : 2 * REGION + 65536]
-                ps = factors["ps"]
-                rows_sb = early.tile([P, 4, P], F32, name="rows_sb")
-                nc.vector.tensor_copy(out=rows_sb[:], in_=ps[:])
-                nc.sync.dma_start(out=area.rearrange("(x p o) -> p x o", x=4, p=P), in_=rows_sb[:])
+            def high_store():
+                rows = early.tile([P, 4, P], F32, name="high_rows_out")
+                nc.scalar.copy(out=rows[:], in_=factors["bank"][:])
+                nc.sync.dma_start(out=row_area.rearrange("(x p o) -> p x o", x=4, p=P), in_=rows[:])
                 spread_rows(0)
 
             def spread_rows(n):
-                area = out_flat[2 * REGION : 2 * REGION + 65536]
-                for q in range(8):
+                for top in range(8):
+                    at = 8192 * top + 4096 * n
                     nc.sync.dma_start(
-                        out=mt[16 * q : 16 * q + 16, 4096 * n : 4096 * (n + 1)],
-                        in_=area[8192 * q + 4096 * n : 8192 * q + 4096 * (n + 1)].partition_broadcast(16),
+                        out=dense[16 * top : 16 * top + 16, 4096 * n : 4096 * (n + 1)],
+                        in_=row_area[at : at + 4096].partition_broadcast(16),
                     )
 
-            def low_a(b):
-                f = factors[b]
-                k = 2**b
-                pair = []
-                for c in range(2):
-                    m = early.tile([P, 16, 8, k], F32, name="m%d_%d" % (b, c), tag="msel%d" % c)
-                    nc.scalar.activation(
-                        out=m[:], in_=f[:].rearrange("p g (o x c) -> p c g x o", x=8, c=2)[:, c], func=COPY, scale=bit_of[:, b, c : c + 1]
-                    )
-                    pair.append(m)
-                factors[("pair", b)] = pair
-
-            def low_b(b):
-                k = 2**b
-                pair = factors[("pair", b)]
-                if b == 3:
-                    sel = low
+            def low_products(b):
+                if b == 1:
+                    before = factors[0][:].rearrange("p g (t r) -> p (g t) r", r=2)
                 else:
-                    sel = early.tile([P, 64, 2, k], F32, name="l%d" % b)
-                nc.vector.tensor_tensor(
-                    out=sel[:].rearrange("p k r o -> p (k r o)"),
-                    in0=pair[0][:].rearrange("p g x o -> p (g x o)"),
-                    in1=pair[1][:].rearrange("p g x o -> p (g x o)"),
-                    op=ADD,
-                )
-                factors[("low", b)] = sel
+                    before = factors[("low", b - 1)][:].rearrange("p k r o -> p k (r o)")
+                products = low if b == 3 else early.tile([P, 2 * BLOCKS, 2, 2**b], F32, name="low_%d" % b)
+                for r in range(2):
+                    nc.vector.tensor_tensor(
+                        out=products[:].rearrange("p (g t) r o -> p r g t o", t=4)[:, r],
+                        in0=factors[b][:].rearrange("p g (o t r) -> p r g t o", t=4, r=2)[:, r],
+                        in1=before.rearrange("p (g t) o -> p g t o", t=4),
+                        op=MULT,
+                    )
+                factors[("low", b)] = products
 
-            def low_c(b):
-                sel = factors[("low", b)]
-                if b > 0:
-                    for r in range(2):
-                        nc.vector.tensor_tensor(
-                            out=sel[:, :, r, :],
-                            in0=sel[:, :, r, :],
-                            in1=factors[("low", b - 1)][:].rearrange("p k r o -> p k (r o)"),
-                            op=MULT,
+            def q_stage0(j):
+                even = ps_front.tile([P, 2, 2 * P], F32, name=uid("turned"), tag="even")
+                odd = ps_front.tile([P, 2, 2 * P], F32, name=uid("turned"), tag="odd")
+                for n in range(4):
+                    block = 4 * j + n
+                    for i in range(2):
+                        nc.tensor.transpose(
+                            (even, odd)[n % 2][:, n // 2, i * P : (i + 1) * P], expanded[:, i, block * P : (block + 1) * P], ident[:]
                         )
+                units = []
+                for n in range(2):
+                    i = 4 * j + 2 * n
+                    units.append((even[:, n, 0:N_PAIRS], odd[:, n, 0:N_PAIRS], q_data[:, i, :], q_data[:, i + 1, :], wq[:, 0, :], 2 * j + n, bias_q))
+                group(units)
 
-            q_weights()
+            def q_stage(s, j):
+                block_stage(q_data, wq[:, s, :], 2**s, range(4 * j, 4 * j + 4))
+
+            widen_q_weights()
+            turn_r_rows()
             widen_x(0)
             widen_x(1)
             turn_x(0)
@@ -486,405 +468,351 @@ def tile_butterflymlp_w4_kernel(
             quantize_x(1)
             for j in range(8):
                 for i in range(2):
-                    a_expand(i, j, i == 1)
+                    expand_pairs(i, j)
                 if j == 5:
                     widen_x(2)
-                    nc.scalar.copy(out=nat[0:112, :], in_=nat_raw[0:112, :])
+                    widen_factors()
                 if j == 6:
                     widen_x(3)
-            bit_columns()
+            bit4_columns()
             park_factors()
-            for b in (4, 5, 6, 0, 1, 2, 3):
-                fetch_factors(b, nc.gpsimd if b in GP_FACTORS else nc.sync)
-            def a_stage0(j):
-                pa, pb = banks()
-                for n in range(4):
-                    blk = 4 * j + n
-                    for i in range(2):
-                        nc.tensor.transpose((pa, pb)[n % 2][:, n // 2, i * P : (i + 1) * P], ht[:, i, blk * P : (blk + 1) * P], ident[:])
-                group(
-                    [
-                        (
-                            pa[:, n, 0:NA],
-                            pb[:, n, 0:NA],
-                            x1[:, 4 * j + 2 * n, :],
-                            x1[:, 4 * j + 2 * n + 1, :],
-                            x1[:, 4 * j + 2 * n : 4 * j + 2 * n + 2, :],
-                            wq[:, 0, :],
-                            2 * j + n,
-                            cq,
-                        )
-                        for n in range(2)
-                    ],
-                    "A0", j,
-                )
-
-            def a_stage(st, j):
-                free_stage(x1, wq[:, st, :], 2**st, range(4 * j, 4 * j + 4), "A", j)
-
+            for b in (4, 5, 6, 3, 2, 1, 0):
+                fetch_factors(b)
             for j in range(8):
-                a_stage0(j)
-                if j in (1, 3):
-                    turn_x(2 + j // 2)
+                q_stage0(j)
+                if j == 1:
+                    turn_x(2)
+                if j == 3:
+                    turn_x(3)
             quantize_x(2)
             quantize_x(3)
-            a_stage(1, 0)
-            a_stage(1, 1)
-            spread_weights()
-            stage0_bias(wp_up, bp[:].rearrange("p (k c) -> p k c", c=2), cp)
-            rest = [lambda st=st, j=j: a_stage(st, j) for st in range(1, 4) for j in range(4)][2:9]
-            side = [high_b, high_a, high_c, high_d, high_e, high_f]
-            side += [lambda: low_a(0), lambda: low_b(0), lambda: low_a(1), lambda: low_b(1), lambda: low_a(2), lambda: low_c(1)]
-            side += [lambda: low_b(2), lambda: low_a(3), lambda: low_c(2), lambda: low_b(3), lambda: low_c(3)]
-            weave((rest, 0, 1), (side, SIDE_FROM, 1))
+            q_stage(1, 0)
+            q_stage(1, 1)
+            weave(
+                ([lambda j=j: q_stage(1, j) for j in (2, 3)] + [lambda s=s, j=j: q_stage(s, j) for s in (2, 3) for j in range(4)], 0, 1),
+                ([lambda n=n: spread(n) for n in range(6)], 0, 0.5),
+                (
+                    [high_masks, high_rows, high_products, high_last_products, high_turns, high_store]
+                    + [lambda b=b: low_products(b) for b in range(1, 4)],
+                    0.7,
+                    1,
+                ),
+            )
 
-        xpool = ctx.enter_context(tc.tile_pool(name="xpool", bufs=1))
-        x = xpool.tile([P, 32, 512], F32, name="x")
+        hidden = ctx.enter_context(tc.tile_pool(name="hidden", bufs=1)).tile([P, BLOCKS, TOKENS], F32, name="hidden")
+        dense_half = hidden[:, :, N_PAIRS:TOKENS]
 
-        xb_all = x[:, :, NA:512]
+        def dense_and_stage9(data, w, first, h, t0, pool):
+            size = data.shape[-1]
+            units = []
+            for t in (t0, t0 + 1):
+                sides = []
+                for side in range(2):
+                    block = 4 * (2 * h + side) + t
+                    bank = pool.tile([P, BANK], F32, name=uid("dense"), tag="even" if side == 0 else "odd")
+                    at = first + block * P
+                    nc.tensor.matmul(out=bank[:, 0:size], lhsT=dense[:, at : at + P], rhs=data[:, block, :], start=True, stop=True)
+                    sides.append(bank[:, 0:size])
+                i = 8 * h + t
+                units.append((sides[0], sides[1], data[:, i, :], data[:, i + 4, :], w[:, 2, :], 4 * h + t, None))
+            group(units)
 
-        def xb(i):
-            return x[:, i, NA:512]
+        def gelu(g, first, last):
+            for block in range(4 * g, 4 * g + 4):
+                part = hidden[:, block, first:last]
+                nc.scalar.activation(out=part, in_=part, func=GELU, bias=up_bias_p[:, block : block + 1])
 
-        def xw(i):
-            return x[:, i, :]
-
-        with ExitStack() as middle:
-            ps0 = middle.enter_context(tc.psum_pool(name="ps0", bufs=2))
-            turned = middle.enter_context(tc.tile_pool(name="turned", bufs=2))
+        with ExitStack() as second:
+            ps_second = second.enter_context(tc.psum_pool(name="ps_second", bufs=2))
+            turned = second.enter_context(tc.tile_pool(name="turned", bufs=2))
 
             turned_tiles = {}
 
-            def b_expand(g):
-                hg = turned.tile([P, 3, 4, P], F32, name=uid("hg"), tag="hg")
+            def p_expand(g):
+                tile = turned.tile([P, 3, 4, P], F32, name=uid("p_expanded"), tag="p_expanded")
                 for i in range(3):
-                    ps = ps0.tile([P, 512], F32, name=uid("mx"), tag="mx", bufs=4)
-                    expand(ps[:], i + 1, g)
-                    src = ps[:].rearrange("p (q t) -> p t q", t=4)
-                    if i == 0 and g % EVAC_MOD == 0:
-                        nc.vector.tensor_copy(out=hg[:, i], in_=src)
-                    else:
-                        nc.scalar.copy(out=hg[:, i], in_=src)
-                turned_tiles[g] = hg
+                    bank = ps_second.tile([P, BANK], F32, name=uid("mx"), tag="mx", bufs=4)
+                    expand(bank[:], i + 1, g)
+                    copy(i == 0 and g % 2 == 0, tile[:, i], bank[:].rearrange("p (q t) -> p t q", t=4))
+                turned_tiles[g] = tile
 
-            def b_stage0(g):
-                hg = turned_tiles[g]
+            def p_stage0(g):
                 units = []
                 for n in range(2):
-                    pair = []
+                    sides = []
                     for t in (2 * n, 2 * n + 1):
-                        ps = ps0.tile([P, 512], F32, name=uid("b"), tag="fa" if t % 2 == 0 else "fb")
+                        bank = ps_second.tile([P, BANK], F32, name=uid("turned"), tag="even" if t % 2 == 0 else "odd")
                         for i in range(3):
-                            nc.tensor.transpose(ps[:, i * P : (i + 1) * P], hg[:, i, t, :], ident[:])
-                        pair.append(ps[:, 384 - NB : 384])
+                            nc.tensor.transpose(bank[:, i * P : (i + 1) * P], turned_tiles[g][:, i, t, :], ident[:])
+                        sides.append(bank[:, 3 * P - N_DENSE : 3 * P])
                     i = 4 * g + 2 * n
-                    units.append((pair[0], pair[1], xb(i), xb(i + 1), xb_all[:, i : i + 2, :], wp_up[:, 0, :], 2 * g + n, cp))
-                group(units, "B0", g)
+                    units.append((sides[0], sides[1], dense_half[:, i, :], dense_half[:, i + 1, :], wp_up[:, 0, :], 2 * g + n, bias_p))
+                group(units)
 
-            def b_stage1(j):
-                free_stage(xb_all, wp_up[:, 1, :], 2, range(4 * j, 4 * j + 4), "B", j)
-
-            def finish_dense(n, h):
-                view = mt[:, n * 4096 : (n + 1) * 4096].rearrange("p (k h l) -> p h k l", h=8, l=16)[:, h]
-                nc.vector.tensor_tensor(out=view, in0=view, in1=low[:, 32 * n : 32 * n + 32].rearrange("p k r o -> p k (r o)"), op=MULT)
-
-            def b_stage9(h, t0):
-                units = []
-                for t in (t0, t0 + 1):
-                    pair = []
-                    for side_ in range(2):
-                        blk = 4 * (2 * h + side_) + t
-                        ps = psg.tile([P, 512], F32, name=uid("b"), tag="fa" if side_ == 0 else "fb")
-                        nc.tensor.matmul(out=ps[:, 0:NB], lhsT=mt[:, blk * P : (blk + 1) * P], rhs=xb(blk), start=True, stop=True)
-                        pair.append(ps[:, 0:NB])
-                    i = 8 * h + t
-                    units.append((pair[0], pair[1], xb(i), xb(i + 4), xb_all[:, i : i + 5 : 4, :], wp_up[:, 2, :], 4 * h + t, None))
-                group(units, "B9", 2 * h + t0 // 2)
-
-            def region(c):
-                return out_flat[(c % 2) * REGION : (c % 2 + 1) * REGION]
+            def quarter(c):
+                return hbm[(c % 2) * QUARTER : (c % 2 + 1) * QUARTER]
 
             def q_store(c):
-                nc.sync.dma_start(out=region(c).rearrange("(x q n) -> q x n", x=8, q=P), in_=x1[:, c:32:4, :])
+                nc.sync.dma_start(out=quarter(c).rearrange("(x q n) -> q x n", x=8, q=P), in_=q_data[:, c:BLOCKS:4, :])
 
             def r_load(c):
-                nc.sync.dma_start(out=x2[c:P:4].rearrange("p m n -> p (m n)"), in_=region(c).rearrange("(z e) -> z e", z=32))
+                nc.sync.dma_start(out=r_data[c:P:4].rearrange("p m n -> p (m n)"), in_=quarter(c).rearrange("(p e) -> p e", p=32))
 
-            x2 = big.tile([P, 32, NA], F32, name="x2", tag="t32")
+            r_data = big.tile([P, BLOCKS, N_PAIRS], F32, name="r_data", tag="wide")
 
-            def a_stage4(c, hf):
-                free_stage(x1, wq[:, 4, :], 16, (c + 8 * hf, c + 4 + 8 * hf), "A4", 2 * c + hf)
-                if hf == 1:
+            def q_stage4(c, half):
+                block_stage(q_data, wq[:, 4, :], 16, (c + 8 * half, c + 4 + 8 * half), 1)
+                if half == 1:
                     q_store(c)
                     if c > 0:
                         r_load(c - 1)
 
-            a_stage(3, 1)
-            a_stage(3, 2)
-            b_expand(0)
-            first_b = []
+            p_steps = []
             for g in range(8):
                 if g < 7:
-                    first_b.append(lambda g=g: b_expand(g + 1))
-                first_b.append(lambda g=g: b_stage0(g))
-            weave(
-                (first_b, 0, 1),
-                (
-                    [lambda: a_stage(3, 3)] + [lambda c=c, hf=hf: a_stage4(c, hf) for c in range(4) for hf in range(2)],
-                    0,
-                    A4_TO,
-                ),
-            )
+                    p_steps.append(lambda g=g: p_expand(g + 1))
+                p_steps.append(lambda g=g: p_stage0(g))
+            p_expand(0)
+            weave((p_steps, 0, 1), ([lambda c=c, half=half: q_stage4(c, half) for c in range(4) for half in range(2)], 0, 0.9))
             r_load(3)
 
-        with ExitStack() as middle:
-            psg = middle.enter_context(tc.psum_pool(name="psg", bufs=4))
+        with ExitStack() as third:
+            ps_third = third.enter_context(tc.psum_pool(name="ps_third", bufs=4))
             spread_rows(1)
-            late = middle.enter_context(tc.tile_pool(name="late", bufs=1))
-            wc, wc_s = load_w(w_con_words, w_con_scales, D, 8)
-            bias_parts = []
+            late = third.enter_context(tc.tile_pool(name="late", bufs=1))
+            con_codes, con_planes = load_weight(w_con_words, w_con_scales, 8, D, 1, nc.gpsimd)
+            bias_rows = []
             for n, vec in enumerate((b_con, down_bias)):
-                raw = late.tile([P, D], BF16, name="bias_raw%d" % n)
-                nc.sync.dma_start(out=raw[:], in_=vec.partition_broadcast(P))
-                bias_parts.append(raw)
-            bias = const.tile([P, D], F32, name="bias")
-            nc.gpsimd.tensor_tensor(out=bias[:], in0=bias_parts[0][:], in1=bias_parts[1][:], op=ADD)
-            x3 = big.tile([P, 32, NA], F32, name="x3", tag="x1")
+                row = late.tile([P, D], BF16, name="bias_row_%d" % n)
+                nc.sync.dma_start(out=row[:], in_=vec.partition_broadcast(P))
+                bias_rows.append(row)
+            out_bias = const.tile([P, D], F32, name="out_bias")
+            nc.gpsimd.tensor_tensor(out=out_bias[:], in0=bias_rows[0][:], in1=bias_rows[1][:], op=ADD)
+            p_data = big.tile([P, BLOCKS, N_PAIRS], F32, name="p_data", tag="pairs")
+
+            def finish_dense(n, o_top):
+                view = dense[:, n * BLOCKS * P : (n + 1) * BLOCKS * P].rearrange("p (k h l) -> p h k l", h=8, l=16)[:, o_top]
+                factor = low[:, BLOCKS * n : BLOCKS * (n + 1)].rearrange("p k r o -> p k (r o)")
+                nc.vector.tensor_tensor(out=view, in0=view, in1=factor, op=MULT)
+
+            def p_stage1(j):
+                block_stage(dense_half, wp_up[:, 1, :], 2, range(4 * j, 4 * j + 4))
+
+            def p_stage9(h, t0):
+                dense_and_stage9(dense_half, wp_up, 0, h, t0, ps_third)
+
             weave(
-                ([lambda j=j: b_stage1(j) for j in range(4)], 0, 1),
-                ([lambda h=h: finish_dense(0, h) for h in range(8)], 0, FIN_TO),
+                ([lambda j=j: p_stage1(j) for j in range(4)], 0, 1),
+                ([lambda o_top=o_top: finish_dense(0, o_top) for o_top in range(8)], 0, 0.5),
             )
-            for t0 in (0, 2):
-                b_stage9(0, t0)
+            p_stage9(0, 0)
+            p_stage9(0, 2)
+
+            def r_stage(s, j):
+                block_stage(r_data, wr[:, s - 5, :], 2 ** (s - 5), range(4 * j, 4 * j + 4))
 
             def r_store(c):
-                reg = region(c).rearrange("(v m z) -> v m z", v=2, m=4)
                 for v in range(2):
                     nc.sync.dma_start(
-                        out=reg[v].rearrange("m (z n) -> z m n", z=P), in_=x2[:, 16 * v + 4 * c : 16 * v + 4 * c + 4, :]
+                        out=quarter(c).rearrange("(v m z) -> v m z", v=2, m=4)[v].rearrange("m (p n) -> p m n", p=P),
+                        in_=r_data[:, 16 * v + 4 * c : 16 * v + 4 * c + 4, :],
                     )
 
             def p_load(c):
-                reg = region(c).rearrange("(v m z) -> v m z", v=2, m=4)
                 for v in range(2):
                     nc.sync.dma_start(
-                        out=x3[32 * c : 32 * c + 32].rearrange("p (g t) n -> p g (t n)", t=4)[:, v:8:2, :],
-                        in_=reg[v].rearrange("m (x h n) -> (m x) h n", x=8, h=4),
+                        out=p_data[32 * c : 32 * c + 32].rearrange("p (g t) n -> p g (t n)", t=4)[:, v:8:2, :],
+                        in_=quarter(c).rearrange("(v m z) -> v m z", v=2, m=4)[v].rearrange("m (x h n) -> (m x) h n", x=8, h=4),
                     )
 
-            def r_stage(st, j):
-                free_stage(x2, wr[:, st, :], 2**st, range(4 * j, 4 * j + 4), "A", j)
-
-            def r_last(c):
-                r_stage(4, c)
+            def r_stage9(c):
+                r_stage(9, c)
                 r_store(c)
                 if c > 0:
                     p_load(c - 1)
                 if c == 3:
                     p_load(3)
 
-            for st in range(3):
+            for s in (5, 6, 7):
                 for j in range(4):
-                    r_stage(st, j)
+                    r_stage(s, j)
             weave(
-                ([lambda j=j: r_stage(3, j) for j in range(4)] + [lambda c=c: r_last(c) for c in range(4)], 0, R9_TO),
-                ([lambda h=h, t0=t0: b_stage9(h, t0) for h in range(1, 4) for t0 in (0, 2)], 0.1, 1),
+                ([lambda j=j: r_stage(8, j) for j in range(4)] + [lambda c=c: r_stage9(c) for c in range(4)], 0, 0.7),
+                ([lambda h=h, t0=t0: p_stage9(h, t0) for h in range(1, 4) for t0 in (0, 2)], 0.1, 1),
             )
 
-            def b_stage10(h2, g0):
-                free_stage(xb_all, wp_up[:, 3, :], 8, [8 * h2 + 4 * g0 + t for t in range(4)], "B", 2 * h2 + g0)
+            def p_stage10(g2, g0):
+                block_stage(dense_half, wp_up[:, 3, :], 8, [8 * g2 + 4 * g0 + t for t in range(4)])
 
-            def b_stage11(gg):
-                free_stage(xb_all, wp_up[:, 4, :], 16, [4 * gg + t for t in range(4)], "B", gg)
+            def p_stage11(g):
+                block_stage(dense_half, wp_up[:, 4, :], 16, [4 * g + t for t in range(4)])
 
-            def gelu(gg, first, last):
-                for g in (gg, gg + 4):
-                    for blk in range(4 * g, 4 * g + 4):
-                        part = x[:, blk, first:last]
-                        nc.scalar.activation(out=part, in_=part, func=GELU, bias=ub[:, blk : blk + 1])
+            def dense_gelu(g):
+                for side in (g, g + 4):
+                    gelu(side, N_PAIRS, TOKENS)
 
             weave(
                 (
-                    [lambda h2=h2, g0=g0: b_stage10(h2, g0) for h2 in range(2) for g0 in range(2)]
-                    + [lambda: b_stage11(0), lambda: b_stage11(1), lambda: gelu(0, NA, 512), lambda: b_stage11(2)]
-                    + [lambda: gelu(1, NA, 512), lambda: b_stage11(3), lambda: gelu(2, NA, 512)],
+                    [lambda g2=g2, g0=g0: p_stage10(g2, g0) for g2 in range(2) for g0 in range(2)]
+                    + [lambda: p_stage11(0), lambda: p_stage11(1), lambda: dense_gelu(0), lambda: p_stage11(2)]
+                    + [lambda: dense_gelu(1), lambda: p_stage11(3), lambda: dense_gelu(2)],
                     0,
                     1,
                 ),
-                ([lambda h=h: finish_dense(1, h) for h in range(8)], 0, 1),
+                ([lambda o_top=o_top: finish_dense(1, o_top) for o_top in range(8)], 0, 1),
             )
 
-        wide_pool["tmp"] = ctx.enter_context(tc.tile_pool(name="tmpw", bufs=1))
+        temps_all["pool"] = ctx.enter_context(tc.tile_pool(name="temps_all", bufs=1))
 
-        def a_stage10(h2, g0):
-            free_stage(x3, wp_up[:, 3, :], 8, [8 * h2 + 4 * g0 + t for t in range(4)], "A3", 2 * h2 + g0)
+        with ExitStack() as fourth:
+            ps_fourth = fourth.enter_context(tc.psum_pool(name="ps_fourth", bufs=4))
 
-        def a_stage11(gg):
-            free_stage(x3, wp_up[:, 4, :], 16, [4 * gg + t for t in range(4)], "A3", gg, dst=x[:, :, 0:NA])
+            def pairs_stage10(g2, g0):
+                block_stage(p_data, wp_up[:, 3, :], 8, [8 * g2 + 4 * g0 + t for t in range(4)], 3)
 
-        with ExitStack() as down:
-            psc = down.enter_context(tc.psum_pool(name="psc", bufs=4))
+            def pairs_stage11(g):
+                block_stage(p_data, wp_up[:, 4, :], 16, [4 * g + t for t in range(4)], 3, hidden[:, :, 0:N_PAIRS])
 
-            def c_gelu(g):
-                for blk in range(4 * g, 4 * g + 4):
-                    part = x[:, blk, 0:NA]
-                    nc.scalar.activation(out=part, in_=part, func=GELU, bias=ub[:, blk : blk + 1])
+            def pairs_gelu(g):
+                gelu(g, 0, N_PAIRS)
 
-            def c_stage0(g):
-                free_stage(x, wp_dn[:, 0, :], 1, (2 * g, 2 * g + 1), "C0", g)
+            def down_stage0(g):
+                block_stage(hidden, wp_down[:, 0, :], 1, (2 * g, 2 * g + 1))
 
-            def c_stage1(g):
-                free_stage(x, wp_dn[:, 1, :], 2, (2 * g, 2 * g + 1), "C1", g)
+            def down_stage1(g):
+                block_stage(hidden, wp_down[:, 1, :], 2, (2 * g, 2 * g + 1), g % 2)
 
-            def c_stage9(h, t0):
-                units = []
-                for t in (t0, t0 + 1):
-                    pair = []
-                    for side_ in range(2):
-                        blk = 4 * (2 * h + side_) + t
-                        ps = psc.tile([P, 512], F32, name=uid("c"), tag="ca" if side_ == 0 else "cb")
-                        nc.tensor.matmul(out=ps[:], lhsT=mt[:, (32 + blk) * P : (33 + blk) * P], rhs=xw(blk), start=True, stop=True)
-                        pair.append(ps)
-                    i = 8 * h + t
-                    units.append((pair[0][:], pair[1][:], xw(i), xw(i + 4), x[:, i : i + 5 : 4, :], wp_dn[:, 2, :], 4 * h + t, None))
-                group(units, "C9", 2 * h + t0 // 2)
+            def down_stage9(h, t0):
+                dense_and_stage9(hidden, wp_down, BLOCKS * P, h, t0, ps_fourth)
 
-            def c_stage10(h2, g0):
+            def down_stage10(g2, g0):
                 for t in (0, 2):
-                    free_stage(x, wp_dn[:, 3, :], 8, [8 * h2 + 4 * g0 + t, 8 * h2 + 4 * g0 + t + 1], "C10", 4 * h2 + 2 * g0 + t // 2)
+                    k = 8 * g2 + 4 * g0 + t
+                    block_stage(hidden, wp_down[:, 3, :], 8, (k, k + 1))
 
-            a_stage10(0, 0)
-            a_stage10(1, 0)
-            gelu(3, NA, 512)
-            a_stage10(0, 1)
-            a_stage11(0)
-            a_stage10(1, 1)
-            c_gelu(0)
-            c_gelu(4)
-            a_stage11(1)
-            c_stage0(0)
-            c_gelu(1)
-            a_stage11(2)
-            c_stage1(0)
-            c_stage0(1)
-            c_gelu(5)
-            c_stage0(4)
-            c_stage1(1)
-            c_gelu(2)
-            c_stage0(5)
-            c_stage1(4)
-            c_stage9(0, 0)
-            a_stage11(3)
-            c_gelu(3)
-            c_stage1(5)
-            c_stage9(0, 2)
-            c_stage0(2)
-            c_gelu(6)
-            c_stage9(2, 0)
-            c_stage0(3)
-            c_stage1(2)
-            c_stage9(2, 2)
-            c_gelu(7)
-            c_stage1(3)
-            c_stage0(6)
-            c_stage9(1, 0)
-            c_stage0(7)
-            c_stage1(6)
-            c_stage9(1, 2)
-            c_stage1(7)
-            c_stage10(0, 0)
-            c_stage9(3, 0)
-            c_stage10(0, 1)
-            c_stage9(3, 2)
-            c_stage10(1, 0)
-            c_stage10(1, 1)
+            pairs_stage10(0, 0)
+            pairs_stage10(1, 0)
+            dense_gelu(3)
+            pairs_stage10(0, 1)
+            pairs_stage11(0)
+            pairs_stage10(1, 1)
+            pairs_gelu(0)
+            pairs_gelu(4)
+            pairs_stage11(1)
+            down_stage0(0)
+            pairs_gelu(1)
+            pairs_stage11(2)
+            down_stage1(0)
+            down_stage0(1)
+            pairs_gelu(5)
+            down_stage0(4)
+            down_stage1(1)
+            pairs_gelu(2)
+            down_stage0(5)
+            down_stage1(4)
+            down_stage9(0, 0)
+            pairs_stage11(3)
+            pairs_gelu(3)
+            down_stage1(5)
+            down_stage9(0, 2)
+            down_stage0(2)
+            pairs_gelu(6)
+            down_stage9(2, 0)
+            down_stage0(3)
+            down_stage1(2)
+            down_stage9(2, 2)
+            pairs_gelu(7)
+            down_stage1(3)
+            down_stage0(6)
+            down_stage9(1, 0)
+            down_stage0(7)
+            down_stage1(6)
+            down_stage9(1, 2)
+            down_stage1(7)
+            down_stage10(0, 0)
+            down_stage9(3, 0)
+            down_stage10(0, 1)
+            down_stage9(3, 2)
+            down_stage10(1, 0)
+            down_stage10(1, 1)
 
-        psa = ctx.enter_context(tc.psum_pool(name="psa", bufs=1))
-        fin = big.tile([P, 12288], BF16, name="fin", tag="x1")
-        accs = {}
+        ps_out = ctx.enter_context(tc.psum_pool(name="ps_out", bufs=1))
+        h2 = big.tile([P, 12288], BF16, name="h2", tag="pairs")
+        sums = {}
         for i in range(4):
             for d in range(2):
-                acc = psa.tile([P, 512], F32, name="acc%d_%d" % (i, d), tag="acc%d_%d" % (i, d))
-                accs[(i, d)] = acc
-        hc = const.tile([P, 2, 512], U32, name="hc", tag="xq", align_bytes=64)
-        hs = const.tile([P, 2, 512], U8, name="hs", tag="xs", align_bytes=64)
+                bank = ps_out.tile([P, BANK], F32, name="sum_%d_%d" % (i, d))
+                sums[(i, d)] = bank
+        h2_codes = const.tile([P, 2, TOKENS], U32, name="h2_codes", tag="codes", align_bytes=64)
+        h2_planes = const.tile([P, 2, TOKENS], U8, name="h2_planes", tag="planes", align_bytes=64)
 
-        def hb(g):
+        def h2_rows(g):
             at = 2048 * (2 * (g % 2) + g // 4)
-            return fin[:, at : at + 2048].rearrange("p (t n) -> p t n", t=4)
+            return h2[:, at : at + 2048].rearrange("p (t n) -> p t n", t=4)
 
-        def fin_pair(gg, t):
-            at = 4096 * (gg % 2)
-            return fin[:, at : at + 4096].rearrange("p (v t n) -> p v t n", v=2, t=4)[:, :, t, :]
+        def h2_grouped(g):
+            at = 8192 + 2048 * (g // 4)
+            return h2[:, at : at + 2048].rearrange("p (n t) -> p n t", t=4)
 
-        def hi(slot):
-            at = 8192 + 2048 * slot
-            return fin[:, at : at + 2048].rearrange("p (n t) -> p n t", t=4)
-
-        def last_stage(gg, t0):
+        def down_stage11(g, t0):
             units = []
             for t in (t0, t0 + 1):
-                k = 4 * gg + t
-                units.append((xw(k), xw(k + 16), hb(gg)[:, t, :], hb(gg + 4)[:, t, :], fin_pair(gg, t), wp_dn[:, 4, :], k, None))
-            group(units, "C11", 2 * gg + t0 // 2)
+                k = 4 * g + t
+                units.append((hidden[:, k, :], hidden[:, k + 16, :], h2_rows(g)[:, t, :], h2_rows(g + 4)[:, t, :], wp_down[:, 4, :], k, None))
+            group(units)
 
-        def lay(g, tok):
-            src = hb(g)[:, :, tok].rearrange("p t n -> p n t")
-            if g < 4:
-                nc.vector.tensor_copy(out=hi(g // 4)[:, tok, :], in_=src)
-            else:
-                nc.scalar.copy(out=hi(g // 4)[:, tok, :], in_=src)
+        def lay_words(g, tokens):
+            for half_pass in (g, g + 4):
+                copy(half_pass < 4, h2_grouped(half_pass)[:, tokens, :], h2_rows(half_pass)[:, :, tokens].rearrange("p t n -> p n t"))
 
-        def quantize_h(g, tok):
-            slot = g // 4
+        def quantize_h2(g, tokens):
             nc.vector.quantize_mx(
-                out=hc[:, slot, tok].bitcast(FP8X4), scales=hs[:, slot, tok], in_=hi(slot)[:, tok, :].rearrange("p n t -> p (n t)")
+                out=h2_codes[:, g // 4, tokens].bitcast(FP8X4),
+                scales=h2_planes[:, g // 4, tokens],
+                in_=h2_grouped(g)[:, tokens, :].rearrange("p n t -> p (n t)"),
             )
 
-        def contract(g, tiles, first_pass, last_pass):
-            slot = g // 4
-            for i in tiles:
+        def contract(g, token_tiles):
+            for i in token_tiles:
                 for d in range(2):
                     nc.tensor.matmul_mx(
-                        out=accs[(i, d)][:],
-                        lhsT=hc[:, slot, i * P : (i + 1) * P].bitcast(FP8X4),
-                        lhsT_scale=hs[:, slot, i * P : (i + 1) * P],
-                        rhs=wc[:, g, 1024 * d : 1024 * (d + 1)].bitcast(FP4X4),
-                        rhs_scale=wc_s[:, g, 512 * d : 512 * (d + 1)],
-                        start=first_pass,
-                        stop=last_pass,
+                        out=sums[(i, d)][:],
+                        lhsT=h2_codes[:, g // 4, i * P : (i + 1) * P].bitcast(FP8X4),
+                        lhsT_scale=h2_planes[:, g // 4, i * P : (i + 1) * P],
+                        rhs=con_codes[:, g, 1024 * d : 1024 * (d + 1)].bitcast(FP4X4),
+                        rhs_scale=con_planes[:, g, 512 * d : 512 * (d + 1)],
+                        start=(g == 0),
+                        stop=(g == 7),
                     )
 
-        def finish(tiles):
-            for i in tiles:
+        def store(token_tiles):
+            for i in token_tiles:
                 for d in range(2):
-                    o = wide_pool["tmp"].tile([P, 512], F32, name=uid("o"), tag="t", bufs=BUFS_T_WIDE)
-                    nc.vector.tensor_tensor(out=o[:], in0=accs[(i, d)][:], in1=bias[:, 512 * d : 512 * (d + 1)], op=ADD)
-                    nc.sync.dma_start(out=out_rows[i * P : (i + 1) * P, 512 * d : 512 * (d + 1)], in_=o[:])
+                    o = temps_all["pool"].tile([P, BANK], F32, name=uid("out"), tag="t", bufs=TEMPS_ALL)
+                    cols = slice(512 * d, 512 * (d + 1))
+                    nc.vector.tensor_tensor(out=o[:], in0=sums[(i, d)][:], in1=out_bias[:, cols], op=ADD)
+                    nc.sync.dma_start(out=out_rows[i * P : (i + 1) * P, cols], in_=o[:])
 
-        whole = slice(0, 512)
-        for gg in range(4):
-            last_stage(gg, 0)
-            if gg > 0:
-                for g in (gg - 1, gg + 3):
-                    lay(g, whole)
-            last_stage(gg, 2)
-            if gg > 0:
-                for g in (gg - 1, gg + 3):
-                    quantize_h(g, whole)
-                    contract(g, range(4), g == 0, False)
-        halves = [slice(0, 256), slice(256, 512)]
+        every = slice(0, TOKENS)
+        for g in range(4):
+            down_stage11(g, 0)
+            if g > 0:
+                lay_words(g - 1, every)
+            down_stage11(g, 2)
+            if g > 0:
+                for done in (g - 1, g + 3):
+                    quantize_h2(done, every)
+                    contract(done, range(4))
+        first_half, second_half = slice(0, 256), slice(256, TOKENS)
+        lay_words(3, first_half)
         for g in (3, 7):
-            lay(g, halves[0])
+            quantize_h2(g, first_half)
+        lay_words(3, second_half)
         for g in (3, 7):
-            quantize_h(g, halves[0])
+            contract(g, (0, 1))
         for g in (3, 7):
-            lay(g, halves[1])
-        contract(3, (0, 1), False, False)
-        contract(7, (0, 1), False, True)
+            quantize_h2(g, second_half)
         for g in (3, 7):
-            quantize_h(g, halves[1])
-        contract(3, (2, 3), False, False)
-        contract(7, (2, 3), False, True)
-        finish((0, 1))
-        finish((2, 3))
+            contract(g, (2, 3))
+        store((0, 1))
+        store((2, 3))

from contextlib import ExitStack

import concourse.mybir as mybir
from concourse.masks import make_identity

F32 = mybir.dt.float32
BF16 = mybir.dt.bfloat16
U32 = mybir.dt.uint32
I32 = mybir.dt.int32
U8 = mybir.dt.uint8
FP8 = mybir.dt.float8_e4m3fn
FP8X4 = mybir.dt.float8_e4m3fn_x4
FP4X4 = mybir.dt.float4_e2m1fn_x4
ADD = mybir.AluOpType.add
MULT = mybir.AluOpType.mult
COPY = mybir.ActivationFunctionType.Copy
IDENTITY = mybir.ActivationFunctionType.Identity
GELU = mybir.ActivationFunctionType.Gelu

P = 128
D = 1024
H = 4096
TOKENS = 512
BLOCKS = 32
BANK = 512
N_PAIRS = 208
N_DENSE = TOKENS - N_PAIRS
QUARTER = N_PAIRS * H // 4
FACTOR = 16 * D
TEMPS = 7
TEMPS_ALL = 5

FLOPS = 2 * 2 * TOKENS * D * H


def weave(*lists):
    keyed = []
    for n, (steps, first, last) in enumerate(lists):
        for i, step in enumerate(steps):
            keyed.append((first + (last - first) * (i + 0.5) / len(steps), n, i, step))
    for entry in sorted(keyed, key=lambda e: e[:3]):
        entry[3]()


def tile_butterflymlp_w4_kernel(
    tc, x_bytes, x_scale, w_exp_words, w_exp_scales, b_exp, up_w, up_bias, down_w, w_con_words, w_con_scales, b_con, down_bias, out
):
    nc = tc.nc
    hbm = out.rearrange("b s d -> (b s d)")
    out_rows = out.rearrange("b s d -> (b s) d")
    x_rows = x_bytes.rearrange("b s k -> (b s) k")
    row_area = hbm[2 * QUARTER : 2 * QUARTER + 65536]
    serial = {"n": 0}

    def uid(prefix):
        serial["n"] += 1
        return "%s_%d" % (prefix, serial["n"])

    with ExitStack() as ctx:
        ctx.enter_context(tc.manual_schedule())
        const = ctx.enter_context(tc.tile_pool(name="const", bufs=1))
        big = ctx.enter_context(tc.tile_pool(name="big", bufs=1))
        temps = ctx.enter_context(tc.tile_pool(name="temps", bufs=1))
        temps_all = {}

        def copy(on_vector, dst, src):
            if on_vector:
                nc.vector.tensor_copy(out=dst, in_=src)
            else:
                nc.scalar.copy(out=dst, in_=src)

        def group(units, n_vector=0):
            size = units[0][0].shape[-1]
            products = []
            for n, (a, b, new_a, new_b, w, k, c) in enumerate(units):
                if size == TOKENS:
                    full = temps_all["pool"].tile([P, 2, TOKENS], F32, name=uid("t"), tag="t", bufs=TEMPS_ALL)
                else:
                    full = temps.tile([P, 2, N_DENSE], F32, name=uid("t"), tag="t", bufs=TEMPS)
                t = full[:, :, 0:size]
                for r in range(2):
                    w_a = w[:, 4 * k + 2 * r : 4 * k + 2 * r + 1]
                    if 2 * n + r < n_vector:
                        nc.vector.tensor_scalar(out=t[:, r], in0=a, scalar1=w_a, scalar2=None, op0=MULT)
                    elif c is not None:
                        nc.scalar.activation(out=t[:, r], in_=a, func=IDENTITY, scale=w_a, bias=c[:, k, r : r + 1])
                    else:
                        nc.scalar.activation(out=t[:, r], in_=a, func=COPY, scale=w_a)
                products.append(t)
            for r in range(2):
                for (a, b, new_a, new_b, w, k, c), t in zip(units, products):
                    w_b = w[:, 4 * k + 2 * r + 1 : 4 * k + 2 * r + 2]
                    nc.vector.scalar_tensor_tensor(out=(new_a, new_b)[r], in0=b, scalar=w_b, in1=t[:, r], op0=MULT, op1=ADD)

        def block_stage(src, w, bit, pairs, n_vector=0, dst=None):
            dst = src if dst is None else dst
            units = []
            for k in pairs:
                i = (k // bit) * 2 * bit + k % bit
                j = i + bit
                units.append((src[:, i, :], src[:, j, :], dst[:, i, :], dst[:, j, :], w, k, None))
            group(units, n_vector)

        ident = const.tile([P, P], F32, name="ident")
        make_identity(nc, ident[:])
        ident_b = const.tile([P, P], BF16, name="ident_b")
        nc.gpsimd.tensor_copy(out=ident_b[:], in_=ident[:])
        wq = const.tile([P, 5, 64], F32, name="wq")
        wr = const.tile([P, 5, 64], F32, name="wr")
        wp_up = const.tile([P, 5, 64], F32, name="wp_up")
        wp_down = const.tile([P, 5, 64], F32, name="wp_down")
        bias_q = const.tile([P, 16, 2], F32, name="bias_q")
        bias_p = const.tile([P, 16, 2], F32, name="bias_p")
        b_exp_p = const.tile([P, BLOCKS], F32, name="b_exp_p")
        up_bias_p = const.tile([P, BLOCKS], F32, name="up_bias_p")
        bit4 = const.tile([P, 2], F32, name="bit4")
        dense = const.tile([P, 2 * BLOCKS * P], F32, name="dense")
        low = const.tile([P, 2 * BLOCKS, 2, 8], F32, name="low")
        x_codes = const.tile([P, 2, TOKENS], U32, name="x_codes", tag="codes", align_bytes=64)
        x_planes = const.tile([P, 2, TOKENS], U8, name="x_planes", tag="planes", align_bytes=64)
        q_data = big.tile([P, BLOCKS, N_PAIRS], F32, name="q_data", tag="pairs")

        def load_weight(words, scales, passes, n, cuts, zeroing):
            w = big.tile([P, 3 * passes * n], U8, name=uid("w"), tag="w", align_bytes=64)
            codes = w[:, 0 : 2 * passes * n].rearrange("p (g n) -> p g n", g=passes)
            planes = w[:, 2 * passes * n :].rearrange("p (g n) -> p g n", g=passes)
            zeroing.memset(w[:, 2 * passes * n :].bitcast(I32), 0)
            plane_cuts = (cuts + 1) // 2
            for cut in range(cuts):
                if cut % 2 == 0:
                    cols = slice(cut // 2 * n // plane_cuts, (cut // 2 + 1) * n // plane_cuts)
                    for j in range(4):
                        nc.sync.dma_start(
                            out=planes[j:P:32, :, cols].bitcast(I32),
                            in_=scales[:, :, cols].rearrange("g (q j) n -> j q g n", j=4)[j].bitcast(I32),
                        )
                cols = slice(cut * 2 * n // cuts, (cut + 1) * 2 * n // cuts)
                nc.sync.dma_start(out=codes[:, :, cols].bitcast(I32), in_=words[:, :, cols].rearrange("g p n -> p g n").bitcast(I32))
            return codes, planes

        with ExitStack() as front:
            early = front.enter_context(tc.tile_pool(name="early", bufs=1))
            ps_turn = front.enter_context(tc.psum_pool(name="ps_turn", bufs=2))
            ps_front = front.enter_context(tc.psum_pool(name="ps_front", bufs=3))

            scale_row = early.tile([P, D], F32, name="scale_row")
            p_rows = early.tile([P, 2048], BF16, name="p_rows")
            nc.gpsimd.memset(p_rows[:].bitcast(I32), 0)
            r_rows = early.tile([P, 512], BF16, name="r_rows")
            nc.gpsimd.memset(r_rows[:].bitcast(I32), 0)
            wq_raw = early.tile([P, 5, 64], BF16, name="wq_raw")
            b_exp_q_raw = early.tile([P, BLOCKS], BF16, name="b_exp_q_raw")
            factor_raw = early.tile([P, D], BF16, name="factor_raw")
            x_byte_tiles = {}

            def load_x(i):
                byte_tile = early.tile([P, D], U8, name="x_bytes_%d" % i, tag="x_bytes", bufs=4)
                nc.sync.dma_start(out=byte_tile[:], in_=x_rows[i * P : (i + 1) * P, :])
                x_byte_tiles[i] = byte_tile

            load_x(0)
            load_x(1)
            nc.sync.dma_start(out=scale_row[:], in_=x_scale.rearrange("a b k -> (a b k)").partition_broadcast(P))
            exp_codes, exp_planes = load_weight(w_exp_words, w_exp_scales, 2, H, 4, nc.vector)
            for b in range(7):
                for n, w in enumerate((up_w, down_w)):
                    row = 16 * b + 8 * n
                    nc.sync.dma_start(out=factor_raw[row : row + 8, :], in_=w[2 + b].rearrange("(g k) r c -> g (k r c)", g=8))
            load_x(2)
            load_x(3)
            nc.sync.dma_start(out=wq_raw[:], in_=up_w[0:5].rearrange("s (q k) r c -> q s (k r c)", q=P))
            nc.sync.dma_start(out=b_exp_q_raw[:], in_=b_exp.rearrange("(q r) -> q r", q=P))
            for n, w in enumerate((up_w, down_w)):
                nc.sync.dma_start(out=p_rows[16 * n : 16 * n + 16, 0:1024], in_=w[0:2].rearrange("s (g k) r c -> (s g) (k r c)", g=8))
                nc.sync.dma_start(out=p_rows[32 + 12 * n : 44 + 12 * n, :], in_=w[9:12].rearrange("s (h k) r c -> (s h) (k r c)", h=4))
            nc.sync.dma_start(out=p_rows[64:72, 0:512], in_=b_exp.rearrange("(g e) -> g e", g=8))
            nc.sync.dma_start(out=p_rows[72:80, 0:512], in_=up_bias.rearrange("(g e) -> g e", g=8))
            for s in range(5):
                nc.sync.dma_start(
                    out=r_rows[16 * s : 16 * s + 16, :].rearrange("p (h e) -> p h e", h=4),
                    in_=up_w[5 + s].rearrange("(h m r) a c -> m h (r a c)", h=4, m=16),
                )

            x_rounded = {}
            x_grouped = {}

            def widen_x(i):
                rounded = early.tile([P, D], BF16, name="x_rounded_%d" % i, tag="x_rounded", bufs=2)
                nc.vector.tensor_tensor(out=rounded[:], in0=x_byte_tiles[i][:].bitcast(FP8), in1=scale_row[:], op=MULT)
                x_rounded[i] = rounded

            def turn_x(i):
                words = x_rounded[i][:].bitcast(F32)
                bank = ps_turn.tile([P, 2, 2, P], F32, name="x_bank_%d" % i, tag="turn")
                for g in range(2):
                    for u in range(2):
                        nc.tensor.transpose(bank[:, g, u, :], words[:, 256 * g + u : 256 * (g + 1) : 2], ident[:])
                grouped = early.tile([P, 2, P, 4], BF16, name="x_grouped_%d" % i, tag="x_grouped", bufs=2, align_bytes=64)
                for g in range(2):
                    dst = grouped[:, g].rearrange("p n t -> p (n t)").bitcast(F32)
                    copy(i < 2, dst.rearrange("p (n u) -> p n u", u=2), bank[:, g].rearrange("p u n -> p n u"))
                x_grouped[i] = grouped

            def quantize_x(i):
                tokens = slice(i * P, (i + 1) * P)
                for g in range(2):
                    nc.vector.quantize_mx(
                        out=x_codes[:, g, tokens].bitcast(FP8X4),
                        scales=x_planes[:, g, tokens],
                        in_=x_grouped[i][:, g].rearrange("p n t -> p (n t)"),
                    )

            def expand(bank, i, j):
                tokens = slice(i * P, (i + 1) * P)
                for g in range(2):
                    nc.tensor.matmul_mx(
                        out=bank,
                        lhsT=x_codes[:, g, tokens].bitcast(FP8X4),
                        lhsT_scale=x_planes[:, g, tokens],
                        rhs=exp_codes[:, g, 1024 * j : 1024 * (j + 1)].bitcast(FP4X4),
                        rhs_scale=exp_planes[:, g, 512 * j : 512 * (j + 1)],
                        start=(g == 0),
                        stop=(g == 1),
                    )

            expanded = big.tile([P, 2, H], F32, name="expanded", tag="wide")

            def expand_pairs(i, j):
                bank = ps_front.tile([P, BANK], F32, name=uid("mx"), tag="even" if i == 0 else "odd")
                expand(bank[:], i, j)
                copy(
                    i == 1,
                    expanded[:, i].rearrange("p (r q) -> p r q", r=BLOCKS)[:, :, 16 * j : 16 * (j + 1)],
                    bank[:].rearrange("p (q r) -> p r q", r=BLOCKS),
                )

            r_rows_turned = early.tile([P, 512], BF16, name="r_rows_turned")
            spread_banks = {}

            def turn_r_rows():
                nc.gpsimd.tensor_copy(
                    out=r_rows_turned[:].rearrange("p (x h e) -> p x h e", x=8, h=4),
                    in_=r_rows[:].rearrange("p (h x e) -> p x h e", x=8, h=4),
                )

            def spread_turns(step):
                rows, count, first, stride = (
                    (p_rows, 8, 0, 8),
                    (p_rows, 8, 0, 16),
                    (p_rows, 8, 8, 16),
                    (p_rows, 4, 0, 4),
                    (r_rows_turned, 4, 0, 4),
                )[step]
                bank = ps_turn.tile([P, 8, P], BF16, name=uid("spread"), tag="turn")
                for j in range(count):
                    nc.tensor.transpose(bank[:, j, :], rows[:, first + j : P * stride : stride], ident_b[:])
                spread_banks[step] = bank

            def spread_copies(step):
                bank = spread_banks[step]
                if step == 0:
                    for n, wp in enumerate((wp_up, wp_down)):
                        nc.scalar.copy(
                            out=wp[:, 0:2, :].rearrange("p s (g j) -> p (s g) j", j=8),
                            in_=bank[:, :, 16 * n : 16 * n + 16].rearrange("p j s -> p s j"),
                        )
                elif step < 3:
                    at = 8 * (step - 1)
                    for n, wp in enumerate((wp_up, wp_down)):
                        nc.scalar.copy(
                            out=wp[:, 2:5, :].rearrange("p s (h j) -> p (s h) j", j=16)[:, :, at : at + 8],
                            in_=bank[:, :, 32 + 12 * n : 44 + 12 * n].rearrange("p j s -> p s j"),
                        )
                elif step == 3:
                    for row, vec in ((64, b_exp_p), (72, up_bias_p)):
                        nc.scalar.copy(
                            out=vec[:].rearrange("p (g t) -> p g t", t=4), in_=bank[:, 0:4, row : row + 8].rearrange("p t g -> p g t")
                        )
                    first_stage_bias(wp_up, b_exp_p[:].rearrange("p (k c) -> p k c", c=2), bias_p)
                else:
                    nc.scalar.copy(
                        out=wr[:].rearrange("p s (m j) -> p (s m) j", j=4), in_=bank[:, 0:4, 0:80].rearrange("p j s -> p s j")
                    )

            def spread(step):
                if step < 5:
                    spread_turns(step)
                if step > 0:
                    spread_copies(step - 1)

            def first_stage_bias(w, b_pairs, bias):
                prod = early.tile([P, 2, 16, 2], F32, name=uid("prod"), tag="prod", bufs=2)
                w_pairs = w[:, 0, :].rearrange("p (k r c) -> p r k c", r=2, c=2)
                for r in range(2):
                    nc.gpsimd.tensor_tensor(out=prod[:, r], in0=w_pairs[:, r], in1=b_pairs, op=MULT)
                    nc.gpsimd.tensor_tensor(out=bias[:, :, r], in0=prod[:, r, :, 0], in1=prod[:, r, :, 1], op=ADD)

            def widen_q_weights():
                b_exp_q = early.tile([P, 16, 2], F32, name="b_exp_q")
                nc.gpsimd.tensor_copy(out=wq[:], in_=wq_raw[:])
                nc.gpsimd.tensor_copy(out=b_exp_q[:].rearrange("p k c -> p (k c)"), in_=b_exp_q_raw[:])
                first_stage_bias(wq, b_exp_q[:], bias_q)

            def factor_area(b):
                return hbm[b * FACTOR : (b + 1) * FACTOR]

            factor_all = early.tile([P, D], F32, name="factor_all")
            factor_by_input = early.tile([P, 2, D // 2], F32, name="factor_by_input")
            factors = {}

            def widen_factors():
                nc.scalar.copy(out=factor_all[0:112, :], in_=factor_raw[0:112, :])
                nc.scalar.copy(out=factor_by_input[0:112], in_=factor_raw[0:112, :].rearrange("p (e c) -> p c e", c=2))

            def park_factors():
                for b in (4, 5, 6, 3, 2, 1, 0):
                    if b < 4:
                        for c in range(2):
                            nc.sync.dma_start(
                                out=factor_area(b).rearrange("(h c g e) -> c g h e", c=2, g=16, h=2 ** (6 - b))[c],
                                in_=factor_by_input[16 * b : 16 * b + 16, c].rearrange("g (h e) -> g h e", h=2 ** (6 - b)),
                            )
                    else:
                        for x in range(2 ** (6 - b)):
                            nc.sync.dma_start(
                                out=factor_area(b).rearrange("(x u g e) -> x g u e", u=2**b, g=16, e=16)[x],
                                in_=factor_all[16 * b : 16 * b + 16, :].rearrange("g (x u e) -> x g u e", u=2**b, e=16)[x],
                            )

            def fetch_factors(b):
                if b < 4:
                    f = early.tile([P, 16, 8 * 2**b], F32, name="factor_%d" % b)
                    for r in range(2**b):
                        nc.sync.dma_start(
                            out=f[:].rearrange("p g e -> p (g e)")[r : P : 2**b, :],
                            in_=factor_area(b).rearrange("(j z) -> j z", j=2 ** (7 - b)),
                        )
                else:
                    rows = 2**b
                    f = early.tile([P, 16 * 2 ** (6 - b), 16], F32, name="factor_%d" % b)
                    for r in range(P // rows):
                        nc.sync.dma_start(
                            out=f[r * rows : (r + 1) * rows].rearrange("p (x g) e -> p x (g e)", g=16),
                            in_=factor_area(b).rearrange("(x u z) -> u x z", u=rows, z=256),
                        )
                factors[b] = f

            def bit4_columns():
                nc.vector.tensor_reduce(
                    out=bit4[:, 1:2],
                    in_=ident[:].rearrange("p (h v l) -> p v h l", v=2, l=16)[:, 1],
                    axis=mybir.AxisListType.XY,
                    op=ADD,
                )
                nc.vector.tensor_scalar(out=bit4[:, 0:1], in0=bit4[:, 1:2], scalar1=-1.0, scalar2=1.0, op0=MULT, op1=ADD)

            def high_masks():
                for r in range(2):
                    m = early.tile([P, 256, 2], F32, name="masked_%d" % r)
                    nc.scalar.activation(
                        out=m[:],
                        in_=factors[4][:].rearrange("p g (t r c) -> p r (g t) c", r=2, c=2)[:, r],
                        func=COPY,
                        scale=bit4[:, r : r + 1],
                    )
                    factors[("masked", r)] = m

            def high_rows():
                row6 = early.tile([P, 64, 2], F32, name="row6")
                for half in range(2):
                    rows = slice(64 * half, 64 * half + 64)
                    nc.scalar.copy(out=row6[rows], in_=factors[6][rows].rearrange("p g (t r c) -> p r (g t) c", r=2, c=2)[:, half])
                row5 = early.tile([P, 128, 2], F32, name="row5")
                for q in range(4):
                    rows = slice(32 * q, 32 * q + 32)
                    nc.scalar.copy(out=row5[rows], in_=factors[5][rows].rearrange("p g (t r c) -> p r (g t) c", r=2, c=2)[:, q % 2])
                factors["row6"] = row6
                factors["row5"] = row5

            def high_products():
                row4 = early.tile([P, 256, 2], F32, name="row4")
                nc.vector.tensor_tensor(out=row4[:], in0=factors[("masked", 0)][:], in1=factors[("masked", 1)][:], op=ADD)
                bits56 = early.tile([P, 2, 2, 16, 4], F32, name="bits56")
                for i6 in range(2):
                    for i5 in range(2):
                        nc.vector.tensor_tensor(
                            out=bits56[:, i6, i5],
                            in0=factors["row6"][:].rearrange("p (g t) c -> p c g t", t=4)[:, i6],
                            in1=factors["row5"][:].rearrange("p (x g t) c -> p x c g t", x=2, t=4)[:, i6, i5],
                            op=MULT,
                        )
                factors["row4"] = row4
                factors["bits56"] = bits56

            def high_last_products():
                high = early.tile([P, 8, 16, 4], F32, name="high")
                for x in range(4):
                    for i4 in range(2):
                        nc.vector.tensor_tensor(
                            out=high[:, 2 * x + i4],
                            in0=factors["bits56"][:, x // 2, x % 2],
                            in1=factors["row4"][:].rearrange("p (x g t) c -> p x c g t", x=4, t=4)[:, x, i4],
                            op=MULT,
                        )
                factors["high"] = high

            def high_turns():
                bank = ps_turn.tile([P, 4, P], F32, name="high_bank", tag="turn")
                columns = factors["high"][:].rearrange("p x g t -> p (x g t)")
                for x in range(4):
                    nc.tensor.transpose(bank[:, x, :], columns[:, x * P : (x + 1) * P], ident[:])
                factors["bank"] = bank

            def high_store():
                rows = early.tile([P, 4, P], F32, name="high_rows_out")
                nc.scalar.copy(out=rows[:], in_=factors["bank"][:])
                nc.sync.dma_start(out=row_area.rearrange("(x p o) -> p x o", x=4, p=P), in_=rows[:])
                spread_rows(0)

            def spread_rows(n):
                for top in range(8):
                    at = 8192 * top + 4096 * n
                    nc.sync.dma_start(
                        out=dense[16 * top : 16 * top + 16, 4096 * n : 4096 * (n + 1)],
                        in_=row_area[at : at + 4096].partition_broadcast(16),
                    )

            def low_products(b):
                if b == 1:
                    before = factors[0][:].rearrange("p g (t r) -> p (g t) r", r=2)
                else:
                    before = factors[("low", b - 1)][:].rearrange("p k r o -> p k (r o)")
                products = low if b == 3 else early.tile([P, 2 * BLOCKS, 2, 2**b], F32, name="low_%d" % b)
                for r in range(2):
                    nc.vector.tensor_tensor(
                        out=products[:].rearrange("p (g t) r o -> p r g t o", t=4)[:, r],
                        in0=factors[b][:].rearrange("p g (o t r) -> p r g t o", t=4, r=2)[:, r],
                        in1=before.rearrange("p (g t) o -> p g t o", t=4),
                        op=MULT,
                    )
                factors[("low", b)] = products

            def q_stage0(j):
                even = ps_front.tile([P, 2, 2 * P], F32, name=uid("turned"), tag="even")
                odd = ps_front.tile([P, 2, 2 * P], F32, name=uid("turned"), tag="odd")
                for n in range(4):
                    block = 4 * j + n
                    for i in range(2):
                        nc.tensor.transpose(
                            (even, odd)[n % 2][:, n // 2, i * P : (i + 1) * P], expanded[:, i, block * P : (block + 1) * P], ident[:]
                        )
                units = []
                for n in range(2):
                    i = 4 * j + 2 * n
                    units.append((even[:, n, 0:N_PAIRS], odd[:, n, 0:N_PAIRS], q_data[:, i, :], q_data[:, i + 1, :], wq[:, 0, :], 2 * j + n, bias_q))
                group(units)

            def q_stage(s, j):
                block_stage(q_data, wq[:, s, :], 2**s, range(4 * j, 4 * j + 4))

            widen_q_weights()
            turn_r_rows()
            widen_x(0)
            widen_x(1)
            turn_x(0)
            turn_x(1)
            quantize_x(0)
            quantize_x(1)
            for j in range(8):
                for i in range(2):
                    expand_pairs(i, j)
                if j == 5:
                    widen_x(2)
                    widen_factors()
                if j == 6:
                    widen_x(3)
            bit4_columns()
            park_factors()
            for b in (4, 5, 6, 3, 2, 1, 0):
                fetch_factors(b)
            for j in range(8):
                q_stage0(j)
                if j == 1:
                    turn_x(2)
                if j == 3:
                    turn_x(3)
            quantize_x(2)
            quantize_x(3)
            q_stage(1, 0)
            q_stage(1, 1)
            weave(
                ([lambda j=j: q_stage(1, j) for j in (2, 3)] + [lambda s=s, j=j: q_stage(s, j) for s in (2, 3) for j in range(4)], 0, 1),
                ([lambda n=n: spread(n) for n in range(6)], 0, 0.5),
                (
                    [high_masks, high_rows, high_products, high_last_products, high_turns, high_store]
                    + [lambda b=b: low_products(b) for b in range(1, 4)],
                    0.7,
                    1,
                ),
            )

        hidden = ctx.enter_context(tc.tile_pool(name="hidden", bufs=1)).tile([P, BLOCKS, TOKENS], F32, name="hidden")
        dense_half = hidden[:, :, N_PAIRS:TOKENS]

        def dense_and_stage9(data, w, first, h, t0, pool):
            size = data.shape[-1]
            units = []
            for t in (t0, t0 + 1):
                sides = []
                for side in range(2):
                    block = 4 * (2 * h + side) + t
                    bank = pool.tile([P, BANK], F32, name=uid("dense"), tag="even" if side == 0 else "odd")
                    at = first + block * P
                    nc.tensor.matmul(out=bank[:, 0:size], lhsT=dense[:, at : at + P], rhs=data[:, block, :], start=True, stop=True)
                    sides.append(bank[:, 0:size])
                i = 8 * h + t
                units.append((sides[0], sides[1], data[:, i, :], data[:, i + 4, :], w[:, 2, :], 4 * h + t, None))
            group(units)

        def gelu(g, first, last):
            for block in range(4 * g, 4 * g + 4):
                part = hidden[:, block, first:last]
                nc.scalar.activation(out=part, in_=part, func=GELU, bias=up_bias_p[:, block : block + 1])

        with ExitStack() as second:
            ps_second = second.enter_context(tc.psum_pool(name="ps_second", bufs=2))
            turned = second.enter_context(tc.tile_pool(name="turned", bufs=2))

            turned_tiles = {}

            def p_expand(g):
                tile = turned.tile([P, 3, 4, P], F32, name=uid("p_expanded"), tag="p_expanded")
                for i in range(3):
                    bank = ps_second.tile([P, BANK], F32, name=uid("mx"), tag="mx", bufs=4)
                    expand(bank[:], i + 1, g)
                    copy(i == 0 and g % 2 == 0, tile[:, i], bank[:].rearrange("p (q t) -> p t q", t=4))
                turned_tiles[g] = tile

            def p_stage0(g):
                units = []
                for n in range(2):
                    sides = []
                    for t in (2 * n, 2 * n + 1):
                        bank = ps_second.tile([P, BANK], F32, name=uid("turned"), tag="even" if t % 2 == 0 else "odd")
                        for i in range(3):
                            nc.tensor.transpose(bank[:, i * P : (i + 1) * P], turned_tiles[g][:, i, t, :], ident[:])
                        sides.append(bank[:, 3 * P - N_DENSE : 3 * P])
                    i = 4 * g + 2 * n
                    units.append((sides[0], sides[1], dense_half[:, i, :], dense_half[:, i + 1, :], wp_up[:, 0, :], 2 * g + n, bias_p))
                group(units)

            def quarter(c):
                return hbm[(c % 2) * QUARTER : (c % 2 + 1) * QUARTER]

            def q_store(c):
                nc.sync.dma_start(out=quarter(c).rearrange("(x q n) -> q x n", x=8, q=P), in_=q_data[:, c:BLOCKS:4, :])

            def r_load(c):
                nc.sync.dma_start(out=r_data[c:P:4].rearrange("p m n -> p (m n)"), in_=quarter(c).rearrange("(p e) -> p e", p=32))

            r_data = big.tile([P, BLOCKS, N_PAIRS], F32, name="r_data", tag="wide")

            def q_stage4(c, half):
                block_stage(q_data, wq[:, 4, :], 16, (c + 8 * half, c + 4 + 8 * half), 1)
                if half == 1:
                    q_store(c)
                    if c > 0:
                        r_load(c - 1)

            p_steps = []
            for g in range(8):
                if g < 7:
                    p_steps.append(lambda g=g: p_expand(g + 1))
                p_steps.append(lambda g=g: p_stage0(g))
            p_expand(0)
            weave((p_steps, 0, 1), ([lambda c=c, half=half: q_stage4(c, half) for c in range(4) for half in range(2)], 0, 0.9))
            r_load(3)

        with ExitStack() as third:
            ps_third = third.enter_context(tc.psum_pool(name="ps_third", bufs=4))
            spread_rows(1)
            late = third.enter_context(tc.tile_pool(name="late", bufs=1))
            con_codes, con_planes = load_weight(w_con_words, w_con_scales, 8, D, 1, nc.gpsimd)
            bias_rows = []
            for n, vec in enumerate((b_con, down_bias)):
                row = late.tile([P, D], BF16, name="bias_row_%d" % n)
                nc.sync.dma_start(out=row[:], in_=vec.partition_broadcast(P))
                bias_rows.append(row)
            out_bias = const.tile([P, D], F32, name="out_bias")
            nc.gpsimd.tensor_tensor(out=out_bias[:], in0=bias_rows[0][:], in1=bias_rows[1][:], op=ADD)
            p_data = big.tile([P, BLOCKS, N_PAIRS], F32, name="p_data", tag="pairs")

            def finish_dense(n, o_top):
                view = dense[:, n * BLOCKS * P : (n + 1) * BLOCKS * P].rearrange("p (k h l) -> p h k l", h=8, l=16)[:, o_top]
                factor = low[:, BLOCKS * n : BLOCKS * (n + 1)].rearrange("p k r o -> p k (r o)")
                nc.vector.tensor_tensor(out=view, in0=view, in1=factor, op=MULT)

            def p_stage1(j):
                block_stage(dense_half, wp_up[:, 1, :], 2, range(4 * j, 4 * j + 4))

            def p_stage9(h, t0):
                dense_and_stage9(dense_half, wp_up, 0, h, t0, ps_third)

            weave(
                ([lambda j=j: p_stage1(j) for j in range(4)], 0, 1),
                ([lambda o_top=o_top: finish_dense(0, o_top) for o_top in range(8)], 0, 0.5),
            )
            p_stage9(0, 0)
            p_stage9(0, 2)

            def r_stage(s, j):
                block_stage(r_data, wr[:, s - 5, :], 2 ** (s - 5), range(4 * j, 4 * j + 4))

            def r_store(c):
                for v in range(2):
                    nc.sync.dma_start(
                        out=quarter(c).rearrange("(v m z) -> v m z", v=2, m=4)[v].rearrange("m (p n) -> p m n", p=P),
                        in_=r_data[:, 16 * v + 4 * c : 16 * v + 4 * c + 4, :],
                    )

            def p_load(c):
                for v in range(2):
                    nc.sync.dma_start(
                        out=p_data[32 * c : 32 * c + 32].rearrange("p (g t) n -> p g (t n)", t=4)[:, v:8:2, :],
                        in_=quarter(c).rearrange("(v m z) -> v m z", v=2, m=4)[v].rearrange("m (x h n) -> (m x) h n", x=8, h=4),
                    )

            def r_stage9(c):
                r_stage(9, c)
                r_store(c)
                if c > 0:
                    p_load(c - 1)
                if c == 3:
                    p_load(3)

            for s in (5, 6, 7):
                for j in range(4):
                    r_stage(s, j)
            weave(
                ([lambda j=j: r_stage(8, j) for j in range(4)] + [lambda c=c: r_stage9(c) for c in range(4)], 0, 0.7),
                ([lambda h=h, t0=t0: p_stage9(h, t0) for h in range(1, 4) for t0 in (0, 2)], 0.1, 1),
            )

            def p_stage10(g2, g0):
                block_stage(dense_half, wp_up[:, 3, :], 8, [8 * g2 + 4 * g0 + t for t in range(4)])

            def p_stage11(g):
                block_stage(dense_half, wp_up[:, 4, :], 16, [4 * g + t for t in range(4)])

            def dense_gelu(g):
                for side in (g, g + 4):
                    gelu(side, N_PAIRS, TOKENS)

            weave(
                (
                    [lambda g2=g2, g0=g0: p_stage10(g2, g0) for g2 in range(2) for g0 in range(2)]
                    + [lambda: p_stage11(0), lambda: p_stage11(1), lambda: dense_gelu(0), lambda: p_stage11(2)]
                    + [lambda: dense_gelu(1), lambda: p_stage11(3), lambda: dense_gelu(2)],
                    0,
                    1,
                ),
                ([lambda o_top=o_top: finish_dense(1, o_top) for o_top in range(8)], 0, 1),
            )

        temps_all["pool"] = ctx.enter_context(tc.tile_pool(name="temps_all", bufs=1))

        with ExitStack() as fourth:
            ps_fourth = fourth.enter_context(tc.psum_pool(name="ps_fourth", bufs=4))

            def pairs_stage10(g2, g0):
                block_stage(p_data, wp_up[:, 3, :], 8, [8 * g2 + 4 * g0 + t for t in range(4)], 3)

            def pairs_stage11(g):
                block_stage(p_data, wp_up[:, 4, :], 16, [4 * g + t for t in range(4)], 3, hidden[:, :, 0:N_PAIRS])

            def pairs_gelu(g):
                gelu(g, 0, N_PAIRS)

            def down_stage0(g):
                block_stage(hidden, wp_down[:, 0, :], 1, (2 * g, 2 * g + 1))

            def down_stage1(g):
                block_stage(hidden, wp_down[:, 1, :], 2, (2 * g, 2 * g + 1), g % 2)

            def down_stage9(h, t0):
                dense_and_stage9(hidden, wp_down, BLOCKS * P, h, t0, ps_fourth)

            def down_stage10(g2, g0):
                for t in (0, 2):
                    k = 8 * g2 + 4 * g0 + t
                    block_stage(hidden, wp_down[:, 3, :], 8, (k, k + 1))

            pairs_stage10(0, 0)
            pairs_stage10(1, 0)
            dense_gelu(3)
            pairs_stage10(0, 1)
            pairs_stage11(0)
            pairs_stage10(1, 1)
            pairs_gelu(0)
            pairs_gelu(4)
            pairs_stage11(1)
            down_stage0(0)
            pairs_gelu(1)
            pairs_stage11(2)
            down_stage1(0)
            down_stage0(1)
            pairs_gelu(5)
            down_stage0(4)
            down_stage1(1)
            pairs_gelu(2)
            down_stage0(5)
            down_stage1(4)
            down_stage9(0, 0)
            pairs_stage11(3)
            pairs_gelu(3)
            down_stage1(5)
            down_stage9(0, 2)
            down_stage0(2)
            pairs_gelu(6)
            down_stage9(2, 0)
            down_stage0(3)
            down_stage1(2)
            down_stage9(2, 2)
            pairs_gelu(7)
            down_stage1(3)
            down_stage0(6)
            down_stage9(1, 0)
            down_stage0(7)
            down_stage1(6)
            down_stage9(1, 2)
            down_stage1(7)
            down_stage10(0, 0)
            down_stage9(3, 0)
            down_stage10(0, 1)
            down_stage9(3, 2)
            down_stage10(1, 0)
            down_stage10(1, 1)

        ps_out = ctx.enter_context(tc.psum_pool(name="ps_out", bufs=1))
        h2 = big.tile([P, 12288], BF16, name="h2", tag="pairs")
        sums = {}
        for i in range(4):
            for d in range(2):
                bank = ps_out.tile([P, BANK], F32, name="sum_%d_%d" % (i, d))
                sums[(i, d)] = bank
        h2_codes = const.tile([P, 2, TOKENS], U32, name="h2_codes", tag="codes", align_bytes=64)
        h2_planes = const.tile([P, 2, TOKENS], U8, name="h2_planes", tag="planes", align_bytes=64)

        def h2_rows(g):
            at = 2048 * (2 * (g % 2) + g // 4)
            return h2[:, at : at + 2048].rearrange("p (t n) -> p t n", t=4)

        def h2_grouped(g):
            at = 8192 + 2048 * (g // 4)
            return h2[:, at : at + 2048].rearrange("p (n t) -> p n t", t=4)

        def down_stage11(g, t0):
            units = []
            for t in (t0, t0 + 1):
                k = 4 * g + t
                units.append((hidden[:, k, :], hidden[:, k + 16, :], h2_rows(g)[:, t, :], h2_rows(g + 4)[:, t, :], wp_down[:, 4, :], k, None))
            group(units)

        def lay_words(g, tokens):
            for half_pass in (g, g + 4):
                copy(half_pass < 4, h2_grouped(half_pass)[:, tokens, :], h2_rows(half_pass)[:, :, tokens].rearrange("p t n -> p n t"))

        def quantize_h2(g, tokens):
            nc.vector.quantize_mx(
                out=h2_codes[:, g // 4, tokens].bitcast(FP8X4),
                scales=h2_planes[:, g // 4, tokens],
                in_=h2_grouped(g)[:, tokens, :].rearrange("p n t -> p (n t)"),
            )

        def contract(g, token_tiles):
            for i in token_tiles:
                for d in range(2):
                    nc.tensor.matmul_mx(
                        out=sums[(i, d)][:],
                        lhsT=h2_codes[:, g // 4, i * P : (i + 1) * P].bitcast(FP8X4),
                        lhsT_scale=h2_planes[:, g // 4, i * P : (i + 1) * P],
                        rhs=con_codes[:, g, 1024 * d : 1024 * (d + 1)].bitcast(FP4X4),
                        rhs_scale=con_planes[:, g, 512 * d : 512 * (d + 1)],
                        start=(g == 0),
                        stop=(g == 7),
                    )

        def store(token_tiles):
            for i in token_tiles:
                for d in range(2):
                    o = temps_all["pool"].tile([P, BANK], F32, name=uid("out"), tag="t", bufs=TEMPS_ALL)
                    cols = slice(512 * d, 512 * (d + 1))
                    nc.vector.tensor_tensor(out=o[:], in0=sums[(i, d)][:], in1=out_bias[:, cols], op=ADD)
                    nc.sync.dma_start(out=out_rows[i * P : (i + 1) * P, cols], in_=o[:])

        every = slice(0, TOKENS)
        for g in range(4):
            down_stage11(g, 0)
            if g > 0:
                lay_words(g - 1, every)
            down_stage11(g, 2)
            if g > 0:
                for done in (g - 1, g + 3):
                    quantize_h2(done, every)
                    contract(done, range(4))
        first_half, second_half = slice(0, 256), slice(256, TOKENS)
        lay_words(3, first_half)
        for g in (3, 7):
            quantize_h2(g, first_half)
        lay_words(3, second_half)
        for g in (3, 7):
            contract(g, (0, 1))
        for g in (3, 7):
            quantize_h2(g, second_half)
        for g in (3, 7):
            contract(g, (2, 3))
        store((0, 1))
        store((2, 3))
